import numpy as np
import ml_dtypes


def mxq(x, axis, fmt="e4m3"):
    dtype, down = {"e4m3": (ml_dtypes.float8_e4m3fn, 7), "e5m2": (ml_dtypes.float8_e5m2, 14)}[fmt]
    v = np.moveaxis(np.asarray(x, np.float32).astype(ml_dtypes.bfloat16).astype(np.float64), axis, -1)
    blocks = v.reshape(v.shape[:-1] + (-1, 32))
    amax = np.abs(blocks).max(-1, keepdims=True)
    byte = np.maximum(np.where(amax > 0, np.frexp(amax)[1] - 1 + 127, 0) - down, 1)
    scale = np.exp2(byte - 127.0)
    codes = (blocks / scale).astype(np.float32).astype(dtype).astype(np.float64)
    return np.moveaxis((codes * scale).reshape(v.shape), -1, axis)


WIDE = False


def mx_kscale(k):
    if not WIDE:
        return np.ones(k)
    levels = np.array([10, -10, 5, -5, 0])
    if k % 512:
        return np.exp2(np.random.permutation(np.resize(levels, k // 32))).repeat(32)
    a = np.empty((k // 512, 16))
    for p in range(k // 512):
        a[p, :8] = np.random.permutation(np.resize(levels, 8))
        for g in range(8):
            far = levels[np.abs(levels - a[p, g]) >= 10]
            a[p, g + 8] = far[np.random.randint(len(far))]
    return np.exp2(a.ravel()).repeat(32)


BF16 = ml_dtypes.bfloat16


def bf(x):
    return np.asarray(x, np.float32).astype(BF16)


def f64(x):
    return np.asarray(x).astype(np.float64)


E2M1 = np.array([0.0, 0.5, 1.0, 1.5, 2.0, 3.0, 4.0, 6.0, -0.0, -0.5, -1.0, -1.5, -2.0, -3.0, -4.0, -6.0])


def pack_weight(w, fmt):
    k, n = w.shape
    w = f64(bf(w)).reshape(k // 32, 32, n)
    amax = np.abs(w).max(1)
    if fmt == "e4m3":
        byte = np.frexp(amax)[1] - 1 + 127 - 7
    else:
        mant, ex = np.frexp(amax / 6.0)
        byte = np.where(mant > 0.5, ex, ex - 1) + 127
    byte = np.clip(np.where(amax > 0, byte, 1), 1, 254)
    scaled = (w * np.exp2(127.0 - byte)[:, None, :]).reshape(k, n).astype(np.float32)
    by_word = np.ascontiguousarray(scaled.reshape(k // 512, 128, 4, n).transpose(0, 1, 3, 2))
    if fmt == "e4m3":
        words = by_word.astype(ml_dtypes.float8_e4m3fn).view(np.uint8)
    else:
        c = by_word.astype(ml_dtypes.float4_e2m1fn).view(np.uint8) & 0xF
        words = c[..., 0::2] | (c[..., 1::2] << 4)
    return np.ascontiguousarray(words), np.ascontiguousarray(byte.astype(np.uint8).reshape(k // 512, 16, n))


def unpack_weight(words, scales, fmt):
    g, p, n, _ = words.shape
    if fmt == "e4m3":
        vals = np.ascontiguousarray(words).view(ml_dtypes.float8_e4m3fn).astype(np.float64)
    else:
        nib = np.empty((g, p, n, 4), np.uint8)
        nib[..., 0::2] = words & 0xF
        nib[..., 1::2] = words >> 4
        vals = E2M1[nib]
    vals = vals * np.repeat(np.exp2(scales.astype(np.float64) - 127.0), 8, axis=1)[..., None]
    return vals.transpose(0, 1, 3, 2).reshape(g * 512, n)


B, C, H, W, DM, GH = 6, 512, 32, 32, 128, 512


def sigmoid(v):
    return 1.0 / (1.0 + np.exp(-v))


def draw0():
    s = np.concatenate([mx_kscale(C), np.ones(C)])
    t = mx_kscale(GH)
    x = bf(np.random.standard_normal((B, C, H, W)) * s[:C][None, :, None, None])
    agg = bf(np.random.standard_normal((B, C, H, W)) * 0.7)
    g1w = np.random.standard_normal((GH, 2 * C)) / np.sqrt(2 * C) * t[:, None] / s[None, :]
    g1w_words, g1w_scales = pack_weight(np.ascontiguousarray(g1w.T), 'e4m3')
    g1b = bf(np.random.standard_normal(GH) * 0.3 * t)
    g2w = np.random.standard_normal((C, GH)) * 2.0 / np.sqrt(GH) / t[None, :]
    g2w_words, g2w_scales = pack_weight(np.ascontiguousarray(g2w.T), 'e4m3')
    g2b = bf(np.random.standard_normal(C) * 0.3)
    return {'x': x,
            'agg': agg,
            'g1w_words': g1w_words,
            'g1w_scales': g1w_scales,
            'g1b': g1b,
            'g2w_words': g2w_words,
            'g2w_scales': g2w_scales,
            'g2b': g2b}


def core(x, agg, g1w_words, g1w_scales, g1b, g2w_words, g2w_scales, g2b):
    a = f64(agg).reshape(B, C, H * W)
    cat = np.concatenate([f64(x).reshape(B, C, H * W), a], axis=1)
    hidden = np.maximum((unpack_weight(g1w_words, g1w_scales, 'e4m3').T @ mxq(cat, 1, 'e4m3')) + f64(g1b)[None, :, None], 0.0)
    gate = sigmoid((unpack_weight(g2w_words, g2w_scales, 'e4m3').T @ mxq(hidden, 1, 'e4m3')) + f64(g2b)[None, :, None])
    return (a * gate).reshape(B, C, H, W)


def e4m3fn_bytes(y):
    return np.clip(np.asarray(y, np.float64), -448.0, 448.0).astype(np.float32).astype(ml_dtypes.float8_e4m3fn).view(np.uint8)


def e4m3fn_values(b):
    return np.asarray(b, np.uint8).view(ml_dtypes.float8_e4m3fn).astype(np.float64)


def setup_inputs():
    d = draw0()
    x0 = np.asarray(d['x']).astype(np.float64)
    s = (np.max(np.abs(x0), axis=(0, 2, 3), keepdims=True) / 448.0).astype(np.float32)
    out = {}
    for k, v in d.items():
        if k == 'x':
            out['x_bytes'] = e4m3fn_bytes(x0 / s.astype(np.float64))
            out['x_scale'] = s
        else:
            out[k] = v
    return out


def reference(x_bytes, x_scale, agg, g1w_words, g1w_scales, g1b, g2w_words, g2w_scales, g2b):
    return core(e4m3fn_values(x_bytes) * x_scale.astype(np.float64), agg, g1w_words, g1w_scales, g1b, g2w_words, g2w_scales, g2b)

@@ -1,0 +1,259 @@
+from contextlib import ExitStack
+
+import concourse.mybir as mybir
+
+F32 = mybir.dt.float32
+BF16 = mybir.dt.bfloat16
+I32 = mybir.dt.int32
+U32 = mybir.dt.uint32
+U8 = mybir.dt.uint8
+FP8 = mybir.dt.float8_e4m3fn
+FP8X4 = mybir.dt.float8_e4m3fn_x4
+ACT = mybir.ActivationFunctionType
+ALU = mybir.AluOpType
+
+IMAGES, C, PIX = 6, 512, 1024
+P = 128
+PACK = 4
+N = 512
+WIDTHS = [256, 512, 256] + [512] * 9 + [256, 256]
+COUNT = len(WIDTHS)
+S_SHARE_H = {COUNT - 3: 128, COUNT - 2: 128, COUNT - 1: 128}
+S_SHARE_X = 128
+STARTS = [sum(WIDTHS[:h]) for h in range(COUNT)]
+
+FLOPS = 2 * IMAGES * PIX * C * (2 * C + C)
+
+
+def tile_graphaugmentation_pb_t_w8_kernel(
+    tc, x_bytes, x_scale, agg, g1w_words, g1w_scales, g1b, g2w_words, g2w_scales, g2b, out
+):
+    nc = tc.nc
+    x_v = x_bytes.rearrange("b (p t) h w -> b p t (h w)", t=PACK)
+    agg_v = agg.rearrange("b (p t) h w -> b p t (h w)", t=PACK)
+    out_v = out.rearrange("b (p t) h w -> b p t (h w)", t=PACK)
+
+    with ExitStack() as ctx:
+        keep = ctx.enter_context(tc.tile_pool(name="keep", bufs=1))
+        two = ctx.enter_context(tc.tile_pool(name="two", bufs=2))
+        three = ctx.enter_context(tc.tile_pool(name="three", bufs=3))
+        four = ctx.enter_context(tc.tile_pool(name="four", bufs=4))
+        ps1 = ctx.enter_context(tc.psum_pool(name="ps1", bufs=4))
+        ps2 = ctx.enter_context(tc.psum_pool(name="ps2", bufs=4))
+        ctx.enter_context(tc.manual_schedule())
+
+        xs = keep.tile([P, PACK], F32, name="xs")
+        b1 = keep.tile([P, PACK], BF16, name="b1")
+        b2 = keep.tile([P, PACK], BF16, name="b2")
+        nc.scalar.dma_start(out=xs[:], in_=x_scale.rearrange("o (p t) h w -> p (o t h w)", t=PACK))
+        nc.gpsimd.dma_start(out=b1[:], in_=g1b.rearrange("(p t) -> p t", t=PACK))
+        nc.gpsimd.dma_start(out=b2[:], in_=g2b.rearrange("(p t) -> p t", t=PACK))
+
+        s1_raw = keep.tile([P, C], U8, name="s1_raw", align_bytes=64)
+        s2_raw = keep.tile([P, C], U8, name="s2_raw", align_bytes=64)
+        nc.vector.memset(s1_raw[:].bitcast(I32), 0)
+        nc.vector.memset(s2_raw[:].bitcast(I32), 0)
+        dummy = keep.tile([P, 1], F32, name="dummy")
+        nc.vector.memset(dummy[:], 0.0)
+        nc.scalar.activation(out=dummy[:], in_=dummy[:], func=ACT.Sigmoid)
+
+        xb = [keep.tile([P, PACK, PIX], U8, name=f"xb{b}") for b in range(IMAGES)]
+        ag = [keep.tile([P, PACK, PIX], BF16, name=f"ag{b}") for b in range(IMAGES)]
+        w1_raw = [keep.tile([P, C], I32, name=f"w1_raw{g}", align_bytes=64) for g in range(2)]
+        w2_raw = keep.tile([P, C], I32, name="w2_raw", align_bytes=64)
+
+        def words(src):
+            return src.rearrange("p n t -> p (n t)").bitcast(I32)
+
+        def load(b, px):
+            nc.sync.dma_start(out=xb[b][:, :, px], in_=x_v[b][:, :, px])
+            nc.sync.dma_start(out=ag[b][:, :, px], in_=agg_v[b][:, :, px])
+
+        load(0, slice(0, 256))
+        load(0, slice(256, 768))
+        for q in range(4):
+            nc.sync.dma_start(
+                out=s1_raw[32 * q : 32 * q + 8, :].bitcast(I32), in_=g1w_scales[:, 4 * q : 4 * q + 4, :].bitcast(I32)
+            )
+        nc.sync.dma_start(out=w1_raw[0][:], in_=words(g1w_words[0]))
+        nc.sync.dma_start(out=w1_raw[1][:], in_=words(g1w_words[1]))
+        load(0, slice(768, PIX))
+        for q in range(4):
+            nc.sync.dma_start(
+                out=s2_raw[32 * q : 32 * q + 4, :].bitcast(I32), in_=g2w_scales[0, 4 * q : 4 * q + 4, :].bitcast(I32)
+            )
+        nc.sync.dma_start(out=w2_raw[:], in_=words(g2w_words[0]))
+        for b in range(1, IMAGES):
+            load(b, slice(0, PIX))
+
+        w1 = [keep.tile([P, C], I32, name=f"w1_{g}", align_bytes=64) for g in range(2)]
+        w2 = keep.tile([P, C], I32, name="w2", align_bytes=64)
+        s1 = keep.tile([P, C], U8, name="s1", align_bytes=64)
+        s2 = keep.tile([P, C], U8, name="s2", align_bytes=64)
+
+        def permute(dst, src):
+            nc.vector.tensor_copy(
+                out=dst[:].rearrange("p (t m) -> p m t", t=PACK), in_=src[:].rearrange("p (m t) -> p m t", t=PACK)
+            )
+
+        xw, xa, codes1, scales1, hp, hi, codes2, scales2, gt, acc1, acc2 = ({} for _ in range(11))
+
+        def where(h):
+            return STARTS[h] // PIX, slice(STARTS[h] % PIX, STARTS[h] % PIX + WIDTHS[h])
+
+        def widen(h):
+            b, px = where(h)
+            xw[h] = two.tile([P, 2, 2 * WIDTHS[h]], BF16, name="xw")
+            for t in range(PACK):
+                nc.vector.tensor_scalar(
+                    out=xw[h][:, t // 2, t % 2 :: 2],
+                    in0=xb[b][:, t, px].bitcast(FP8),
+                    scalar1=xs[:, t : t + 1],
+                    scalar2=None,
+                    op0=ALU.mult,
+                )
+
+        def join(copy, h, c0, c1):
+            if c1 > c0:
+                copy(
+                    out=xa[h][:, 0, PACK * c0 : PACK * c1].bitcast(F32).rearrange("p (c u) -> p c u", u=2),
+                    in_=xw[h][:, :, 2 * c0 : 2 * c1].bitcast(F32).rearrange("p u c -> p c u"),
+                )
+
+        def x_split(h):
+            return WIDTHS[h] - (S_SHARE_X if h > 2 and WIDTHS[h] == N else 0)
+
+        def inter(copy, dst, src, c0, c1):
+            if c1 > c0:
+                copy(
+                    out=dst[:, PACK * c0 : PACK * c1].rearrange("p (c i t) -> p c t i", i=4, t=PACK),
+                    in_=src[:, :, c0:c1].rearrange("p t (c i) -> p c t i", i=4),
+                )
+
+        def inter_a(h):
+            b, px = where(h)
+            xa[h] = three.tile([P, 2, PACK * WIDTHS[h]], BF16, name="xa", align_bytes=64)
+            inter(nc.scalar.copy, xa[h][:, 1, :], ag[b][:, :, px], 0, WIDTHS[h])
+
+        def quant_in(h):
+            n = WIDTHS[h]
+            codes1[h] = two.tile([P, 2, n], U32, name="codes1", align_bytes=64)
+            scales1[h] = two.tile([P, 2, n], U8, name="scales1", align_bytes=64)
+            nc.vector.quantize_mx(
+                out=codes1[h][:].rearrange("p g n -> p (g n)").bitcast(FP8X4),
+                scales=scales1[h][:].rearrange("p g n -> p (g n)"),
+                in_=xa[h][:].rearrange("p g m -> p (g m)"),
+            )
+
+        def h_split(h):
+            return WIDTHS[h] - S_SHARE_H.get(h, 0)
+
+        def inter_h_scalar(h):
+            hi[h] = two.tile([P, PACK * WIDTHS[h]], BF16, name="hi", align_bytes=64)
+            inter(nc.scalar.copy, hi[h], hp[h], h_split(h), WIDTHS[h])
+
+        def inter_h_vector(h):
+            inter(nc.vector.tensor_copy, hi[h], hp[h], 0, h_split(h))
+
+        def quant_h(h):
+            n = WIDTHS[h]
+            codes2[h] = two.tile([P, n], U32, name="codes2", align_bytes=64)
+            scales2[h] = two.tile([P, n], U8, name="scales2", align_bytes=64)
+            nc.vector.quantize_mx(out=codes2[h][:].bitcast(FP8X4), scales=scales2[h][:], in_=hi[h][:])
+
+        def mm1(h):
+            for t in range(PACK):
+                m = slice(P * t, P * t + P)
+                acc1[h, t] = ps1.tile([P, WIDTHS[h]], F32, name="acc1")
+                for g in range(2):
+                    nc.tensor.matmul_mx(
+                        out=acc1[h, t][:],
+                        lhsT=w1[g][:, m].bitcast(FP8X4),
+                        lhsT_scale=s1[4 * g :, m],
+                        rhs=codes1[h][:, g, :].bitcast(FP8X4),
+                        rhs_scale=scales1[h][:, g, :],
+                        start=(g == 0),
+                        stop=(g == 1),
+                    )
+
+        def mm2(h):
+            for t in range(PACK):
+                m = slice(P * t, P * t + P)
+                acc2[h, t] = ps2.tile([P, WIDTHS[h]], F32, name="acc2")
+                nc.tensor.matmul_mx(
+                    out=acc2[h, t][:],
+                    lhsT=w2[:, m].bitcast(FP8X4),
+                    lhsT_scale=s2[:, m],
+                    rhs=codes2[h][:].bitcast(FP8X4),
+                    rhs_scale=scales2[h][:],
+                    start=True,
+                    stop=True,
+                )
+
+        def relu(h):
+            hp[h] = two.tile([P, PACK, WIDTHS[h]], BF16, name="hp")
+            for t in range(PACK):
+                nc.scalar.activation(out=hp[h][:, t, :], in_=acc1[h, t][:], func=ACT.Relu, bias=b1[:, t : t + 1])
+
+        def sig(h):
+            gt[h] = four.tile([P, PACK, WIDTHS[h]], F32, name="gt")
+            for t in range(PACK):
+                nc.scalar.activation(out=gt[h][:, t, :], in_=acc2[h, t][:], func=ACT.Sigmoid, bias=b2[:, t : t + 1])
+
+        def prod(h):
+            b, px = where(h)
+            step = 1 if h >= COUNT - 2 else PACK
+            for t in range(0, PACK, step):
+                ts = slice(t, t + step)
+                nc.vector.tensor_tensor(out=gt[h][:, ts, :], in0=gt[h][:, ts, :], in1=ag[b][:, ts, px], op=ALU.mult)
+                if step == PACK or t % 2 == 1:
+                    ts = slice(0, PACK) if step == PACK else slice(t - 1, t + 1)
+                    nc.sync.dma_start(out=out_v[b][:, ts, px], in_=gt[h][:, ts, :])
+
+        def on(h):
+            return 0 <= h < COUNT
+
+        inter_a(0)
+        widen(0)
+        join(nc.vector.tensor_copy, 0, 0, WIDTHS[0])
+        inter_a(1)
+        widen(1)
+        quant_in(0)
+        permute(s1, s1_raw)
+        permute(w1[0], w1_raw[0])
+        permute(w1[1], w1_raw[1])
+        join(nc.vector.tensor_copy, 1, 0, WIDTHS[1])
+        mm1(0)
+        relu(0)
+        inter_a(2)
+        for i in range(COUNT + 1):
+            if on(i):
+                inter_h_scalar(i)
+            if on(i - 1):
+                sig(i - 1)
+            if on(i + 1):
+                quant_in(i + 1)
+                mm1(i + 1)
+            if i == 0:
+                relu(1)
+                widen(2)
+            if on(i):
+                inter_h_vector(i)
+            if on(i + 2) and i > 0:
+                widen(i + 2)
+            if on(i + 3):
+                inter_a(i + 3)
+            if on(i + 2):
+                join(nc.scalar.copy, i + 2, x_split(i + 2), WIDTHS[i + 2])
+            if on(i + 1) and i > 0:
+                relu(i + 1)
+            if i == 0:
+                permute(s2, s2_raw)
+                permute(w2, w2_raw)
+            if on(i):
+                quant_h(i)
+                mm2(i)
+            if on(i + 2):
+                join(nc.vector.tensor_copy, i + 2, 0, x_split(i + 2))
+            if on(i - 1):
+                prod(i - 1)

@@ -1,6 +1,7 @@
 from contextlib import ExitStack
 
 import concourse.mybir as mybir
+from concourse.masks import make_identity
 
 F32 = mybir.dt.float32
 BF16 = mybir.dt.bfloat16
@@ -15,12 +16,14 @@ ALU = mybir.AluOpType
 IMAGES, C, PIX = 6, 512, 1024
 P = 128
 PACK = 4
-N = 512
-WIDTHS = [256, 512, 256] + [512] * 9 + [256, 256]
+BANK_BF16 = 1024
+WIDTHS = [256, 256] + [512] * 10 + [256, 256]
+LOADS = [256, 256, 512, 512, 512] + [PIX] * (IMAGES - 2)
+DIRECT = 2
 COUNT = len(WIDTHS)
-S_SHARE_H = {COUNT - 3: 128, COUNT - 2: 128, COUNT - 1: 128}
-S_SHARE_X = 128
+VECTOR_RELU = range(COUNT - 5, COUNT - 3)
 STARTS = [sum(WIDTHS[:h]) for h in range(COUNT)]
+LOAD_STARTS = [sum(LOADS[:j]) for j in range(len(LOADS))]
 
 FLOPS = 2 * IMAGES * PIX * C * (2 * C + C)
 
@@ -38,14 +41,15 @@ def tile_graphaugmentation_pb_t_w8_kernel(
         two = ctx.enter_context(tc.tile_pool(name="two", bufs=2))
         three = ctx.enter_context(tc.tile_pool(name="three", bufs=3))
         four = ctx.enter_context(tc.tile_pool(name="four", bufs=4))
-        ps1 = ctx.enter_context(tc.psum_pool(name="ps1", bufs=4))
-        ps2 = ctx.enter_context(tc.psum_pool(name="ps2", bufs=4))
+        banks = ctx.enter_context(tc.psum_pool(name="banks", bufs=8))
         ctx.enter_context(tc.manual_schedule())
 
         xs = keep.tile([P, PACK], F32, name="xs")
         b1 = keep.tile([P, PACK], BF16, name="b1")
         b2 = keep.tile([P, PACK], BF16, name="b2")
+        ident = keep.tile([P, P], BF16, name="ident")
         nc.scalar.dma_start(out=xs[:], in_=x_scale.rearrange("o (p t) h w -> p (o t h w)", t=PACK))
+        make_identity(nc, ident[:])
         nc.gpsimd.dma_start(out=b1[:], in_=g1b.rearrange("(p t) -> p t", t=PACK))
         nc.gpsimd.dma_start(out=b2[:], in_=g2b.rearrange("(p t) -> p t", t=PACK))
 
@@ -53,38 +57,50 @@ def tile_graphaugmentation_pb_t_w8_kernel(
         s2_raw = keep.tile([P, C], U8, name="s2_raw", align_bytes=64)
         nc.vector.memset(s1_raw[:].bitcast(I32), 0)
         nc.vector.memset(s2_raw[:].bitcast(I32), 0)
-        dummy = keep.tile([P, 1], F32, name="dummy")
-        nc.vector.memset(dummy[:], 0.0)
-        nc.scalar.activation(out=dummy[:], in_=dummy[:], func=ACT.Sigmoid)
+        warm = keep.tile([P, 1], F32, name="warm")
+        nc.vector.memset(warm[:], 0.0)
+        nc.scalar.activation(out=warm[:], in_=warm[:], func=ACT.Sigmoid)
 
-        xb = [keep.tile([P, PACK, PIX], U8, name=f"xb{b}") for b in range(IMAGES)]
-        ag = [keep.tile([P, PACK, PIX], BF16, name=f"ag{b}") for b in range(IMAGES)]
+        x_loaded = [keep.tile([P, PACK, n], U8, name=f"x_loaded{j}") for j, n in enumerate(LOADS)]
+        agg_loaded = [keep.tile([P, PACK, n], BF16, name=f"agg_loaded{j}") for j, n in enumerate(LOADS)]
+
+        def chunk_of(loaded, h):
+            j = max(j for j in range(len(LOADS)) if LOAD_STARTS[j] <= STARTS[h])
+            c0 = STARTS[h] - LOAD_STARTS[j]
+            return loaded[j][:, :, c0 : c0 + WIDTHS[h]]
+
+        xb = [chunk_of(x_loaded, h) for h in range(COUNT)]
+        ag = [chunk_of(agg_loaded, h) for h in range(COUNT)]
         w1_raw = [keep.tile([P, C], I32, name=f"w1_raw{g}", align_bytes=64) for g in range(2)]
         w2_raw = keep.tile([P, C], I32, name="w2_raw", align_bytes=64)
 
         def words(src):
             return src.rearrange("p n t -> p (n t)").bitcast(I32)
 
-        def load(b, px):
-            nc.sync.dma_start(out=xb[b][:, :, px], in_=x_v[b][:, :, px])
-            nc.sync.dma_start(out=ag[b][:, :, px], in_=agg_v[b][:, :, px])
+        def where(h):
+            return STARTS[h] // PIX, slice(STARTS[h] % PIX, STARTS[h] % PIX + WIDTHS[h])
 
-        load(0, slice(0, 256))
-        load(0, slice(256, 768))
+        def load(j):
+            b, px = LOAD_STARTS[j] // PIX, slice(LOAD_STARTS[j] % PIX, LOAD_STARTS[j] % PIX + LOADS[j])
+            nc.sync.dma_start(out=x_loaded[j][:], in_=x_v[b][:, :, px])
+            nc.sync.dma_start(out=agg_loaded[j][:], in_=agg_v[b][:, :, px])
+
+        load(0)
+        load(1)
         for q in range(4):
             nc.sync.dma_start(
                 out=s1_raw[32 * q : 32 * q + 8, :].bitcast(I32), in_=g1w_scales[:, 4 * q : 4 * q + 4, :].bitcast(I32)
             )
         nc.sync.dma_start(out=w1_raw[0][:], in_=words(g1w_words[0]))
         nc.sync.dma_start(out=w1_raw[1][:], in_=words(g1w_words[1]))
-        load(0, slice(768, PIX))
+        load(2)
         for q in range(4):
             nc.sync.dma_start(
                 out=s2_raw[32 * q : 32 * q + 4, :].bitcast(I32), in_=g2w_scales[0, 4 * q : 4 * q + 4, :].bitcast(I32)
             )
         nc.sync.dma_start(out=w2_raw[:], in_=words(g2w_words[0]))
-        for b in range(1, IMAGES):
-            load(b, slice(0, PIX))
+        for j in range(3, len(LOADS)):
+            load(j)
 
         w1 = [keep.tile([P, C], I32, name=f"w1_{g}", align_bytes=64) for g in range(2)]
         w2 = keep.tile([P, C], I32, name="w2", align_bytes=64)
@@ -96,44 +112,48 @@ def tile_graphaugmentation_pb_t_w8_kernel(
                 out=dst[:].rearrange("p (t m) -> p m t", t=PACK), in_=src[:].rearrange("p (m t) -> p m t", t=PACK)
             )
 
-        xw, xa, codes1, scales1, hp, hi, codes2, scales2, gt, acc1, acc2 = ({} for _ in range(11))
-
-        def where(h):
-            return STARTS[h] // PIX, slice(STARTS[h] % PIX, STARTS[h] % PIX + WIDTHS[h])
+        xw, xa, codes1, scales1, hp, hi, codes2, scales2, gt = ({} for _ in range(9))
 
         def widen(h):
-            b, px = where(h)
-            xw[h] = two.tile([P, 2, 2 * WIDTHS[h]], BF16, name="xw")
+            xw[h] = three.tile([P, 2, 2 * WIDTHS[h]], BF16, name="xw")
             for t in range(PACK):
                 nc.vector.tensor_scalar(
                     out=xw[h][:, t // 2, t % 2 :: 2],
-                    in0=xb[b][:, t, px].bitcast(FP8),
+                    in0=xb[h][:, t, :].bitcast(FP8),
                     scalar1=xs[:, t : t + 1],
                     scalar2=None,
                     op0=ALU.mult,
                 )
 
-        def join(copy, h, c0, c1):
-            if c1 > c0:
-                copy(
-                    out=xa[h][:, 0, PACK * c0 : PACK * c1].bitcast(F32).rearrange("p (c u) -> p c u", u=2),
-                    in_=xw[h][:, :, 2 * c0 : 2 * c1].bitcast(F32).rearrange("p u c -> p c u"),
-                )
+        def join(copy, h):
+            copy(
+                out=xa[h][:, 0, :].bitcast(F32).rearrange("p (c u) -> p c u", u=2),
+                in_=xw[h][:].bitcast(F32).rearrange("p u c -> p c u"),
+            )
 
-        def x_split(h):
-            return WIDTHS[h] - (S_SHARE_X if h > 2 and WIDTHS[h] == N else 0)
+        def weave(copy, dst, src):
+            copy(
+                out=dst.rearrange("p (c i t) -> p c t i", i=4, t=PACK),
+                in_=src.rearrange("p t (c i) -> p c t i", i=4),
+            )
 
-        def inter(copy, dst, src, c0, c1):
-            if c1 > c0:
-                copy(
-                    out=dst[:, PACK * c0 : PACK * c1].rearrange("p (c i t) -> p c t i", i=4, t=PACK),
-                    in_=src[:, :, c0:c1].rearrange("p t (c i) -> p c t i", i=4),
-                )
-
-        def inter_a(h):
-            b, px = where(h)
+        def weave_agg(h):
             xa[h] = three.tile([P, 2, PACK * WIDTHS[h]], BF16, name="xa", align_bytes=64)
-            inter(nc.scalar.copy, xa[h][:, 1, :], ag[b][:, :, px], 0, WIDTHS[h])
+            if h < DIRECT:
+                weave(nc.scalar.copy, xa[h][:, 1, :], ag[h])
+                return
+            n = min(WIDTHS[h], BANK_BF16 // PACK)
+            for c0 in range(0, WIDTHS[h], n):
+                bank = banks.tile([P, PACK * n], BF16, name="bank")
+                for c in range(0, n, P):
+                    nc.tensor.matmul(
+                        out=bank[:, PACK * c : PACK * (c + P)].rearrange("p (n t) -> p t n", t=PACK),
+                        lhsT=ident[:],
+                        rhs=ag[h][:, :, c0 + c : c0 + c + P],
+                        start=True,
+                        stop=True,
+                    )
+                nc.scalar.copy(out=xa[h][:, 1, PACK * c0 : PACK * (c0 + n)], in_=bank[:])
 
         def quant_in(h):
             n = WIDTHS[h]
@@ -145,29 +165,24 @@ def tile_graphaugmentation_pb_t_w8_kernel(
                 in_=xa[h][:].rearrange("p g m -> p (g m)"),
             )
 
-        def h_split(h):
-            return WIDTHS[h] - S_SHARE_H.get(h, 0)
-
-        def inter_h_scalar(h):
+        def weave_hidden(h):
             hi[h] = two.tile([P, PACK * WIDTHS[h]], BF16, name="hi", align_bytes=64)
-            inter(nc.scalar.copy, hi[h], hp[h], h_split(h), WIDTHS[h])
+            weave(nc.vector.tensor_copy, hi[h][:], hp[h][:])
 
-        def inter_h_vector(h):
-            inter(nc.vector.tensor_copy, hi[h], hp[h], 0, h_split(h))
-
-        def quant_h(h):
+        def quant_hidden(h):
             n = WIDTHS[h]
             codes2[h] = two.tile([P, n], U32, name="codes2", align_bytes=64)
             scales2[h] = two.tile([P, n], U8, name="scales2", align_bytes=64)
             nc.vector.quantize_mx(out=codes2[h][:].bitcast(FP8X4), scales=scales2[h][:], in_=hi[h][:])
 
-        def mm1(h):
+        def first_layer(h):
+            hp[h] = two.tile([P, PACK, WIDTHS[h]], BF16, name="hp")
             for t in range(PACK):
                 m = slice(P * t, P * t + P)
-                acc1[h, t] = ps1.tile([P, WIDTHS[h]], F32, name="acc1")
+                acc = banks.tile([P, WIDTHS[h]], F32, name="bank")
                 for g in range(2):
                     nc.tensor.matmul_mx(
-                        out=acc1[h, t][:],
+                        out=acc[:],
                         lhsT=w1[g][:, m].bitcast(FP8X4),
                         lhsT_scale=s1[4 * g :, m],
                         rhs=codes1[h][:, g, :].bitcast(FP8X4),
@@ -175,13 +190,20 @@ def tile_graphaugmentation_pb_t_w8_kernel(
                         start=(g == 0),
                         stop=(g == 1),
                     )
+                if t == 0 and h in VECTOR_RELU:
+                    nc.vector.tensor_scalar(
+                        out=hp[h][:, t, :], in0=acc[:], scalar1=b1[:, t : t + 1], scalar2=0.0, op0=ALU.add, op1=ALU.max
+                    )
+                else:
+                    nc.scalar.activation(out=hp[h][:, t, :], in_=acc[:], func=ACT.Relu, bias=b1[:, t : t + 1])
 
-        def mm2(h):
+        def second_layer(h):
+            gt[h] = four.tile([P, PACK, WIDTHS[h]], F32, name="gt")
             for t in range(PACK):
                 m = slice(P * t, P * t + P)
-                acc2[h, t] = ps2.tile([P, WIDTHS[h]], F32, name="acc2")
+                acc = banks.tile([P, WIDTHS[h]], F32, name="bank")
                 nc.tensor.matmul_mx(
-                    out=acc2[h, t][:],
+                    out=acc[:],
                     lhsT=w2[:, m].bitcast(FP8X4),
                     lhsT_scale=s2[:, m],
                     rhs=codes2[h][:].bitcast(FP8X4),
@@ -189,71 +211,62 @@ def tile_graphaugmentation_pb_t_w8_kernel(
                     start=True,
                     stop=True,
                 )
+                nc.scalar.activation(out=gt[h][:, t, :], in_=acc[:], func=ACT.Sigmoid, bias=b2[:, t : t + 1])
 
-        def relu(h):
-            hp[h] = two.tile([P, PACK, WIDTHS[h]], BF16, name="hp")
-            for t in range(PACK):
-                nc.scalar.activation(out=hp[h][:, t, :], in_=acc1[h, t][:], func=ACT.Relu, bias=b1[:, t : t + 1])
-
-        def sig(h):
-            gt[h] = four.tile([P, PACK, WIDTHS[h]], F32, name="gt")
-            for t in range(PACK):
-                nc.scalar.activation(out=gt[h][:, t, :], in_=acc2[h, t][:], func=ACT.Sigmoid, bias=b2[:, t : t + 1])
-
-        def prod(h):
+        def product(h):
             b, px = where(h)
-            step = 1 if h >= COUNT - 2 else PACK
-            for t in range(0, PACK, step):
-                ts = slice(t, t + step)
-                nc.vector.tensor_tensor(out=gt[h][:, ts, :], in0=gt[h][:, ts, :], in1=ag[b][:, ts, px], op=ALU.mult)
-                if step == PACK or t % 2 == 1:
-                    ts = slice(0, PACK) if step == PACK else slice(t - 1, t + 1)
-                    nc.sync.dma_start(out=out_v[b][:, ts, px], in_=gt[h][:, ts, :])
+            rows = 2 if h == COUNT - 1 else PACK
+            for t in range(0, PACK, rows):
+                ts = slice(t, t + rows)
+                nc.vector.tensor_tensor(out=gt[h][:, ts, :], in0=gt[h][:, ts, :], in1=ag[h][:, ts, :], op=ALU.mult)
+                nc.sync.dma_start(out=out_v[b][:, ts, px], in_=gt[h][:, ts, :])
 
         def on(h):
             return 0 <= h < COUNT
 
-        inter_a(0)
+        weave_agg(0)
         widen(0)
-        join(nc.vector.tensor_copy, 0, 0, WIDTHS[0])
-        inter_a(1)
         widen(1)
-        quant_in(0)
+        join(nc.vector.tensor_copy, 0)
+        weave_agg(1)
+        join(nc.scalar.copy, 1)
         permute(s1, s1_raw)
+        quant_in(0)
         permute(w1[0], w1_raw[0])
         permute(w1[1], w1_raw[1])
-        join(nc.vector.tensor_copy, 1, 0, WIDTHS[1])
-        mm1(0)
-        relu(0)
-        inter_a(2)
-        for i in range(COUNT + 1):
-            if on(i):
-                inter_h_scalar(i)
-            if on(i - 1):
-                sig(i - 1)
-            if on(i + 1):
-                quant_in(i + 1)
-                mm1(i + 1)
-            if i == 0:
-                relu(1)
-                widen(2)
-            if on(i):
-                inter_h_vector(i)
-            if on(i + 2) and i > 0:
-                widen(i + 2)
-            if on(i + 3):
-                inter_a(i + 3)
-            if on(i + 2):
-                join(nc.scalar.copy, i + 2, x_split(i + 2), WIDTHS[i + 2])
-            if on(i + 1) and i > 0:
-                relu(i + 1)
-            if i == 0:
-                permute(s2, s2_raw)
-                permute(w2, w2_raw)
-            if on(i):
-                quant_h(i)
-                mm2(i)
-            if on(i + 2):
-                join(nc.vector.tensor_copy, i + 2, 0, x_split(i + 2))
-            if on(i - 1):
-                prod(i - 1)
+        quant_in(1)
+        first_layer(0)
+        first_layer(1)
+        widen(2)
+        weave_hidden(0)
+        permute(s2, s2_raw)
+        permute(w2, w2_raw)
+        quant_hidden(0)
+        weave_agg(2)
+        join(nc.scalar.copy, 2)
+        weave_hidden(1)
+        widen(3)
+        quant_in(2)
+        quant_hidden(1)
+        weave_agg(3)
+        join(nc.scalar.copy, 3)
+        second_layer(0)
+        widen(4)
+        for s in range(2, COUNT + 2):
+            if on(s):
+                first_layer(s)
+            if on(s + 2):
+                weave_agg(s + 2)
+                join(nc.scalar.copy, s + 2)
+            if on(s - 1):
+                second_layer(s - 1)
+            if on(s + 1):
+                quant_in(s + 1)
+            if on(s - 2):
+                product(s - 2)
+            if on(s):
+                weave_hidden(s)
+            if on(s + 3):
+                widen(s + 3)
+            if on(s):
+                quant_hidden(s)

@@ -21,7 +21,8 @@ WIDTHS = [256, 256] + [512] * 10 + [256, 256]
 LOADS = [256, 256, 512, 512, 512] + [PIX] * (IMAGES - 2)
 DIRECT = 2
 COUNT = len(WIDTHS)
-VECTOR_RELU = range(COUNT - 5, COUNT - 3)
+X_BY_MATMUL = (6, 8, 10)
+VECTOR_JOIN = (4, 11)
 STARTS = [sum(WIDTHS[:h]) for h in range(COUNT)]
 LOAD_STARTS = [sum(LOADS[:j]) for j in range(len(LOADS))]
 
@@ -48,7 +49,6 @@ def tile_graphaugmentation_pb_t_w8_kernel(
         b1 = keep.tile([P, PACK], BF16, name="b1")
         b2 = keep.tile([P, PACK], BF16, name="b2")
         ident = keep.tile([P, P], BF16, name="ident")
-        nc.scalar.dma_start(out=xs[:], in_=x_scale.rearrange("o (p t) h w -> p (o t h w)", t=PACK))
         make_identity(nc, ident[:])
         nc.gpsimd.dma_start(out=b1[:], in_=g1b.rearrange("(p t) -> p t", t=PACK))
         nc.gpsimd.dma_start(out=b2[:], in_=g2b.rearrange("(p t) -> p t", t=PACK))
@@ -57,9 +57,6 @@ def tile_graphaugmentation_pb_t_w8_kernel(
         s2_raw = keep.tile([P, C], U8, name="s2_raw", align_bytes=64)
         nc.vector.memset(s1_raw[:].bitcast(I32), 0)
         nc.vector.memset(s2_raw[:].bitcast(I32), 0)
-        warm = keep.tile([P, 1], F32, name="warm")
-        nc.vector.memset(warm[:], 0.0)
-        nc.scalar.activation(out=warm[:], in_=warm[:], func=ACT.Sigmoid)
 
         x_loaded = [keep.tile([P, PACK, n], U8, name=f"x_loaded{j}") for j, n in enumerate(LOADS)]
         agg_loaded = [keep.tile([P, PACK, n], BF16, name=f"agg_loaded{j}") for j, n in enumerate(LOADS)]
@@ -80,27 +77,34 @@ def tile_graphaugmentation_pb_t_w8_kernel(
         def where(h):
             return STARTS[h] // PIX, slice(STARTS[h] % PIX, STARTS[h] % PIX + WIDTHS[h])
 
-        def load(j):
-            b, px = LOAD_STARTS[j] // PIX, slice(LOAD_STARTS[j] % PIX, LOAD_STARTS[j] % PIX + LOADS[j])
-            nc.sync.dma_start(out=x_loaded[j][:], in_=x_v[b][:, :, px])
-            nc.sync.dma_start(out=agg_loaded[j][:], in_=agg_v[b][:, :, px])
+        def load(loaded, src, j):
+            b, c0 = divmod(LOAD_STARTS[j], PIX)
+            nc.sync.dma_start(out=loaded[j][:], in_=src[b][:, :, c0 : c0 + LOADS[j]])
 
-        load(0)
-        load(1)
+        nc.scalar.dma_start(out=xs[:], in_=x_scale.rearrange("o (p t) h w -> p (o t h w)", t=PACK))
         for q in range(4):
-            nc.sync.dma_start(
+            nc.scalar.dma_start(
                 out=s1_raw[32 * q : 32 * q + 8, :].bitcast(I32), in_=g1w_scales[:, 4 * q : 4 * q + 4, :].bitcast(I32)
             )
+        warm = keep.tile([P, 1], F32, name="warm")
+        nc.vector.memset(warm[:], 0.0)
+        nc.scalar.activation(out=warm[:], in_=warm[:], func=ACT.Sigmoid)
+        load(x_loaded, x_v, 0)
+        load(agg_loaded, agg_v, 0)
+        load(x_loaded, x_v, 1)
+        load(agg_loaded, agg_v, 1)
         nc.sync.dma_start(out=w1_raw[0][:], in_=words(g1w_words[0]))
         nc.sync.dma_start(out=w1_raw[1][:], in_=words(g1w_words[1]))
-        load(2)
+        load(x_loaded, x_v, 2)
+        load(agg_loaded, agg_v, 2)
         for q in range(4):
             nc.sync.dma_start(
                 out=s2_raw[32 * q : 32 * q + 4, :].bitcast(I32), in_=g2w_scales[0, 4 * q : 4 * q + 4, :].bitcast(I32)
             )
         nc.sync.dma_start(out=w2_raw[:], in_=words(g2w_words[0]))
         for j in range(3, len(LOADS)):
-            load(j)
+            load(x_loaded, x_v, j)
+            load(agg_loaded, agg_v, j)
 
         w1 = [keep.tile([P, C], I32, name=f"w1_{g}", align_bytes=64) for g in range(2)]
         w2 = keep.tile([P, C], I32, name="w2", align_bytes=64)
@@ -115,10 +119,12 @@ def tile_graphaugmentation_pb_t_w8_kernel(
         xw, xa, codes1, scales1, hp, hi, codes2, scales2, gt = ({} for _ in range(9))
 
         def widen(h):
-            xw[h] = three.tile([P, 2, 2 * WIDTHS[h]], BF16, name="xw")
+            rows = PACK if h in X_BY_MATMUL else 2
+            xa[h] = four.tile([P, 2, PACK * WIDTHS[h]], BF16, name="xa", align_bytes=64)
+            xw[h] = three.tile([P, rows, PACK * WIDTHS[h] // rows], BF16, name="xw")
             for t in range(PACK):
                 nc.vector.tensor_scalar(
-                    out=xw[h][:, t // 2, t % 2 :: 2],
+                    out=xw[h][:, t, :] if h in X_BY_MATMUL else xw[h][:, t // 2, t % 2 :: 2],
                     in0=xb[h][:, t, :].bitcast(FP8),
                     scalar1=xs[:, t : t + 1],
                     scalar2=None,
@@ -126,6 +132,9 @@ def tile_graphaugmentation_pb_t_w8_kernel(
                 )
 
         def join(copy, h):
+            if h in X_BY_MATMUL:
+                weave_by_matmul(xa[h][:, 0, :], xw[h][:], WIDTHS[h])
+                return
             copy(
                 out=xa[h][:, 0, :].bitcast(F32).rearrange("p (c u) -> p c u", u=2),
                 in_=xw[h][:].bitcast(F32).rearrange("p u c -> p c u"),
@@ -137,23 +146,25 @@ def tile_graphaugmentation_pb_t_w8_kernel(
                 in_=src.rearrange("p t (c i) -> p c t i", i=4),
             )
 
-        def weave_agg(h):
-            xa[h] = three.tile([P, 2, PACK * WIDTHS[h]], BF16, name="xa", align_bytes=64)
-            if h < DIRECT:
-                weave(nc.scalar.copy, xa[h][:, 1, :], ag[h])
-                return
-            n = min(WIDTHS[h], BANK_BF16 // PACK)
-            for c0 in range(0, WIDTHS[h], n):
+        def weave_by_matmul(dst, src, width):
+            n = min(width, BANK_BF16 // PACK)
+            for c0 in range(0, width, n):
                 bank = banks.tile([P, PACK * n], BF16, name="bank")
                 for c in range(0, n, P):
                     nc.tensor.matmul(
                         out=bank[:, PACK * c : PACK * (c + P)].rearrange("p (n t) -> p t n", t=PACK),
                         lhsT=ident[:],
-                        rhs=ag[h][:, :, c0 + c : c0 + c + P],
+                        rhs=src[:, :, c0 + c : c0 + c + P],
                         start=True,
                         stop=True,
                     )
-                nc.scalar.copy(out=xa[h][:, 1, PACK * c0 : PACK * (c0 + n)], in_=bank[:])
+                nc.scalar.copy(out=dst[:, PACK * c0 : PACK * (c0 + n)], in_=bank[:])
+
+        def weave_agg(h):
+            if h < DIRECT:
+                weave(nc.scalar.copy, xa[h][:, 1, :], ag[h])
+            else:
+                weave_by_matmul(xa[h][:, 1, :], ag[h], WIDTHS[h])
 
         def quant_in(h):
             n = WIDTHS[h]
@@ -190,16 +201,12 @@ def tile_graphaugmentation_pb_t_w8_kernel(
                         start=(g == 0),
                         stop=(g == 1),
                     )
-                if t == 0 and h in VECTOR_RELU:
-                    nc.vector.tensor_scalar(
-                        out=hp[h][:, t, :], in0=acc[:], scalar1=b1[:, t : t + 1], scalar2=0.0, op0=ALU.add, op1=ALU.max
-                    )
-                else:
-                    nc.scalar.activation(out=hp[h][:, t, :], in_=acc[:], func=ACT.Relu, bias=b1[:, t : t + 1])
+                nc.scalar.activation(out=hp[h][:, t, :], in_=acc[:], func=ACT.Relu, bias=b1[:, t : t + 1])
 
-        def second_layer(h):
-            gt[h] = four.tile([P, PACK, WIDTHS[h]], F32, name="gt")
-            for t in range(PACK):
+        def second_layer(h, rows=range(PACK)):
+            if 0 in rows:
+                gt[h] = four.tile([P, PACK, WIDTHS[h]], F32, name="gt")
+            for t in rows:
                 m = slice(P * t, P * t + P)
                 acc = banks.tile([P, WIDTHS[h]], F32, name="bank")
                 nc.tensor.matmul_mx(
@@ -213,60 +220,72 @@ def tile_graphaugmentation_pb_t_w8_kernel(
                 )
                 nc.scalar.activation(out=gt[h][:, t, :], in_=acc[:], func=ACT.Sigmoid, bias=b2[:, t : t + 1])
 
-        def product(h):
+        def product(h, t0, t1):
             b, px = where(h)
-            rows = 2 if h == COUNT - 1 else PACK
-            for t in range(0, PACK, rows):
-                ts = slice(t, t + rows)
-                nc.vector.tensor_tensor(out=gt[h][:, ts, :], in0=gt[h][:, ts, :], in1=ag[h][:, ts, :], op=ALU.mult)
-                nc.sync.dma_start(out=out_v[b][:, ts, px], in_=gt[h][:, ts, :])
+            ts = slice(t0, t1)
+            nc.vector.tensor_tensor(out=gt[h][:, ts, :], in0=gt[h][:, ts, :], in1=ag[h][:, ts, :], op=ALU.mult)
+            nc.sync.dma_start(out=out_v[b][:, ts, px], in_=gt[h][:, ts, :])
 
-        def on(h):
-            return 0 <= h < COUNT
-
-        weave_agg(0)
         widen(0)
-        widen(1)
+        weave_agg(0)
+        permute(s1, s1_raw)
         join(nc.vector.tensor_copy, 0)
+        widen(1)
         weave_agg(1)
         join(nc.scalar.copy, 1)
-        permute(s1, s1_raw)
         quant_in(0)
         permute(w1[0], w1_raw[0])
         permute(w1[1], w1_raw[1])
         quant_in(1)
+        widen(2)
         first_layer(0)
         first_layer(1)
-        widen(2)
         weave_hidden(0)
         permute(s2, s2_raw)
         permute(w2, w2_raw)
         quant_hidden(0)
-        weave_agg(2)
         join(nc.scalar.copy, 2)
+        weave_agg(2)
         weave_hidden(1)
         widen(3)
         quant_in(2)
         quant_hidden(1)
-        weave_agg(3)
-        join(nc.scalar.copy, 3)
         second_layer(0)
-        widen(4)
-        for s in range(2, COUNT + 2):
-            if on(s):
-                first_layer(s)
-            if on(s + 2):
-                weave_agg(s + 2)
+        join(nc.scalar.copy, 3)
+        weave_agg(3)
+        product(0, 0, 2)
+        product(0, 2, 4)
+        for s in range(2, COUNT - 2):
+            first_layer(s)
+            second_layer(s - 1)
+            widen(s + 2)
+            weave_agg(s + 2)
+            if s + 2 not in VECTOR_JOIN:
                 join(nc.scalar.copy, s + 2)
-            if on(s - 1):
-                second_layer(s - 1)
-            if on(s + 1):
-                quant_in(s + 1)
-            if on(s - 2):
-                product(s - 2)
-            if on(s):
-                weave_hidden(s)
-            if on(s + 3):
-                widen(s + 3)
-            if on(s):
-                quant_hidden(s)
+            quant_in(s + 1)
+            weave_hidden(s)
+            if s + 2 in VECTOR_JOIN:
+                join(nc.vector.tensor_copy, s + 2)
+            product(s - 1, 0, 2)
+            quant_hidden(s)
+            product(s - 1, 2, 4)
+        last = COUNT - 1
+        first_layer(last - 1)
+        quant_in(last)
+        second_layer(last - 2, range(0, 2))
+        first_layer(last)
+        second_layer(last - 2, range(2, 4))
+        weave_hidden(last - 1)
+        product(last - 2, 0, 2)
+        quant_hidden(last - 1)
+        weave_hidden(last)
+        product(last - 2, 2, 3)
+        quant_hidden(last)
+        product(last - 2, 3, 4)
+        second_layer(last - 1)
+        second_layer(last)
+        product(last - 1, 0, 2)
+        product(last - 1, 2, 4)
+        product(last, 0, 2)
+        product(last, 2, 3)
+        product(last, 3, 4)

@@ -50,8 +50,6 @@ def tile_graphaugmentation_pb_t_w8_kernel(
         b2 = keep.tile([P, PACK], BF16, name="b2")
         ident = keep.tile([P, P], BF16, name="ident")
         make_identity(nc, ident[:])
-        nc.gpsimd.dma_start(out=b1[:], in_=g1b.rearrange("(p t) -> p t", t=PACK))
-        nc.gpsimd.dma_start(out=b2[:], in_=g2b.rearrange("(p t) -> p t", t=PACK))
 
         s1_raw = keep.tile([P, C], U8, name="s1_raw", align_bytes=64)
         s2_raw = keep.tile([P, C], U8, name="s2_raw", align_bytes=64)
@@ -82,10 +80,7 @@ def tile_graphaugmentation_pb_t_w8_kernel(
             nc.sync.dma_start(out=loaded[j][:], in_=src[b][:, :, c0 : c0 + LOADS[j]])
 
         nc.scalar.dma_start(out=xs[:], in_=x_scale.rearrange("o (p t) h w -> p (o t h w)", t=PACK))
-        for q in range(4):
-            nc.scalar.dma_start(
-                out=s1_raw[32 * q : 32 * q + 8, :].bitcast(I32), in_=g1w_scales[:, 4 * q : 4 * q + 4, :].bitcast(I32)
-            )
+        nc.scalar.dma_start(out=b1[:], in_=g1b.rearrange("(p t) -> p t", t=PACK))
         warm = keep.tile([P, 1], F32, name="warm")
         nc.vector.memset(warm[:], 0.0)
         nc.scalar.activation(out=warm[:], in_=warm[:], func=ACT.Sigmoid)
@@ -93,6 +88,10 @@ def tile_graphaugmentation_pb_t_w8_kernel(
         load(agg_loaded, agg_v, 0)
         load(x_loaded, x_v, 1)
         load(agg_loaded, agg_v, 1)
+        for q in range(4):
+            nc.sync.dma_start(
+                out=s1_raw[32 * q : 32 * q + 8, :].bitcast(I32), in_=g1w_scales[:, 4 * q : 4 * q + 4, :].bitcast(I32)
+            )
         nc.sync.dma_start(out=w1_raw[0][:], in_=words(g1w_words[0]))
         nc.sync.dma_start(out=w1_raw[1][:], in_=words(g1w_words[1]))
         load(x_loaded, x_v, 2)
@@ -102,6 +101,7 @@ def tile_graphaugmentation_pb_t_w8_kernel(
                 out=s2_raw[32 * q : 32 * q + 4, :].bitcast(I32), in_=g2w_scales[0, 4 * q : 4 * q + 4, :].bitcast(I32)
             )
         nc.sync.dma_start(out=w2_raw[:], in_=words(g2w_words[0]))
+        nc.sync.dma_start(out=b2[:], in_=g2b.rearrange("(p t) -> p t", t=PACK))
         for j in range(3, len(LOADS)):
             load(x_loaded, x_v, j)
             load(agg_loaded, agg_v, j)
@@ -228,11 +228,11 @@ def tile_graphaugmentation_pb_t_w8_kernel(
 
         widen(0)
         weave_agg(0)
-        permute(s1, s1_raw)
-        join(nc.vector.tensor_copy, 0)
         widen(1)
+        join(nc.vector.tensor_copy, 0)
         weave_agg(1)
         join(nc.scalar.copy, 1)
+        permute(s1, s1_raw)
         quant_in(0)
         permute(w1[0], w1_raw[0])
         permute(w1[1], w1_raw[1])

@@ -18,13 +18,13 @@ P = 128
 PACK = 4
 BANK_BF16 = 1024
 WIDTHS = [256, 256] + [512] * 10 + [256, 256]
-LOADS = [256, 256, 512, 512, 512] + [PIX] * (IMAGES - 2)
+X_LOADS = [512] * 4 + [PIX] * (IMAGES - 2)
+AGG_LOADS = [256, 256] + [512] * 3 + [PIX] * (IMAGES - 2)
 DIRECT = 2
 COUNT = len(WIDTHS)
 X_BY_MATMUL = (6, 8, 10)
 VECTOR_JOIN = (4, 11)
 STARTS = [sum(WIDTHS[:h]) for h in range(COUNT)]
-LOAD_STARTS = [sum(LOADS[:j]) for j in range(len(LOADS))]
 
 FLOPS = 2 * IMAGES * PIX * C * (2 * C + C)
 
@@ -56,16 +56,16 @@ def tile_graphaugmentation_pb_t_w8_kernel(
         nc.vector.memset(s1_raw[:].bitcast(I32), 0)
         nc.vector.memset(s2_raw[:].bitcast(I32), 0)
 
-        x_loaded = [keep.tile([P, PACK, n], U8, name=f"x_loaded{j}") for j, n in enumerate(LOADS)]
-        agg_loaded = [keep.tile([P, PACK, n], BF16, name=f"agg_loaded{j}") for j, n in enumerate(LOADS)]
+        x_loaded = [keep.tile([P, PACK, n], U8, name=f"x_loaded{j}") for j, n in enumerate(X_LOADS)]
+        agg_loaded = [keep.tile([P, PACK, n], BF16, name=f"agg_loaded{j}") for j, n in enumerate(AGG_LOADS)]
 
-        def chunk_of(loaded, h):
-            j = max(j for j in range(len(LOADS)) if LOAD_STARTS[j] <= STARTS[h])
-            c0 = STARTS[h] - LOAD_STARTS[j]
+        def chunk_of(loaded, sizes, h):
+            j = max(j for j in range(len(sizes)) if sum(sizes[:j]) <= STARTS[h])
+            c0 = STARTS[h] - sum(sizes[:j])
             return loaded[j][:, :, c0 : c0 + WIDTHS[h]]
 
-        xb = [chunk_of(x_loaded, h) for h in range(COUNT)]
-        ag = [chunk_of(agg_loaded, h) for h in range(COUNT)]
+        xb = [chunk_of(x_loaded, X_LOADS, h) for h in range(COUNT)]
+        ag = [chunk_of(agg_loaded, AGG_LOADS, h) for h in range(COUNT)]
         w1_raw = [keep.tile([P, C], I32, name=f"w1_raw{g}", align_bytes=64) for g in range(2)]
         w2_raw = keep.tile([P, C], I32, name="w2_raw", align_bytes=64)
 
@@ -75,36 +75,41 @@ def tile_graphaugmentation_pb_t_w8_kernel(
         def where(h):
             return STARTS[h] // PIX, slice(STARTS[h] % PIX, STARTS[h] % PIX + WIDTHS[h])
 
-        def load(loaded, src, j):
-            b, c0 = divmod(LOAD_STARTS[j], PIX)
-            nc.sync.dma_start(out=loaded[j][:], in_=src[b][:, :, c0 : c0 + LOADS[j]])
+        def load(loaded, src, sizes, j):
+            b, c0 = divmod(sum(sizes[:j]), PIX)
+            nc.sync.dma_start(out=loaded[j][:], in_=src[b][:, :, c0 : c0 + sizes[j]])
+
+        def load_x(j):
+            load(x_loaded, x_v, X_LOADS, j)
+
+        def load_agg(j):
+            load(agg_loaded, agg_v, AGG_LOADS, j)
 
         nc.scalar.dma_start(out=xs[:], in_=x_scale.rearrange("o (p t) h w -> p (o t h w)", t=PACK))
         nc.scalar.dma_start(out=b1[:], in_=g1b.rearrange("(p t) -> p t", t=PACK))
         warm = keep.tile([P, 1], F32, name="warm")
         nc.vector.memset(warm[:], 0.0)
         nc.scalar.activation(out=warm[:], in_=warm[:], func=ACT.Sigmoid)
-        load(x_loaded, x_v, 0)
-        load(agg_loaded, agg_v, 0)
-        load(x_loaded, x_v, 1)
-        load(agg_loaded, agg_v, 1)
+        load_x(0)
+        load_agg(0)
+        load_agg(1)
         for q in range(4):
             nc.sync.dma_start(
                 out=s1_raw[32 * q : 32 * q + 8, :].bitcast(I32), in_=g1w_scales[:, 4 * q : 4 * q + 4, :].bitcast(I32)
             )
         nc.sync.dma_start(out=w1_raw[0][:], in_=words(g1w_words[0]))
         nc.sync.dma_start(out=w1_raw[1][:], in_=words(g1w_words[1]))
-        load(x_loaded, x_v, 2)
-        load(agg_loaded, agg_v, 2)
+        load_x(1)
         for q in range(4):
             nc.sync.dma_start(
                 out=s2_raw[32 * q : 32 * q + 4, :].bitcast(I32), in_=g2w_scales[0, 4 * q : 4 * q + 4, :].bitcast(I32)
             )
         nc.sync.dma_start(out=w2_raw[:], in_=words(g2w_words[0]))
+        load_agg(2)
         nc.sync.dma_start(out=b2[:], in_=g2b.rearrange("(p t) -> p t", t=PACK))
-        for j in range(3, len(LOADS)):
-            load(x_loaded, x_v, j)
-            load(agg_loaded, agg_v, j)
+        for j in range(2, len(X_LOADS)):
+            load_x(j)
+            load_agg(j + 1)
 
         w1 = [keep.tile([P, C], I32, name=f"w1_{g}", align_bytes=64) for g in range(2)]
         w2 = keep.tile([P, C], I32, name="w2", align_bytes=64)
@@ -188,20 +193,23 @@ def tile_graphaugmentation_pb_t_w8_kernel(
 
         def first_layer(h):
             hp[h] = two.tile([P, PACK, WIDTHS[h]], BF16, name="hp")
-            for t in range(PACK):
+            acc = {}
+            order = [(g, t) for t in range(PACK) for g in range(2)]
+            for g, t in sorted(order) if h == 0 else order:
                 m = slice(P * t, P * t + P)
-                acc = banks.tile([P, WIDTHS[h]], F32, name="bank")
-                for g in range(2):
-                    nc.tensor.matmul_mx(
-                        out=acc[:],
-                        lhsT=w1[g][:, m].bitcast(FP8X4),
-                        lhsT_scale=s1[4 * g :, m],
-                        rhs=codes1[h][:, g, :].bitcast(FP8X4),
-                        rhs_scale=scales1[h][:, g, :],
-                        start=(g == 0),
-                        stop=(g == 1),
-                    )
-                nc.scalar.activation(out=hp[h][:, t, :], in_=acc[:], func=ACT.Relu, bias=b1[:, t : t + 1])
+                if g == 0:
+                    acc[t] = banks.tile([P, WIDTHS[h]], F32, name="bank")
+                nc.tensor.matmul_mx(
+                    out=acc[t][:],
+                    lhsT=w1[g][:, m].bitcast(FP8X4),
+                    lhsT_scale=s1[4 * g :, m],
+                    rhs=codes1[h][:, g, :].bitcast(FP8X4),
+                    rhs_scale=scales1[h][:, g, :],
+                    start=(g == 0),
+                    stop=(g == 1),
+                )
+                if g == 1:
+                    nc.scalar.activation(out=hp[h][:, t, :], in_=acc[t][:], func=ACT.Relu, bias=b1[:, t : t + 1])
 
         def second_layer(h, rows=range(PACK)):
             if 0 in rows:
@@ -240,8 +248,8 @@ def tile_graphaugmentation_pb_t_w8_kernel(
         widen(2)
         first_layer(0)
         first_layer(1)
-        weave_hidden(0)
         permute(s2, s2_raw)
+        weave_hidden(0)
         permute(w2, w2_raw)
         quant_hidden(0)
         join(nc.scalar.copy, 2)
@@ -272,20 +280,19 @@ def tile_graphaugmentation_pb_t_w8_kernel(
         last = COUNT - 1
         first_layer(last - 1)
         quant_in(last)
-        second_layer(last - 2, range(0, 2))
+        second_layer(last - 2, range(0, 3))
         first_layer(last)
-        second_layer(last - 2, range(2, 4))
+        second_layer(last - 2, range(3, 4))
         weave_hidden(last - 1)
         product(last - 2, 0, 2)
         quant_hidden(last - 1)
-        weave_hidden(last)
         product(last - 2, 2, 3)
-        quant_hidden(last)
+        weave_hidden(last)
         product(last - 2, 3, 4)
+        quant_hidden(last)
         second_layer(last - 1)
         second_layer(last)
         product(last - 1, 0, 2)
         product(last - 1, 2, 4)
-        product(last, 0, 2)
-        product(last, 2, 3)
-        product(last, 3, 4)
+        for t in range(4):
+            product(last, t, t + 1)

@@ -15,27 +15,34 @@ ALU = mybir.AluOpType
 
 IMAGES, C, PIX = 6, 512, 1024
 P = 128
-PACK = 4
-BANK_BF16 = 1024
-WIDTHS = [256, 256] + [512] * 10 + [256, 256]
-X_LOADS = [512] * 4 + [PIX] * (IMAGES - 2)
-AGG_LOADS = [256, 256] + [512] * 3 + [PIX] * (IMAGES - 2)
-DIRECT = 2
-COUNT = len(WIDTHS)
-X_BY_MATMUL = (6, 8, 10)
-VECTOR_JOIN = (4, 11)
-STARTS = [sum(WIDTHS[:h]) for h in range(COUNT)]
+ROWS = 4
+BANK_PIXELS = 256
+NEIGHBOURS = 4
 
 FLOPS = 2 * IMAGES * PIX * C * (2 * C + C)
+
+WIDTHS = [256, 256] + [512] * 10 + [256, 256]
+COUNT = len(WIDTHS)
+LAST = COUNT - 1
+STARTS = [sum(WIDTHS[:h]) for h in range(COUNT)]
+
+X_LOADS = [512] * 4 + [PIX] * (IMAGES - 2)
+AGG_LOADS = [256, 256] + [512] * 3 + [PIX] * (IMAGES - 2)
+
+FULL_FROM = 6
+X_BY_MATMUL = list(range(FULL_FROM, COUNT, 2)) + [LAST]
+VECTOR_JOIN = list(range(0, FULL_FROM, 2)) + [LAST - 2]
+WEAVING_MATMULS = FLOPS // 10 // (2 * P * P * ROWS * P)
+SCALAR_WEAVES = IMAGES * PIX + sum(WIDTHS[h] for h in X_BY_MATMUL) - WEAVING_MATMULS * P
 
 
 def tile_graphaugmentation_pb_t_w8_kernel(
     tc, x_bytes, x_scale, agg, g1w_words, g1w_scales, g1b, g2w_words, g2w_scales, g2b, out
 ):
     nc = tc.nc
-    x_v = x_bytes.rearrange("b (p t) h w -> b p t (h w)", t=PACK)
-    agg_v = agg.rearrange("b (p t) h w -> b p t (h w)", t=PACK)
-    out_v = out.rearrange("b (p t) h w -> b p t (h w)", t=PACK)
+    x_hbm = x_bytes.rearrange("b (p t) h w -> b p t (h w)", t=ROWS)
+    agg_hbm = agg.rearrange("b (p t) h w -> b p t (h w)", t=ROWS)
+    out_hbm = out.rearrange("b (p t) h w -> b p t (h w)", t=ROWS)
 
     with ExitStack() as ctx:
         keep = ctx.enter_context(tc.tile_pool(name="keep", bufs=1))
@@ -45,9 +52,9 @@ def tile_graphaugmentation_pb_t_w8_kernel(
         banks = ctx.enter_context(tc.psum_pool(name="banks", bufs=8))
         ctx.enter_context(tc.manual_schedule())
 
-        xs = keep.tile([P, PACK], F32, name="xs")
-        b1 = keep.tile([P, PACK], BF16, name="b1")
-        b2 = keep.tile([P, PACK], BF16, name="b2")
+        xs = keep.tile([P, ROWS], F32, name="xs")
+        b1 = keep.tile([P, ROWS], BF16, name="b1")
+        b2 = keep.tile([P, ROWS], BF16, name="b2")
         ident = keep.tile([P, P], BF16, name="ident")
         make_identity(nc, ident[:])
 
@@ -56,40 +63,38 @@ def tile_graphaugmentation_pb_t_w8_kernel(
         nc.vector.memset(s1_raw[:].bitcast(I32), 0)
         nc.vector.memset(s2_raw[:].bitcast(I32), 0)
 
-        x_loaded = [keep.tile([P, PACK, n], U8, name=f"x_loaded{j}") for j, n in enumerate(X_LOADS)]
-        agg_loaded = [keep.tile([P, PACK, n], BF16, name=f"agg_loaded{j}") for j, n in enumerate(AGG_LOADS)]
+        x_loaded = [keep.tile([P, ROWS, n], U8, name=f"x_loaded{j}") for j, n in enumerate(X_LOADS)]
+        agg_loaded = [keep.tile([P, ROWS, n], BF16, name=f"agg_loaded{j}") for j, n in enumerate(AGG_LOADS)]
+        w1_raw = [keep.tile([P, C], I32, name=f"w1_raw{g}", align_bytes=64) for g in range(2)]
+        w2_raw = keep.tile([P, C], I32, name="w2_raw", align_bytes=64)
 
         def chunk_of(loaded, sizes, h):
             j = max(j for j in range(len(sizes)) if sum(sizes[:j]) <= STARTS[h])
             c0 = STARTS[h] - sum(sizes[:j])
             return loaded[j][:, :, c0 : c0 + WIDTHS[h]]
 
-        xb = [chunk_of(x_loaded, X_LOADS, h) for h in range(COUNT)]
-        ag = [chunk_of(agg_loaded, AGG_LOADS, h) for h in range(COUNT)]
-        w1_raw = [keep.tile([P, C], I32, name=f"w1_raw{g}", align_bytes=64) for g in range(2)]
-        w2_raw = keep.tile([P, C], I32, name="w2_raw", align_bytes=64)
+        x_rows = [chunk_of(x_loaded, X_LOADS, h) for h in range(COUNT)]
+        agg_rows = [chunk_of(agg_loaded, AGG_LOADS, h) for h in range(COUNT)]
 
-        def words(src):
-            return src.rearrange("p n t -> p (n t)").bitcast(I32)
-
-        def where(h):
-            return STARTS[h] // PIX, slice(STARTS[h] % PIX, STARTS[h] % PIX + WIDTHS[h])
-
-        def load(loaded, src, sizes, j):
+        def load(loaded, hbm, sizes, j):
             b, c0 = divmod(sum(sizes[:j]), PIX)
-            nc.sync.dma_start(out=loaded[j][:], in_=src[b][:, :, c0 : c0 + sizes[j]])
+            nc.sync.dma_start(out=loaded[j][:], in_=hbm[b][:, :, c0 : c0 + sizes[j]])
 
         def load_x(j):
-            load(x_loaded, x_v, X_LOADS, j)
+            load(x_loaded, x_hbm, X_LOADS, j)
 
         def load_agg(j):
-            load(agg_loaded, agg_v, AGG_LOADS, j)
+            load(agg_loaded, agg_hbm, AGG_LOADS, j)
 
-        nc.scalar.dma_start(out=xs[:], in_=x_scale.rearrange("o (p t) h w -> p (o t h w)", t=PACK))
-        nc.scalar.dma_start(out=b1[:], in_=g1b.rearrange("(p t) -> p t", t=PACK))
+        def load_words(dst, words):
+            nc.sync.dma_start(out=dst[:], in_=words.rearrange("p n t -> p (n t)").bitcast(I32))
+
+        nc.scalar.dma_start(out=xs[:], in_=x_scale.rearrange("o (p t) h w -> p (o t h w)", t=ROWS))
+        nc.scalar.dma_start(out=b1[:], in_=g1b.rearrange("(p t) -> p t", t=ROWS))
         warm = keep.tile([P, 1], F32, name="warm")
         nc.vector.memset(warm[:], 0.0)
         nc.scalar.activation(out=warm[:], in_=warm[:], func=ACT.Sigmoid)
+
         load_x(0)
         load_agg(0)
         load_agg(1)
@@ -97,16 +102,16 @@ def tile_graphaugmentation_pb_t_w8_kernel(
             nc.sync.dma_start(
                 out=s1_raw[32 * q : 32 * q + 8, :].bitcast(I32), in_=g1w_scales[:, 4 * q : 4 * q + 4, :].bitcast(I32)
             )
-        nc.sync.dma_start(out=w1_raw[0][:], in_=words(g1w_words[0]))
-        nc.sync.dma_start(out=w1_raw[1][:], in_=words(g1w_words[1]))
+        load_words(w1_raw[0], g1w_words[0])
+        load_words(w1_raw[1], g1w_words[1])
         load_x(1)
         for q in range(4):
             nc.sync.dma_start(
                 out=s2_raw[32 * q : 32 * q + 4, :].bitcast(I32), in_=g2w_scales[0, 4 * q : 4 * q + 4, :].bitcast(I32)
             )
-        nc.sync.dma_start(out=w2_raw[:], in_=words(g2w_words[0]))
+        load_words(w2_raw, g2w_words[0])
         load_agg(2)
-        nc.sync.dma_start(out=b2[:], in_=g2b.rearrange("(p t) -> p t", t=PACK))
+        nc.sync.dma_start(out=b2[:], in_=g2b.rearrange("(p t) -> p t", t=ROWS))
         for j in range(2, len(X_LOADS)):
             load_x(j)
             load_agg(j + 1)
@@ -116,86 +121,79 @@ def tile_graphaugmentation_pb_t_w8_kernel(
         s1 = keep.tile([P, C], U8, name="s1", align_bytes=64)
         s2 = keep.tile([P, C], U8, name="s2", align_bytes=64)
 
-        def permute(dst, src):
+        def move_columns(dst, src):
             nc.vector.tensor_copy(
-                out=dst[:].rearrange("p (t m) -> p m t", t=PACK), in_=src[:].rearrange("p (m t) -> p m t", t=PACK)
+                out=dst[:].rearrange("p (t m) -> p m t", t=ROWS), in_=src[:].rearrange("p (m t) -> p m t", t=ROWS)
             )
 
-        xw, xa, codes1, scales1, hp, hi, codes2, scales2, gt = ({} for _ in range(9))
+        x_wide, cat, cat_codes, cat_scales, hidden, hidden_woven, hidden_codes, hidden_scales, gate = (
+            {} for stage in range(9)
+        )
 
         def widen(h):
-            rows = PACK if h in X_BY_MATMUL else 2
-            xa[h] = four.tile([P, 2, PACK * WIDTHS[h]], BF16, name="xa", align_bytes=64)
-            xw[h] = three.tile([P, rows, PACK * WIDTHS[h] // rows], BF16, name="xw")
-            for t in range(PACK):
+            in_rows = h in X_BY_MATMUL
+            cat[h] = four.tile([P, 2, ROWS * WIDTHS[h]], BF16, name="cat", align_bytes=64)
+            x_wide[h] = three.tile([P, ROWS, WIDTHS[h]] if in_rows else [P, 2, 2 * WIDTHS[h]], BF16, name="x_wide")
+            for t in range(ROWS):
                 nc.vector.tensor_scalar(
-                    out=xw[h][:, t, :] if h in X_BY_MATMUL else xw[h][:, t // 2, t % 2 :: 2],
-                    in0=xb[h][:, t, :].bitcast(FP8),
+                    out=x_wide[h][:, t, :] if in_rows else x_wide[h][:, t // 2, t % 2 :: 2],
+                    in0=x_rows[h][:, t, :].bitcast(FP8),
                     scalar1=xs[:, t : t + 1],
                     scalar2=None,
                     op0=ALU.mult,
                 )
 
-        def join(copy, h):
-            if h in X_BY_MATMUL:
-                weave_by_matmul(xa[h][:, 0, :], xw[h][:], WIDTHS[h])
-                return
+        def weave(copy, dst, rows):
             copy(
-                out=xa[h][:, 0, :].bitcast(F32).rearrange("p (c u) -> p c u", u=2),
-                in_=xw[h][:].bitcast(F32).rearrange("p u c -> p c u"),
+                out=dst.rearrange("p (c i t) -> p c t i", i=NEIGHBOURS, t=ROWS),
+                in_=rows.rearrange("p t (c i) -> p c t i", i=NEIGHBOURS),
             )
 
-        def weave(copy, dst, src):
-            copy(
-                out=dst.rearrange("p (c i t) -> p c t i", i=4, t=PACK),
-                in_=src.rearrange("p t (c i) -> p c t i", i=4),
-            )
-
-        def weave_by_matmul(dst, src, width):
-            n = min(width, BANK_BF16 // PACK)
+        def weave_by_matmul(dst, rows, width):
+            n = min(width, BANK_PIXELS)
             for c0 in range(0, width, n):
-                bank = banks.tile([P, PACK * n], BF16, name="bank")
+                bank = banks.tile([P, ROWS * n], BF16, name="bank")
                 for c in range(0, n, P):
                     nc.tensor.matmul(
-                        out=bank[:, PACK * c : PACK * (c + P)].rearrange("p (n t) -> p t n", t=PACK),
+                        out=bank[:, ROWS * c : ROWS * (c + P)].rearrange("p (n t) -> p t n", t=ROWS),
                         lhsT=ident[:],
-                        rhs=src[:, :, c0 + c : c0 + c + P],
+                        rhs=rows[:, :, c0 + c : c0 + c + P],
                         start=True,
                         stop=True,
                     )
-                nc.scalar.copy(out=dst[:, PACK * c0 : PACK * (c0 + n)], in_=bank[:])
+                nc.scalar.copy(out=dst[:, ROWS * c0 : ROWS * (c0 + n)], in_=bank[:])
+
+        def weave_x(h):
+            if h in X_BY_MATMUL:
+                weave_by_matmul(cat[h][:, 0, :], x_wide[h][:], WIDTHS[h])
+            else:
+                copy = nc.vector.tensor_copy if h in VECTOR_JOIN else nc.scalar.copy
+                copy(
+                    out=cat[h][:, 0, :].bitcast(F32).rearrange("p (n u) -> p n u", u=2),
+                    in_=x_wide[h][:].bitcast(F32).rearrange("p u n -> p n u"),
+                )
 
         def weave_agg(h):
-            if h < DIRECT:
-                weave(nc.scalar.copy, xa[h][:, 1, :], ag[h])
-            else:
-                weave_by_matmul(xa[h][:, 1, :], ag[h], WIDTHS[h])
+            c = min(max(SCALAR_WEAVES - STARTS[h], 0), WIDTHS[h])
+            if c > 0:
+                weave(nc.scalar.copy, cat[h][:, 1, : ROWS * c], agg_rows[h][:, :, :c])
+            if c < WIDTHS[h]:
+                weave_by_matmul(cat[h][:, 1, ROWS * c :], agg_rows[h][:, :, c:], WIDTHS[h] - c)
 
-        def quant_in(h):
-            n = WIDTHS[h]
-            codes1[h] = two.tile([P, 2, n], U32, name="codes1", align_bytes=64)
-            scales1[h] = two.tile([P, 2, n], U8, name="scales1", align_bytes=64)
+        def quantize_cat(h):
+            cat_codes[h] = two.tile([P, 2, WIDTHS[h]], U32, name="cat_codes", align_bytes=64)
+            cat_scales[h] = two.tile([P, 2, WIDTHS[h]], U8, name="cat_scales", align_bytes=64)
             nc.vector.quantize_mx(
-                out=codes1[h][:].rearrange("p g n -> p (g n)").bitcast(FP8X4),
-                scales=scales1[h][:].rearrange("p g n -> p (g n)"),
-                in_=xa[h][:].rearrange("p g m -> p (g m)"),
+                out=cat_codes[h][:].rearrange("p g n -> p (g n)").bitcast(FP8X4),
+                scales=cat_scales[h][:].rearrange("p g n -> p (g n)"),
+                in_=cat[h][:].rearrange("p g m -> p (g m)"),
             )
 
-        def weave_hidden(h):
-            hi[h] = two.tile([P, PACK * WIDTHS[h]], BF16, name="hi", align_bytes=64)
-            weave(nc.vector.tensor_copy, hi[h][:], hp[h][:])
-
-        def quant_hidden(h):
-            n = WIDTHS[h]
-            codes2[h] = two.tile([P, n], U32, name="codes2", align_bytes=64)
-            scales2[h] = two.tile([P, n], U8, name="scales2", align_bytes=64)
-            nc.vector.quantize_mx(out=codes2[h][:].bitcast(FP8X4), scales=scales2[h][:], in_=hi[h][:])
-
         def first_layer(h):
-            hp[h] = two.tile([P, PACK, WIDTHS[h]], BF16, name="hp")
+            hidden[h] = two.tile([P, ROWS, WIDTHS[h]], BF16, name="hidden")
             acc = {}
-            order = [(g, t) for t in range(PACK) for g in range(2)]
-            for g, t in sorted(order) if h == 0 else order:
+            passes = [(g, t) for t in range(ROWS) for g in range(2)]
+            for g, t in sorted(passes) if h == 0 else passes:
                 m = slice(P * t, P * t + P)
                 if g == 0:
                     acc[t] = banks.tile([P, WIDTHS[h]], F32, name="bank")
@@ -203,96 +201,106 @@ def tile_graphaugmentation_pb_t_w8_kernel(
                     out=acc[t][:],
                     lhsT=w1[g][:, m].bitcast(FP8X4),
                     lhsT_scale=s1[4 * g :, m],
-                    rhs=codes1[h][:, g, :].bitcast(FP8X4),
-                    rhs_scale=scales1[h][:, g, :],
+                    rhs=cat_codes[h][:, g, :].bitcast(FP8X4),
+                    rhs_scale=cat_scales[h][:, g, :],
                     start=(g == 0),
                     stop=(g == 1),
                 )
                 if g == 1:
-                    nc.scalar.activation(out=hp[h][:, t, :], in_=acc[t][:], func=ACT.Relu, bias=b1[:, t : t + 1])
+                    nc.scalar.activation(out=hidden[h][:, t, :], in_=acc[t][:], func=ACT.Relu, bias=b1[:, t : t + 1])
 
-        def second_layer(h, rows=range(PACK)):
-            if 0 in rows:
-                gt[h] = four.tile([P, PACK, WIDTHS[h]], F32, name="gt")
-            for t in rows:
+        def weave_hidden(h):
+            hidden_woven[h] = two.tile([P, ROWS * WIDTHS[h]], BF16, name="hidden_woven", align_bytes=64)
+            weave(nc.vector.tensor_copy, hidden_woven[h][:], hidden[h][:])
+
+        def quantize_hidden(h):
+            hidden_codes[h] = two.tile([P, WIDTHS[h]], U32, name="hidden_codes", align_bytes=64)
+            hidden_scales[h] = two.tile([P, WIDTHS[h]], U8, name="hidden_scales", align_bytes=64)
+            nc.vector.quantize_mx(
+                out=hidden_codes[h][:].bitcast(FP8X4), scales=hidden_scales[h][:], in_=hidden_woven[h][:]
+            )
+
+        def second_layer(h, t0=0, t1=ROWS):
+            if t0 == 0:
+                gate[h] = four.tile([P, ROWS, WIDTHS[h]], F32, name="gate")
+            for t in range(t0, t1):
                 m = slice(P * t, P * t + P)
                 acc = banks.tile([P, WIDTHS[h]], F32, name="bank")
                 nc.tensor.matmul_mx(
                     out=acc[:],
                     lhsT=w2[:, m].bitcast(FP8X4),
                     lhsT_scale=s2[:, m],
-                    rhs=codes2[h][:].bitcast(FP8X4),
-                    rhs_scale=scales2[h][:],
+                    rhs=hidden_codes[h][:].bitcast(FP8X4),
+                    rhs_scale=hidden_scales[h][:],
                     start=True,
                     stop=True,
                 )
-                nc.scalar.activation(out=gt[h][:, t, :], in_=acc[:], func=ACT.Sigmoid, bias=b2[:, t : t + 1])
+                nc.scalar.activation(out=gate[h][:, t, :], in_=acc[:], func=ACT.Sigmoid, bias=b2[:, t : t + 1])
 
         def product(h, t0, t1):
-            b, px = where(h)
-            ts = slice(t0, t1)
-            nc.vector.tensor_tensor(out=gt[h][:, ts, :], in0=gt[h][:, ts, :], in1=ag[h][:, ts, :], op=ALU.mult)
-            nc.sync.dma_start(out=out_v[b][:, ts, px], in_=gt[h][:, ts, :])
+            b, c0 = divmod(STARTS[h], PIX)
+            rows = gate[h][:, t0:t1, :]
+            nc.vector.tensor_tensor(out=rows, in0=rows, in1=agg_rows[h][:, t0:t1, :], op=ALU.mult)
+            nc.sync.dma_start(out=out_hbm[b][:, t0:t1, c0 : c0 + WIDTHS[h]], in_=rows)
 
         widen(0)
         weave_agg(0)
         widen(1)
-        join(nc.vector.tensor_copy, 0)
+        weave_x(0)
         weave_agg(1)
-        join(nc.scalar.copy, 1)
-        permute(s1, s1_raw)
-        quant_in(0)
-        permute(w1[0], w1_raw[0])
-        permute(w1[1], w1_raw[1])
-        quant_in(1)
+        weave_x(1)
+        move_columns(s1, s1_raw)
+        quantize_cat(0)
+        move_columns(w1[0], w1_raw[0])
+        move_columns(w1[1], w1_raw[1])
+        quantize_cat(1)
         widen(2)
         first_layer(0)
         first_layer(1)
-        permute(s2, s2_raw)
+        move_columns(s2, s2_raw)
+        weave_x(2)
         weave_hidden(0)
-        permute(w2, w2_raw)
-        quant_hidden(0)
-        join(nc.scalar.copy, 2)
+        move_columns(w2, w2_raw)
+        quantize_hidden(0)
         weave_agg(2)
         weave_hidden(1)
         widen(3)
-        quant_in(2)
-        quant_hidden(1)
+        quantize_cat(2)
+        quantize_hidden(1)
         second_layer(0)
-        join(nc.scalar.copy, 3)
+        weave_x(3)
         weave_agg(3)
         product(0, 0, 2)
         product(0, 2, 4)
-        for s in range(2, COUNT - 2):
+        for s in range(2, LAST - 1):
             first_layer(s)
             second_layer(s - 1)
             widen(s + 2)
             weave_agg(s + 2)
             if s + 2 not in VECTOR_JOIN:
-                join(nc.scalar.copy, s + 2)
-            quant_in(s + 1)
+                weave_x(s + 2)
+            quantize_cat(s + 1)
             weave_hidden(s)
             if s + 2 in VECTOR_JOIN:
-                join(nc.vector.tensor_copy, s + 2)
+                weave_x(s + 2)
             product(s - 1, 0, 2)
-            quant_hidden(s)
+            quantize_hidden(s)
             product(s - 1, 2, 4)
-        last = COUNT - 1
-        first_layer(last - 1)
-        quant_in(last)
-        second_layer(last - 2, range(0, 3))
-        first_layer(last)
-        second_layer(last - 2, range(3, 4))
-        weave_hidden(last - 1)
-        product(last - 2, 0, 2)
-        quant_hidden(last - 1)
-        product(last - 2, 2, 3)
-        weave_hidden(last)
-        product(last - 2, 3, 4)
-        quant_hidden(last)
-        second_layer(last - 1)
-        second_layer(last)
-        product(last - 1, 0, 2)
-        product(last - 1, 2, 4)
-        for t in range(4):
-            product(last, t, t + 1)
+        first_layer(LAST - 1)
+        quantize_cat(LAST)
+        second_layer(LAST - 2, 0, 3)
+        first_layer(LAST)
+        second_layer(LAST - 2, 3, 4)
+        weave_hidden(LAST - 1)
+        product(LAST - 2, 0, 2)
+        quantize_hidden(LAST - 1)
+        product(LAST - 2, 2, 3)
+        weave_hidden(LAST)
+        product(LAST - 2, 3, 4)
+        quantize_hidden(LAST)
+        second_layer(LAST - 1)
+        second_layer(LAST)
+        product(LAST - 1, 0, 2)
+        product(LAST - 1, 2, 4)
+        for t in range(ROWS):
+            product(LAST, t, t + 1)

@@ -153,11 +153,11 @@ def tile_graphaugmentation_pb_t_w8_kernel(
             n = min(width, BANK_PIXELS)
             for c0 in range(0, width, n):
                 bank = banks.tile([P, ROWS * n], BF16, name="bank")
-                for c in range(0, n, P):
+                for u in range(2):
                     nc.tensor.matmul(
-                        out=bank[:, ROWS * c : ROWS * (c + P)].rearrange("p (n t) -> p t n", t=ROWS),
+                        out=bank[:].rearrange("p (n u e) -> p u n e", u=2, e=2)[:, u],
                         lhsT=ident[:],
-                        rhs=rows[:, :, c0 + c : c0 + c + P],
+                        rhs=rows[:, 2 * u : 2 * u + 2, c0 : c0 + n].rearrange("p e n -> p n e"),
                         start=True,
                         stop=True,
                     )

@@ -31,7 +31,7 @@ AGG_LOADS = [256, 256] + [512] * 3 + [PIX] * (IMAGES - 2)
 
 FULL_FROM = 6
 X_BY_MATMUL = list(range(FULL_FROM, COUNT, 2)) + [LAST]
-VECTOR_JOIN = list(range(0, FULL_FROM, 2)) + [LAST - 2]
+VECTOR_JOIN = [0, 2, LAST - 2]
 WEAVING_MATMULS = FLOPS // 10 // (2 * P * P * ROWS * P)
 SCALAR_WEAVES = IMAGES * PIX + sum(WIDTHS[h] for h in X_BY_MATMUL) - WEAVING_MATMULS * P
 

@@ -152,16 +152,19 @@ def tile_graphaugmentation_pb_t_w8_kernel(
         def weave_by_matmul(dst, rows, width):
             n = min(width, BANK_PIXELS)
             for c0 in range(0, width, n):
-                bank = banks.tile([P, ROWS * n], BF16, name="bank")
+                bank = banks.tile([P, 2, n, 2], BF16, name="bank")
                 for u in range(2):
                     nc.tensor.matmul(
-                        out=bank[:].rearrange("p (n u e) -> p u n e", u=2, e=2)[:, u],
+                        out=bank[:, u],
                         lhsT=ident[:],
                         rhs=rows[:, 2 * u : 2 * u + 2, c0 : c0 + n].rearrange("p e n -> p n e"),
                         start=True,
                         stop=True,
                     )
-                nc.scalar.copy(out=dst[:, ROWS * c0 : ROWS * (c0 + n)], in_=bank[:])
+                nc.scalar.copy(
+                    out=dst[:, ROWS * c0 : ROWS * (c0 + n)].bitcast(F32).rearrange("p (n u) -> p n u", u=2),
+                    in_=bank[:].rearrange("p u n e -> p u (n e)").bitcast(F32).rearrange("p u n -> p n u"),
+                )
 
         def weave_x(h):
             if h in X_BY_MATMUL:

@@ -212,9 +212,11 @@ def tile_graphaugmentation_pb_t_w8_kernel(
                 if g == 1:
                     nc.scalar.activation(out=hidden[h][:, t, :], in_=acc[t][:], func=ACT.Relu, bias=b1[:, t : t + 1])
 
-        def weave_hidden(h):
-            hidden_woven[h] = two.tile([P, ROWS * WIDTHS[h]], BF16, name="hidden_woven", align_bytes=64)
-            weave(nc.vector.tensor_copy, hidden_woven[h][:], hidden[h][:])
+        def weave_hidden(h, copy=nc.vector.tensor_copy, c0=0, c1=None):
+            c1 = WIDTHS[h] if c1 is None else c1
+            if h not in hidden_woven:
+                hidden_woven[h] = two.tile([P, ROWS * WIDTHS[h]], BF16, name="hidden_woven", align_bytes=64)
+            weave(copy, hidden_woven[h][:, ROWS * c0 : ROWS * c1], hidden[h][:, :, c0:c1])
 
         def quantize_hidden(h):
             hidden_codes[h] = two.tile([P, WIDTHS[h]], U32, name="hidden_codes", align_bytes=64)
@@ -275,7 +277,7 @@ def tile_graphaugmentation_pb_t_w8_kernel(
         weave_agg(3)
         product(0, 0, 2)
         product(0, 2, 4)
-        for s in range(2, LAST - 1):
+        for s in range(2, LAST - 2):
             first_layer(s)
             second_layer(s - 1)
             widen(s + 2)
@@ -289,19 +291,35 @@ def tile_graphaugmentation_pb_t_w8_kernel(
             product(s - 1, 0, 2)
             quantize_hidden(s)
             product(s - 1, 2, 4)
+        s = LAST - 2
+        first_layer(s)
+        second_layer(s - 1)
+        widen(LAST)
+        weave_agg(LAST)
+        weave_x(LAST)
+        quantize_cat(LAST - 1)
+        weave_hidden(s)
+        product(s - 1, 0, 1)
+        quantize_hidden(s)
         first_layer(LAST - 1)
+        product(s - 1, 1, 2)
         quantize_cat(LAST)
-        second_layer(LAST - 2, 0, 3)
+        second_layer(s, 0, 1)
+        weave_hidden(LAST - 1, nc.scalar.copy, 192)
+        second_layer(s, 1, 3)
         first_layer(LAST)
-        second_layer(LAST - 2, 3, 4)
-        weave_hidden(LAST - 1)
-        product(LAST - 2, 0, 2)
+        second_layer(s, 3, 4)
+        product(s - 1, 2, 3)
+        weave_hidden(LAST - 1, c1=192)
+        product(s - 1, 3, 4)
         quantize_hidden(LAST - 1)
-        product(LAST - 2, 2, 3)
-        weave_hidden(LAST)
-        product(LAST - 2, 3, 4)
-        quantize_hidden(LAST)
         second_layer(LAST - 1)
+        product(s, 0, 1)
+        product(s, 1, 2)
+        product(s, 2, 3)
+        weave_hidden(LAST)
+        product(s, 3, 4)
+        quantize_hidden(LAST)
         second_layer(LAST)
         product(LAST - 1, 0, 2)
         product(LAST - 1, 2, 4)

@@ -16,7 +16,7 @@ ALU = mybir.AluOpType
 IMAGES, C, PIX = 6, 512, 1024
 P = 128
 ROWS = 4
-BANK_PIXELS = 256
+HALF = 256
 NEIGHBOURS = 4
 
 FLOPS = 2 * IMAGES * PIX * C * (2 * C + C)
@@ -29,11 +29,9 @@ STARTS = [sum(WIDTHS[:h]) for h in range(COUNT)]
 X_LOADS = [512] * 4 + [PIX] * (IMAGES - 2)
 AGG_LOADS = [256, 256] + [512] * 3 + [PIX] * (IMAGES - 2)
 
-FULL_FROM = 6
-X_BY_MATMUL = list(range(FULL_FROM, COUNT, 2)) + [LAST]
-VECTOR_JOIN = [0, 2, LAST - 2]
-WEAVING_MATMULS = FLOPS // 10 // (2 * P * P * ROWS * P)
-SCALAR_WEAVES = IMAGES * PIX + sum(WIDTHS[h] for h in X_BY_MATMUL) - WEAVING_MATMULS * P
+BY_GPSIMD = list(range(4, LAST))
+ROWS_FROM = LAST - 2
+LAST_ROW = 128
 
 
 def tile_graphaugmentation_pb_t_w8_kernel(
@@ -46,15 +44,18 @@ def tile_graphaugmentation_pb_t_w8_kernel(
 
     with ExitStack() as ctx:
         keep = ctx.enter_context(tc.tile_pool(name="keep", bufs=1))
+        one = ctx.enter_context(tc.tile_pool(name="one", bufs=1))
         two = ctx.enter_context(tc.tile_pool(name="two", bufs=2))
         three = ctx.enter_context(tc.tile_pool(name="three", bufs=3))
         four = ctx.enter_context(tc.tile_pool(name="four", bufs=4))
-        banks = ctx.enter_context(tc.psum_pool(name="banks", bufs=8))
+        vector_banks = ctx.enter_context(tc.psum_pool(name="vector_banks", bufs=4))
+        scalar_banks = ctx.enter_context(tc.psum_pool(name="scalar_banks", bufs=4))
         ctx.enter_context(tc.manual_schedule())
 
         xs = keep.tile([P, ROWS], F32, name="xs")
         b1 = keep.tile([P, ROWS], BF16, name="b1")
         b2 = keep.tile([P, ROWS], BF16, name="b2")
+        b1_pairs = keep.tile([P, 2, 2 * HALF], BF16, name="b1_pairs")
         ident = keep.tile([P, P], BF16, name="ident")
         make_identity(nc, ident[:])
 
@@ -126,97 +127,168 @@ def tile_graphaugmentation_pb_t_w8_kernel(
                 out=dst[:].rearrange("p (t m) -> p m t", t=ROWS), in_=src[:].rearrange("p (m t) -> p m t", t=ROWS)
             )
 
-        x_wide, cat, cat_codes, cat_scales, hidden, hidden_woven, hidden_codes, hidden_scales, gate = (
-            {} for stage in range(9)
-        )
+        def spread_bias():
+            nc.scalar.copy(
+                out=b1_pairs[:].rearrange("p u (n e) -> p u n e", e=2),
+                in_=b1[:].rearrange("p (u e) -> p u e", e=2).unsqueeze(2).to_broadcast([P, 2, HALF, 2]),
+            )
 
-        def widen(h):
-            in_rows = h in X_BY_MATMUL
-            cat[h] = four.tile([P, 2, ROWS * WIDTHS[h]], BF16, name="cat", align_bytes=64)
-            x_wide[h] = three.tile([P, ROWS, WIDTHS[h]] if in_rows else [P, 2, 2 * WIDTHS[h]], BF16, name="x_wide")
+        x_wide, x_woven, agg_woven, cat_codes, cat_scales, sums, biased, hidden = ({} for stage in range(8))
+        hidden_woven, hidden_codes, hidden_scales, gate, x_bank, agg_bank = ({} for stage in range(6))
+
+        def widen(h, engine, t0=0, t1=ROWS):
+            if t0 == 0:
+                x_wide[h] = three.tile([P, ROWS, WIDTHS[h]], BF16, name="x_wide")
+            for t in range(t0, t1):
+                codes = x_rows[h][:, t, :].bitcast(FP8)
+                if engine == "scalar":
+                    nc.scalar.activation(out=x_wide[h][:, t, :], in_=codes, func=ACT.Copy, scale=xs[:, t : t + 1])
+                else:
+                    nc.vector.tensor_scalar(
+                        out=x_wide[h][:, t, :], in0=codes, scalar1=xs[:, t : t + 1], scalar2=None, op0=ALU.mult
+                    )
+
+        def widen_pairs(h):
+            x_wide[h] = three.tile([P, 2, 2 * WIDTHS[h]], BF16, name="x_wide")
             for t in range(ROWS):
                 nc.vector.tensor_scalar(
-                    out=x_wide[h][:, t, :] if in_rows else x_wide[h][:, t // 2, t % 2 :: 2],
+                    out=x_wide[h][:, t // 2, t % 2 :: 2],
                     in0=x_rows[h][:, t, :].bitcast(FP8),
                     scalar1=xs[:, t : t + 1],
                     scalar2=None,
                     op0=ALU.mult,
                 )
 
-        def weave(copy, dst, rows):
-            copy(
-                out=dst.rearrange("p (c i t) -> p c t i", i=NEIGHBOURS, t=ROWS),
-                in_=rows.rearrange("p t (c i) -> p c t i", i=NEIGHBOURS),
-            )
+        def woven_tile(store, pool, name, h):
+            if h not in store:
+                store[h] = pool.tile([P, ROWS * WIDTHS[h]], BF16, name=name, align_bytes=64)
+            return store[h]
 
-        def weave_by_matmul(dst, rows, width):
-            n = min(width, BANK_PIXELS)
-            for c0 in range(0, width, n):
-                bank = banks.tile([P, 2, n, 2], BF16, name="bank")
-                for u in range(2):
-                    nc.tensor.matmul(
-                        out=bank[:, u],
-                        lhsT=ident[:],
-                        rhs=rows[:, 2 * u : 2 * u + 2, c0 : c0 + n].rearrange("p e n -> p n e"),
-                        start=True,
-                        stop=True,
-                    )
-                nc.scalar.copy(
-                    out=dst[:, ROWS * c0 : ROWS * (c0 + n)].bitcast(F32).rearrange("p (n u) -> p n u", u=2),
-                    in_=bank[:].rearrange("p u n e -> p u (n e)").bitcast(F32).rearrange("p u n -> p n u"),
+        def weave(engine, dst, rows, c0, c1):
+            if engine == "gpsimd":
+                nc.gpsimd.tensor_scalar(
+                    out=dst[:, ROWS * c0 : ROWS * c1].rearrange("p (n t) -> p n t", t=ROWS),
+                    in0=rows[:, :, c0:c1].rearrange("p t n -> p n t"),
+                    scalar1=1.0,
+                    scalar2=0.0,
+                    op0=ALU.mult,
+                    op1=ALU.add,
                 )
-
-        def weave_x(h):
-            if h in X_BY_MATMUL:
-                weave_by_matmul(cat[h][:, 0, :], x_wide[h][:], WIDTHS[h])
             else:
-                copy = nc.vector.tensor_copy if h in VECTOR_JOIN else nc.scalar.copy
+                copy = nc.vector.tensor_copy if engine == "vector" else nc.scalar.copy
                 copy(
-                    out=cat[h][:, 0, :].bitcast(F32).rearrange("p (n u) -> p n u", u=2),
-                    in_=x_wide[h][:].bitcast(F32).rearrange("p u n -> p n u"),
+                    out=dst[:, ROWS * c0 : ROWS * c1].rearrange("p (c i t) -> p c t i", i=NEIGHBOURS, t=ROWS),
+                    in_=rows[:, :, c0:c1].rearrange("p t (c i) -> p c t i", i=NEIGHBOURS),
                 )
 
-        def weave_agg(h):
-            c = min(max(SCALAR_WEAVES - STARTS[h], 0), WIDTHS[h])
-            if c > 0:
-                weave(nc.scalar.copy, cat[h][:, 1, : ROWS * c], agg_rows[h][:, :, :c])
-            if c < WIDTHS[h]:
-                weave_by_matmul(cat[h][:, 1, ROWS * c :], agg_rows[h][:, :, c:], WIDTHS[h] - c)
-
-        def quantize_cat(h):
-            cat_codes[h] = two.tile([P, 2, WIDTHS[h]], U32, name="cat_codes", align_bytes=64)
-            cat_scales[h] = two.tile([P, 2, WIDTHS[h]], U8, name="cat_scales", align_bytes=64)
-            nc.vector.quantize_mx(
-                out=cat_codes[h][:].rearrange("p g n -> p (g n)").bitcast(FP8X4),
-                scales=cat_scales[h][:].rearrange("p g n -> p (g n)"),
-                in_=cat[h][:].rearrange("p g m -> p (g m)"),
+        def join_x(h, copy):
+            dst = woven_tile(x_woven, two, "x_woven", h)
+            copy(
+                out=dst[:].bitcast(F32).rearrange("p (n u) -> p n u", u=2),
+                in_=x_wide[h][:].bitcast(F32).rearrange("p u n -> p n u"),
             )
 
-        def first_layer(h):
-            hidden[h] = two.tile([P, ROWS, WIDTHS[h]], BF16, name="hidden")
-            acc = {}
-            passes = [(g, t) for t in range(ROWS) for g in range(2)]
-            for g, t in sorted(passes) if h == 0 else passes:
-                m = slice(P * t, P * t + P)
-                if g == 0:
-                    acc[t] = banks.tile([P, WIDTHS[h]], F32, name="bank")
-                nc.tensor.matmul_mx(
-                    out=acc[t][:],
-                    lhsT=w1[g][:, m].bitcast(FP8X4),
-                    lhsT_scale=s1[4 * g :, m],
-                    rhs=cat_codes[h][:, g, :].bitcast(FP8X4),
-                    rhs_scale=cat_scales[h][:, g, :],
-                    start=(g == 0),
-                    stop=(g == 1),
-                )
-                if g == 1:
-                    nc.scalar.activation(out=hidden[h][:, t, :], in_=acc[t][:], func=ACT.Relu, bias=b1[:, t : t + 1])
+        def weave_x(h, engine, c0=0, c1=None):
+            weave(engine, woven_tile(x_woven, two, "x_woven", h), x_wide[h], c0, WIDTHS[h] if c1 is None else c1)
 
-        def weave_hidden(h, copy=nc.vector.tensor_copy, c0=0, c1=None):
-            c1 = WIDTHS[h] if c1 is None else c1
-            if h not in hidden_woven:
-                hidden_woven[h] = two.tile([P, ROWS * WIDTHS[h]], BF16, name="hidden_woven", align_bytes=64)
-            weave(copy, hidden_woven[h][:, ROWS * c0 : ROWS * c1], hidden[h][:, :, c0:c1])
+        def pair_in_bank(rows, c0, c1):
+            bank = scalar_banks.tile([P, 2, c1 - c0, 2], BF16, name="bank")
+            for u in range(2):
+                nc.tensor.matmul(
+                    out=bank[:, u],
+                    lhsT=ident[:],
+                    rhs=rows[:, 2 * u : 2 * u + 2, c0:c1].rearrange("p e n -> p n e"),
+                    start=True,
+                    stop=True,
+                )
+            return bank
+
+        def join_bank(bank, dst, c0, c1):
+            nc.scalar.copy(
+                out=dst[:, ROWS * c0 : ROWS * c1].bitcast(F32).rearrange("p (n u) -> p n u", u=2),
+                in_=bank[:].rearrange("p u n e -> p u (n e)").bitcast(F32).rearrange("p u n -> p n u"),
+            )
+
+        def pair_x(h, c0, c1):
+            x_bank[h, c0] = pair_in_bank(x_wide[h], c0, c1)
+
+        def join_x_bank(h, c0, c1):
+            join_bank(x_bank[h, c0], woven_tile(x_woven, two, "x_woven", h), c0, c1)
+
+        def agg_tile(h):
+            pool, name = (one, "agg_woven") if h in BY_GPSIMD else (two, "agg_woven_first")
+            return woven_tile(agg_woven, pool, name, h)
+
+        def weave_agg_by_matmul(h, c0, c1):
+            join_bank(pair_in_bank(agg_rows[h], c0, c1), agg_tile(h), c0, c1)
+
+        def weave_agg(h, engine, c0=0, c1=None):
+            weave(engine, agg_tile(h), agg_rows[h], c0, WIDTHS[h] if c1 is None else c1)
+
+        def quantize_cat(h, g):
+            if h not in cat_codes:
+                cat_codes[h] = two.tile([P, 2, WIDTHS[h]], U32, name="cat_codes", align_bytes=64)
+                cat_scales[h] = two.tile([P, 2, WIDTHS[h]], U8, name="cat_scales", align_bytes=64)
+            nc.vector.quantize_mx(
+                out=cat_codes[h][:, g, :].bitcast(FP8X4),
+                scales=cat_scales[h][:, g, :],
+                in_=(x_woven, agg_woven)[g][h][:],
+            )
+
+        def first_pass(dst, h, g, t, n):
+            m = slice(P * t, P * t + P)
+            nc.tensor.matmul_mx(
+                out=dst,
+                lhsT=w1[g][:, m].bitcast(FP8X4),
+                lhsT_scale=s1[4 * g :, m],
+                rhs=cat_codes[h][:, g, n].bitcast(FP8X4),
+                rhs_scale=cat_scales[h][:, g, n],
+                start=(g == 0),
+                stop=(g == 1),
+            )
+
+        def first_layer(h, j0=0, j1=None):
+            for j in range(j0, WIDTHS[h] // P if j1 is None else j1):
+                c, u = divmod(j, 2)
+                sums[h, j] = vector_banks.tile([P, 2, HALF], F32, name="bank")
+                for e in range(2):
+                    for g in range(2):
+                        first_pass(sums[h, j][:, e, :], h, g, 2 * u + e, slice(HALF * c, HALF * (c + 1)))
+
+        def add_bias(h, j0=0, j1=None):
+            if j0 == 0:
+                biased[h] = two.tile([P, 2, 2 * WIDTHS[h]], BF16, name="biased")
+            for j in range(j0, WIDTHS[h] // P if j1 is None else j1):
+                c, u = divmod(j, 2)
+                nc.vector.tensor_tensor(
+                    out=biased[h][:, u, 2 * HALF * c : 2 * HALF * (c + 1)].rearrange("p (n e) -> p n e", e=2),
+                    in0=b1_pairs[:, u, :].rearrange("p (n e) -> p n e", e=2),
+                    in1=sums[h, j][:].rearrange("p e n -> p n e"),
+                    op=ALU.add,
+                )
+
+        def relu(h):
+            dst = woven_tile(hidden_woven, two, "hidden_woven", h)
+            nc.vector.tensor_scalar(
+                out=dst[:].rearrange("p (n u e) -> p n u e", u=2, e=2),
+                in0=biased[h][:].rearrange("p u (n e) -> p n u e", e=2),
+                scalar1=0.0,
+                scalar2=None,
+                op0=ALU.max,
+            )
+
+        def first_layer_rows(h, t0=0, t1=ROWS):
+            if t0 == 0:
+                hidden[h] = two.tile([P, ROWS, WIDTHS[h]], BF16, name="hidden")
+            for t in range(t0, t1):
+                acc = scalar_banks.tile([P, WIDTHS[h]], F32, name="bank")
+                for g in range(2):
+                    first_pass(acc[:], h, g, t, slice(0, WIDTHS[h]))
+                nc.scalar.activation(out=hidden[h][:, t, :], in_=acc[:], func=ACT.Relu, bias=b1[:, t : t + 1])
+
+        def weave_hidden(h, engine, c0=0, c1=None):
+            dst = woven_tile(hidden_woven, two, "hidden_woven", h)
+            weave(engine, dst, hidden[h], c0, WIDTHS[h] if c1 is None else c1)
 
         def quantize_hidden(h):
             hidden_codes[h] = two.tile([P, WIDTHS[h]], U32, name="hidden_codes", align_bytes=64)
@@ -230,7 +302,7 @@ def tile_graphaugmentation_pb_t_w8_kernel(
                 gate[h] = four.tile([P, ROWS, WIDTHS[h]], F32, name="gate")
             for t in range(t0, t1):
                 m = slice(P * t, P * t + P)
-                acc = banks.tile([P, WIDTHS[h]], F32, name="bank")
+                acc = scalar_banks.tile([P, WIDTHS[h]], F32, name="bank")
                 nc.tensor.matmul_mx(
                     out=acc[:],
                     lhsT=w2[:, m].bitcast(FP8X4),
@@ -242,86 +314,136 @@ def tile_graphaugmentation_pb_t_w8_kernel(
                 )
                 nc.scalar.activation(out=gate[h][:, t, :], in_=acc[:], func=ACT.Sigmoid, bias=b2[:, t : t + 1])
 
-        def product(h, t0, t1):
-            b, c0 = divmod(STARTS[h], PIX)
-            rows = gate[h][:, t0:t1, :]
-            nc.vector.tensor_tensor(out=rows, in0=rows, in1=agg_rows[h][:, t0:t1, :], op=ALU.mult)
-            nc.sync.dma_start(out=out_hbm[b][:, t0:t1, c0 : c0 + WIDTHS[h]], in_=rows)
+        def agg_to_bank(h, a, b):
+            agg_bank[h, a] = vector_banks.tile([P, b - a], BF16, name="bank")
+            for t in range(a // WIDTHS[h], (b - 1) // WIDTHS[h] + 1):
+                n = min(b - t * WIDTHS[h], WIDTHS[h])
+                c0 = t * WIDTHS[h] - a
+                nc.tensor.matmul(
+                    out=agg_bank[h, a][:, c0 : c0 + n], lhsT=ident[:], rhs=agg_rows[h][:, t, :n], start=True, stop=True
+                )
 
-        widen(0)
-        weave_agg(0)
-        widen(1)
-        weave_x(0)
-        weave_agg(1)
-        weave_x(1)
+        def product_from_bank(h, a, b):
+            part = gate[h][:].rearrange("p t n -> p (t n)")[:, a:b]
+            nc.vector.tensor_tensor(out=part, in0=part, in1=agg_bank[h, a][:], op=ALU.mult)
+
+        def store(h, t0, t1):
+            b, c0 = divmod(STARTS[h], PIX)
+            nc.sync.dma_start(out=out_hbm[b][:, t0:t1, c0 : c0 + WIDTHS[h]], in_=gate[h][:, t0:t1, :])
+
+        def product(h, t0, t1, engine="vector", c0=0):
+            rows = gate[h][:, t0:t1, c0:]
+            multiply = nc.vector.tensor_tensor if engine == "vector" else nc.gpsimd.tensor_tensor
+            multiply(out=rows, in0=rows, in1=agg_rows[h][:, t0:t1, c0:], op=ALU.mult)
+
+        widen_pairs(0)
+        weave_agg(0, "scalar")
+        widen_pairs(1)
+        join_x(0, nc.vector.tensor_copy)
+        weave_agg(1, "scalar")
+        join_x(1, nc.scalar.copy)
+        spread_bias()
         move_columns(s1, s1_raw)
-        quantize_cat(0)
+        quantize_cat(0, 0)
+        quantize_cat(0, 1)
         move_columns(w1[0], w1_raw[0])
         move_columns(w1[1], w1_raw[1])
-        quantize_cat(1)
-        widen(2)
-        first_layer(0)
-        first_layer(1)
+        quantize_cat(1, 0)
+        quantize_cat(1, 1)
+        widen_pairs(2)
+        first_layer_rows(0)
+        first_layer_rows(1)
         move_columns(s2, s2_raw)
-        weave_x(2)
-        weave_hidden(0)
+        join_x(2, nc.vector.tensor_copy)
+        weave_hidden(0, "vector")
         move_columns(w2, w2_raw)
         quantize_hidden(0)
-        weave_agg(2)
-        weave_hidden(1)
-        widen(3)
-        quantize_cat(2)
+        weave_agg_by_matmul(2, 0, HALF)
+        weave_agg_by_matmul(2, HALF, 2 * HALF)
+        weave_hidden(1, "vector")
+        widen_pairs(3)
+        quantize_cat(2, 0)
+        quantize_cat(2, 1)
         quantize_hidden(1)
         second_layer(0)
-        weave_x(3)
-        weave_agg(3)
-        product(0, 0, 2)
-        product(0, 2, 4)
-        for s in range(2, LAST - 2):
-            first_layer(s)
-            second_layer(s - 1)
-            widen(s + 2)
-            weave_agg(s + 2)
-            if s + 2 not in VECTOR_JOIN:
-                weave_x(s + 2)
-            quantize_cat(s + 1)
-            weave_hidden(s)
-            if s + 2 in VECTOR_JOIN:
-                weave_x(s + 2)
-            product(s - 1, 0, 2)
-            quantize_hidden(s)
-            product(s - 1, 2, 4)
-        s = LAST - 2
-        first_layer(s)
+        join_x(3, nc.scalar.copy)
+        weave_agg_by_matmul(3, 0, HALF)
+        weave_agg_by_matmul(3, HALF, 2 * HALF)
+        first_layer(2)
+        widen(4, "vector")
+        second_layer(1)
+        product(0, 0, 4)
+        store(0, 0, 4)
+        for s in range(2, ROWS_FROM):
+            half = WIDTHS[s + 2] // 2
+            if s > 2:
+                relu(s - 1)
+            quantize_cat(s + 1, 0)
+            if s > 2:
+                quantize_hidden(s - 1)
+            quantize_cat(s + 1, 1)
+            if s > 2:
+                second_layer(s - 1)
+            weave_agg(s + 2, "gpsimd")
+            add_bias(s)
+            h = s - 1
+            w = WIDTHS[h]
+            last_row = w if w == HALF else LAST_ROW
+            agg_to_bank(h, 0, 2 * w)
+            agg_to_bank(h, 2 * w, 3 * w + last_row)
+            pair_x(s + 2, 0, half)
+            weave_x(s + 2, "scalar", half)
+            join_x_bank(s + 2, 0, half)
+            product_from_bank(h, 0, 2 * w)
+            store(h, 0, 2)
+            product_from_bank(h, 2 * w, 3 * w + last_row)
+            if last_row < w:
+                product(h, 3, 4, "gpsimd", last_row)
+            store(h, 2, ROWS)
+            if s + 1 < ROWS_FROM:
+                first_layer(s + 1)
+            widen(s + 3, "scalar")
+        s = ROWS_FROM
+        w = WIDTHS[s]
+        first_layer_rows(s)
+        relu(s - 1)
+        quantize_cat(s + 1, 0)
+        quantize_hidden(s - 1)
+        quantize_cat(s + 1, 1)
         second_layer(s - 1)
-        widen(LAST)
-        weave_agg(LAST)
-        weave_x(LAST)
-        quantize_cat(LAST - 1)
-        weave_hidden(s)
-        product(s - 1, 0, 1)
+        weave_x(LAST, "vector")
+        weave_agg(LAST, "vector")
+        quantize_cat(LAST, 0)
+        weave_hidden(s, "vector")
+        quantize_cat(LAST, 1)
         quantize_hidden(s)
-        first_layer(LAST - 1)
-        product(s - 1, 1, 2)
-        quantize_cat(LAST)
-        second_layer(s, 0, 1)
-        weave_hidden(LAST - 1, nc.scalar.copy, 192)
-        second_layer(s, 1, 3)
-        first_layer(LAST)
-        second_layer(s, 3, 4)
-        product(s - 1, 2, 3)
-        weave_hidden(LAST - 1, c1=192)
-        product(s - 1, 3, 4)
-        quantize_hidden(LAST - 1)
-        second_layer(LAST - 1)
+        agg_to_bank(s - 1, 0, 2 * w)
+        agg_to_bank(s - 1, 2 * w, 3 * w)
+        first_layer_rows(s + 1)
+        product_from_bank(s - 1, 0, 2 * w)
+        store(s - 1, 0, 2)
+        product(s - 1, 3, 4, "gpsimd")
+        product_from_bank(s - 1, 2 * w, 3 * w)
+        store(s - 1, 2, 4)
+        second_layer(s, 0, 2)
+        first_layer_rows(LAST)
+        second_layer(s, 2, 4)
+        weave_hidden(s + 1, "vector")
         product(s, 0, 1)
+        quantize_hidden(s + 1)
+        second_layer(s + 1)
         product(s, 1, 2)
+        store(s, 0, 2)
+        weave_hidden(LAST, "vector")
         product(s, 2, 3)
-        weave_hidden(LAST)
-        product(s, 3, 4)
         quantize_hidden(LAST)
         second_layer(LAST)
-        product(LAST - 1, 0, 2)
-        product(LAST - 1, 2, 4)
+        product(s, 3, 4)
+        store(s, 2, 4)
+        product(s + 1, 0, 2)
+        store(s + 1, 0, 2)
+        product(s + 1, 2, 4)
+        store(s + 1, 2, 4)
         for t in range(ROWS):
             product(LAST, t, t + 1)
+            store(LAST, t, t + 1)

@@ -17,6 +17,7 @@ IMAGES, C, PIX = 6, 512, 1024
 P = 128
 ROWS = 4
 HALF = 256
+SPREAD = 16
 NEIGHBOURS = 4
 
 FLOPS = 2 * IMAGES * PIX * C * (2 * C + C)
@@ -29,9 +30,9 @@ STARTS = [sum(WIDTHS[:h]) for h in range(COUNT)]
 X_LOADS = [512] * 4 + [PIX] * (IMAGES - 2)
 AGG_LOADS = [256, 256] + [512] * 3 + [PIX] * (IMAGES - 2)
 
-BY_GPSIMD = list(range(4, LAST))
+BY_GPSIMD = list(range(3, LAST))
 ROWS_FROM = LAST - 2
-LAST_ROW = 128
+LAST_ROW = 64
 
 
 def tile_graphaugmentation_pb_t_w8_kernel(
@@ -55,7 +56,7 @@ def tile_graphaugmentation_pb_t_w8_kernel(
         xs = keep.tile([P, ROWS], F32, name="xs")
         b1 = keep.tile([P, ROWS], BF16, name="b1")
         b2 = keep.tile([P, ROWS], BF16, name="b2")
-        b1_pairs = keep.tile([P, 2, 2 * HALF], BF16, name="b1_pairs")
+        b1_pairs = keep.tile([P, 2, 4 * SPREAD], BF16, name="b1_pairs")
         ident = keep.tile([P, P], BF16, name="ident")
         make_identity(nc, ident[:])
 
@@ -128,17 +129,18 @@ def tile_graphaugmentation_pb_t_w8_kernel(
             )
 
         def spread_bias():
-            nc.scalar.copy(
-                out=b1_pairs[:].rearrange("p u (n e) -> p u n e", e=2),
-                in_=b1[:].rearrange("p (u e) -> p u e", e=2).unsqueeze(2).to_broadcast([P, 2, HALF, 2]),
-            )
+            for u in range(2):
+                nc.scalar.copy(
+                    out=b1_pairs[:, u, :].rearrange("p (n e i) -> p n e i", e=2, i=2),
+                    in_=b1[:, 2 * u : 2 * u + 2].unsqueeze(1).unsqueeze(3).to_broadcast([P, SPREAD, 2, 2]),
+                )
 
         x_wide, x_woven, agg_woven, cat_codes, cat_scales, sums, biased, hidden = ({} for stage in range(8))
         hidden_woven, hidden_codes, hidden_scales, gate, x_bank, agg_bank = ({} for stage in range(6))
 
         def widen(h, engine, t0=0, t1=ROWS):
             if t0 == 0:
-                x_wide[h] = three.tile([P, ROWS, WIDTHS[h]], BF16, name="x_wide")
+                x_wide[h] = four.tile([P, ROWS, WIDTHS[h]], BF16, name="x_wide")
             for t in range(t0, t1):
                 codes = x_rows[h][:, t, :].bitcast(FP8)
                 if engine == "scalar":
@@ -149,7 +151,7 @@ def tile_graphaugmentation_pb_t_w8_kernel(
                     )
 
         def widen_pairs(h):
-            x_wide[h] = three.tile([P, 2, 2 * WIDTHS[h]], BF16, name="x_wide")
+            x_wide[h] = four.tile([P, 2, 2 * WIDTHS[h]], BF16, name="x_wide")
             for t in range(ROWS):
                 nc.vector.tensor_scalar(
                     out=x_wide[h][:, t // 2, t % 2 :: 2],
@@ -260,10 +262,14 @@ def tile_graphaugmentation_pb_t_w8_kernel(
                 biased[h] = two.tile([P, 2, 2 * WIDTHS[h]], BF16, name="biased")
             for j in range(j0, WIDTHS[h] // P if j1 is None else j1):
                 c, u = divmod(j, 2)
+                pixels = biased[h][:, u, 2 * HALF * c : 2 * HALF * (c + 1)]
                 nc.vector.tensor_tensor(
-                    out=biased[h][:, u, 2 * HALF * c : 2 * HALF * (c + 1)].rearrange("p (n e) -> p n e", e=2),
-                    in0=b1_pairs[:, u, :].rearrange("p (n e) -> p n e", e=2),
-                    in1=sums[h, j][:].rearrange("p e n -> p n e"),
+                    out=pixels.rearrange("p (r n i e) -> p r n e i", n=SPREAD, i=2, e=2),
+                    in0=b1_pairs[:, u, :]
+                    .rearrange("p (n e i) -> p n e i", e=2, i=2)
+                    .unsqueeze(1)
+                    .to_broadcast([P, HALF // (2 * SPREAD), SPREAD, 2, 2]),
+                    in1=sums[h, j][:].rearrange("p e (r n i) -> p r n e i", n=SPREAD, i=2),
                     op=ALU.add,
                 )
 
@@ -323,9 +329,10 @@ def tile_graphaugmentation_pb_t_w8_kernel(
                     out=agg_bank[h, a][:, c0 : c0 + n], lhsT=ident[:], rhs=agg_rows[h][:, t, :n], start=True, stop=True
                 )
 
-        def product_from_bank(h, a, b):
+        def product_from_bank(h, a, b, first=None):
+            first = a if first is None else first
             part = gate[h][:].rearrange("p t n -> p (t n)")[:, a:b]
-            nc.vector.tensor_tensor(out=part, in0=part, in1=agg_bank[h, a][:], op=ALU.mult)
+            nc.vector.tensor_tensor(out=part, in0=part, in1=agg_bank[h, first][:, a - first : b - first], op=ALU.mult)
 
         def store(h, t0, t1):
             b, c0 = divmod(STARTS[h], PIX)
@@ -348,47 +355,62 @@ def tile_graphaugmentation_pb_t_w8_kernel(
         quantize_cat(0, 1)
         move_columns(w1[0], w1_raw[0])
         move_columns(w1[1], w1_raw[1])
+        first_layer(0)
         quantize_cat(1, 0)
         quantize_cat(1, 1)
-        widen_pairs(2)
-        first_layer_rows(0)
-        first_layer_rows(1)
+        first_layer(1)
+        widen(2, "scalar")
         move_columns(s2, s2_raw)
-        join_x(2, nc.vector.tensor_copy)
-        weave_hidden(0, "vector")
         move_columns(w2, w2_raw)
-        quantize_hidden(0)
+        add_bias(0)
+        add_bias(1)
+        weave_agg(2, "scalar", HALF)
         weave_agg_by_matmul(2, 0, HALF)
-        weave_agg_by_matmul(2, HALF, 2 * HALF)
-        weave_hidden(1, "vector")
-        widen_pairs(3)
-        quantize_cat(2, 0)
-        quantize_cat(2, 1)
-        quantize_hidden(1)
-        second_layer(0)
-        join_x(3, nc.scalar.copy)
+        relu(0)
+        weave_x(2, "vector")
+        quantize_hidden(0)
+        widen(3, "scalar")
         weave_agg_by_matmul(3, 0, HALF)
         weave_agg_by_matmul(3, HALF, 2 * HALF)
+        second_layer(0)
+        relu(1)
+        quantize_cat(2, 0)
+        quantize_hidden(1)
+        quantize_cat(2, 1)
         first_layer(2)
-        widen(4, "vector")
+        weave_x(3, "vector")
+        widen(4, "scalar")
         second_layer(1)
-        product(0, 0, 4)
+        quantize_cat(3, 0)
+        quantize_cat(3, 1)
+        weave_agg(4, "gpsimd")
+        add_bias(2)
+        agg_to_bank(0, 0, 2 * HALF)
+        agg_to_bank(1, 0, 4 * HALF)
+        pair_x(4, 0, HALF)
+        weave_x(4, "scalar", HALF)
+        join_x_bank(4, 0, HALF)
+        product(0, 2, 4, "gpsimd")
+        product_from_bank(0, 0, 2 * HALF)
         store(0, 0, 4)
-        for s in range(2, ROWS_FROM):
-            half = WIDTHS[s + 2] // 2
-            if s > 2:
-                relu(s - 1)
-            quantize_cat(s + 1, 0)
-            if s > 2:
-                quantize_hidden(s - 1)
-            quantize_cat(s + 1, 1)
-            if s > 2:
-                second_layer(s - 1)
-            weave_agg(s + 2, "gpsimd")
-            add_bias(s)
+        product_from_bank(1, 0, 4 * HALF)
+        store(1, 0, 4)
+        first_layer(3)
+        widen(5, "scalar")
+        for s in range(3, ROWS_FROM):
             h = s - 1
             w = WIDTHS[h]
-            last_row = w if w == HALF else LAST_ROW
+            half = WIDTHS[s + 2] // 2
+            last_row = HALF if s + 3 == LAST else LAST_ROW
+            relu(h)
+            quantize_cat(s + 1, 0)
+            quantize_hidden(h)
+            quantize_cat(s + 1, 1)
+            second_layer(h)
+            weave_agg(s + 2, "gpsimd")
+            if s + 3 == LAST:
+                weave_agg(LAST, "gpsimd")
+            add_bias(s)
             agg_to_bank(h, 0, 2 * w)
             agg_to_bank(h, 2 * w, 3 * w + last_row)
             pair_x(s + 2, 0, half)
@@ -397,12 +419,14 @@ def tile_graphaugmentation_pb_t_w8_kernel(
             product_from_bank(h, 0, 2 * w)
             store(h, 0, 2)
             product_from_bank(h, 2 * w, 3 * w + last_row)
-            if last_row < w:
-                product(h, 3, 4, "gpsimd", last_row)
+            product(h, 3, 4, "gpsimd", last_row)
             store(h, 2, ROWS)
             if s + 1 < ROWS_FROM:
                 first_layer(s + 1)
-            widen(s + 3, "scalar")
+            if s + 3 < LAST:
+                widen(s + 3, "scalar")
+            if s + 4 == LAST:
+                widen(LAST, "scalar")
         s = ROWS_FROM
         w = WIDTHS[s]
         first_layer_rows(s)
@@ -410,40 +434,46 @@ def tile_graphaugmentation_pb_t_w8_kernel(
         quantize_cat(s + 1, 0)
         quantize_hidden(s - 1)
         quantize_cat(s + 1, 1)
+        weave_x(LAST, "scalar", P)
         second_layer(s - 1)
-        weave_x(LAST, "vector")
-        weave_agg(LAST, "vector")
-        quantize_cat(LAST, 0)
-        weave_hidden(s, "vector")
+        weave_x(LAST, "vector", 0, P)
         quantize_cat(LAST, 1)
-        quantize_hidden(s)
-        agg_to_bank(s - 1, 0, 2 * w)
-        agg_to_bank(s - 1, 2 * w, 3 * w)
+        weave_hidden(s, "vector", 0, HALF)
+        quantize_cat(LAST, 0)
+        weave_hidden(s, "vector", HALF)
+        agg_to_bank(s - 1, w, 3 * w)
         first_layer_rows(s + 1)
-        product_from_bank(s - 1, 0, 2 * w)
-        store(s - 1, 0, 2)
-        product(s - 1, 3, 4, "gpsimd")
-        product_from_bank(s - 1, 2 * w, 3 * w)
-        store(s - 1, 2, 4)
+        product(s - 1, 0, 1)
+        store(s - 1, 0, 1)
+        quantize_hidden(s)
         second_layer(s, 0, 2)
         first_layer_rows(LAST)
         second_layer(s, 2, 4)
+        product(s - 1, 3, 4, "gpsimd")
+        for t in (1, 2):
+            product_from_bank(s - 1, t * w, (t + 1) * w, w)
+            store(s - 1, t, t + 1)
+        store(s - 1, 3, 4)
         weave_hidden(s + 1, "vector")
         product(s, 0, 1)
+        store(s, 0, 1)
         quantize_hidden(s + 1)
         second_layer(s + 1)
         product(s, 1, 2)
-        store(s, 0, 2)
+        store(s, 1, 2)
         weave_hidden(LAST, "vector")
         product(s, 2, 3)
+        store(s, 2, 3)
         quantize_hidden(LAST)
         second_layer(LAST)
         product(s, 3, 4)
-        store(s, 2, 4)
+        store(s, 3, 4)
         product(s + 1, 0, 2)
         store(s + 1, 0, 2)
         product(s + 1, 2, 4)
         store(s + 1, 2, 4)
-        for t in range(ROWS):
+        product(LAST, 0, 2)
+        store(LAST, 0, 2)
+        for t in range(2, ROWS):
             product(LAST, t, t + 1)
             store(LAST, t, t + 1)

@@ -227,14 +227,15 @@ def tile_graphaugmentation_pb_t_w8_kernel(
         def weave_agg(h, engine, c0=0, c1=None):
             weave(engine, agg_tile(h), agg_rows[h], c0, WIDTHS[h] if c1 is None else c1)
 
-        def quantize_cat(h, g):
+        def quantize_cat(h, g, c0=0, c1=None):
+            c1 = WIDTHS[h] if c1 is None else c1
             if h not in cat_codes:
                 cat_codes[h] = two.tile([P, 2, WIDTHS[h]], U32, name="cat_codes", align_bytes=64)
                 cat_scales[h] = two.tile([P, 2, WIDTHS[h]], U8, name="cat_scales", align_bytes=64)
             nc.vector.quantize_mx(
-                out=cat_codes[h][:, g, :].bitcast(FP8X4),
-                scales=cat_scales[h][:, g, :],
-                in_=(x_woven, agg_woven)[g][h][:],
+                out=cat_codes[h][:, g, c0:c1].bitcast(FP8X4),
+                scales=cat_scales[h][:, g, c0:c1],
+                in_=(x_woven, agg_woven)[g][h][:, ROWS * c0 : ROWS * c1],
             )
 
         def first_pass(dst, h, g, t, n):
@@ -381,8 +382,9 @@ def tile_graphaugmentation_pb_t_w8_kernel(
         weave_x(3, "vector")
         widen(4, "scalar")
         second_layer(1)
-        quantize_cat(3, 0)
+        quantize_cat(3, 0, HALF)
         quantize_cat(3, 1)
+        quantize_cat(3, 0, 0, HALF)
         weave_agg(4, "gpsimd")
         add_bias(2)
         agg_to_bank(0, 0, 2 * HALF)
@@ -403,9 +405,10 @@ def tile_graphaugmentation_pb_t_w8_kernel(
             half = WIDTHS[s + 2] // 2
             last_row = HALF if s + 3 == LAST else LAST_ROW
             relu(h)
-            quantize_cat(s + 1, 0)
+            quantize_cat(s + 1, 0, HALF)
             quantize_hidden(h)
             quantize_cat(s + 1, 1)
+            quantize_cat(s + 1, 0, 0, HALF)
             second_layer(h)
             weave_agg(s + 2, "gpsimd")
             if s + 3 == LAST:

@@ -250,10 +250,12 @@ def tile_graphaugmentation_pb_t_w8_kernel(
                 stop=(g == 1),
             )
 
-        def first_layer(h, j0=0, j1=None):
-            for j in range(j0, WIDTHS[h] // P if j1 is None else j1):
-                c, u = divmod(j, 2)
+        def first_layer(h, first_last=False):
+            count = WIDTHS[h] // P
+            for j in range(count):
                 sums[h, j] = vector_banks.tile([P, 2, HALF], F32, name="bank")
+            for j in list(range(1, count)) + [0] if first_last else range(count):
+                c, u = divmod(j, 2)
                 for e in range(2):
                     for g in range(2):
                         first_pass(sums[h, j][:, e, :], h, g, 2 * u + e, slice(HALF * c, HALF * (c + 1)))
@@ -397,7 +399,7 @@ def tile_graphaugmentation_pb_t_w8_kernel(
         store(0, 0, 4)
         product_from_bank(1, 0, 4 * HALF)
         store(1, 0, 4)
-        first_layer(3)
+        first_layer(3, first_last=True)
         widen(5, "scalar")
         for s in range(3, ROWS_FROM):
             h = s - 1
@@ -425,7 +427,7 @@ def tile_graphaugmentation_pb_t_w8_kernel(
             product(h, 3, 4, "gpsimd", last_row)
             store(h, 2, ROWS)
             if s + 1 < ROWS_FROM:
-                first_layer(s + 1)
+                first_layer(s + 1, first_last=True)
             if s + 3 < LAST:
                 widen(s + 3, "scalar")
             if s + 4 == LAST:

@@ -32,7 +32,10 @@ AGG_LOADS = [256, 256] + [512] * 3 + [PIX] * (IMAGES - 2)
 
 BY_GPSIMD = list(range(3, LAST))
 ROWS_FROM = LAST - 2
-LAST_ROW = 64
+VECTOR_PIXELS = 256
+VECTOR_PIXELS_LATE = 384
+HEAD_SPLIT = 96
+AGG_PAIRED = 64
 
 
 def tile_graphaugmentation_pb_t_w8_kernel(
@@ -323,19 +326,16 @@ def tile_graphaugmentation_pb_t_w8_kernel(
                 )
                 nc.scalar.activation(out=gate[h][:, t, :], in_=acc[:], func=ACT.Sigmoid, bias=b2[:, t : t + 1])
 
-        def agg_to_bank(h, a, b):
-            agg_bank[h, a] = vector_banks.tile([P, b - a], BF16, name="bank")
-            for t in range(a // WIDTHS[h], (b - 1) // WIDTHS[h] + 1):
-                n = min(b - t * WIDTHS[h], WIDTHS[h])
-                c0 = t * WIDTHS[h] - a
-                nc.tensor.matmul(
-                    out=agg_bank[h, a][:, c0 : c0 + n], lhsT=ident[:], rhs=agg_rows[h][:, t, :n], start=True, stop=True
-                )
+        def agg_to_bank(h, t0, t1, c1=None):
+            c1 = WIDTHS[h] if c1 is None else c1
+            bank = vector_banks.tile([P, t1 - t0, c1], BF16, name="bank")
+            for t in range(t0, t1):
+                agg_bank[h, t] = bank[:, t - t0 :, :]
+                nc.tensor.matmul(out=bank[:, t - t0, :], lhsT=ident[:], rhs=agg_rows[h][:, t, :c1], start=True, stop=True)
 
-        def product_from_bank(h, a, b, first=None):
-            first = a if first is None else first
-            part = gate[h][:].rearrange("p t n -> p (t n)")[:, a:b]
-            nc.vector.tensor_tensor(out=part, in0=part, in1=agg_bank[h, first][:, a - first : b - first], op=ALU.mult)
+        def product_from_bank(h, t0, t1, c1=None):
+            part = gate[h][:, t0:t1, :c1]
+            nc.vector.tensor_tensor(out=part, in0=part, in1=agg_bank[h, t0][:, : t1 - t0, :], op=ALU.mult)
 
         def store(h, t0, t1):
             b, c0 = divmod(STARTS[h], PIX)
@@ -346,12 +346,12 @@ def tile_graphaugmentation_pb_t_w8_kernel(
             multiply = nc.vector.tensor_tensor if engine == "vector" else nc.gpsimd.tensor_tensor
             multiply(out=rows, in0=rows, in1=agg_rows[h][:, t0:t1, c0:], op=ALU.mult)
 
+        widen(1, "scalar")
         widen_pairs(0)
         weave_agg(0, "scalar")
-        widen_pairs(1)
         join_x(0, nc.vector.tensor_copy)
+        weave_x(1, "vector")
         weave_agg(1, "scalar")
-        join_x(1, nc.scalar.copy)
         spread_bias()
         move_columns(s1, s1_raw)
         quantize_cat(0, 0)
@@ -362,26 +362,31 @@ def tile_graphaugmentation_pb_t_w8_kernel(
         quantize_cat(1, 0)
         quantize_cat(1, 1)
         first_layer(1)
-        widen(2, "scalar")
+        widen(2, "scalar", 0, 2)
         move_columns(s2, s2_raw)
-        move_columns(w2, w2_raw)
+        widen(2, "vector", 2, 4)
+        weave_x(2, "gpsimd", HEAD_SPLIT)
+        weave_x(2, "scalar", 0, HEAD_SPLIT)
         add_bias(0)
         add_bias(1)
         weave_agg(2, "scalar", HALF)
+        widen(3, "scalar", 0, 2)
         weave_agg_by_matmul(2, 0, HALF)
         relu(0)
-        weave_x(2, "vector")
+        move_columns(w2, w2_raw)
         quantize_hidden(0)
-        widen(3, "scalar")
+        quantize_cat(2, 0)
+        widen(3, "scalar", 2, 4)
         weave_agg_by_matmul(3, 0, HALF)
-        weave_agg_by_matmul(3, HALF, 2 * HALF)
+        weave_x(3, "scalar", 0, HEAD_SPLIT)
         second_layer(0)
         relu(1)
-        quantize_cat(2, 0)
-        quantize_hidden(1)
         quantize_cat(2, 1)
+        weave_agg(3, "vector", HALF)
+        quantize_hidden(1)
         first_layer(2)
-        weave_x(3, "vector")
+        weave_x(3, "vector", HALF)
+        weave_x(3, "vector", HEAD_SPLIT, HALF)
         widen(4, "scalar")
         second_layer(1)
         quantize_cat(3, 0, HALF)
@@ -389,42 +394,44 @@ def tile_graphaugmentation_pb_t_w8_kernel(
         quantize_cat(3, 0, 0, HALF)
         weave_agg(4, "gpsimd")
         add_bias(2)
-        agg_to_bank(0, 0, 2 * HALF)
-        agg_to_bank(1, 0, 4 * HALF)
+        agg_to_bank(0, 0, 2)
+        agg_to_bank(1, 0, 4)
         pair_x(4, 0, HALF)
         weave_x(4, "scalar", HALF)
         join_x_bank(4, 0, HALF)
         product(0, 2, 4, "gpsimd")
-        product_from_bank(0, 0, 2 * HALF)
+        product_from_bank(0, 0, 2)
         store(0, 0, 4)
-        product_from_bank(1, 0, 4 * HALF)
+        product_from_bank(1, 0, 4)
         store(1, 0, 4)
         first_layer(3, first_last=True)
         widen(5, "scalar")
         for s in range(3, ROWS_FROM):
             h = s - 1
-            w = WIDTHS[h]
             half = WIDTHS[s + 2] // 2
-            last_row = HALF if s + 3 == LAST else LAST_ROW
+            mine = VECTOR_PIXELS_LATE if s + 3 == LAST else VECTOR_PIXELS
+            paired = AGG_PAIRED if s + 3 < LAST else 0
             relu(h)
             quantize_cat(s + 1, 0, HALF)
             quantize_hidden(h)
             quantize_cat(s + 1, 1)
             quantize_cat(s + 1, 0, 0, HALF)
             second_layer(h)
-            weave_agg(s + 2, "gpsimd")
+            weave_agg(s + 2, "gpsimd", paired)
             if s + 3 == LAST:
                 weave_agg(LAST, "gpsimd")
             add_bias(s)
-            agg_to_bank(h, 0, 2 * w)
-            agg_to_bank(h, 2 * w, 3 * w + last_row)
+            agg_to_bank(h, 0, 2)
+            agg_to_bank(h, 2, 4, mine)
             pair_x(s + 2, 0, half)
             weave_x(s + 2, "scalar", half)
             join_x_bank(s + 2, 0, half)
-            product_from_bank(h, 0, 2 * w)
+            if paired:
+                weave_agg_by_matmul(s + 2, 0, paired)
+            product_from_bank(h, 0, 2)
             store(h, 0, 2)
-            product_from_bank(h, 2 * w, 3 * w + last_row)
-            product(h, 3, 4, "gpsimd", last_row)
+            product_from_bank(h, 2, 4, mine)
+            product(h, 2, 4, "gpsimd", mine)
             store(h, 2, ROWS)
             if s + 1 < ROWS_FROM:
                 first_layer(s + 1, first_last=True)
@@ -433,30 +440,27 @@ def tile_graphaugmentation_pb_t_w8_kernel(
             if s + 4 == LAST:
                 widen(LAST, "scalar")
         s = ROWS_FROM
-        w = WIDTHS[s]
         first_layer_rows(s)
         relu(s - 1)
         quantize_cat(s + 1, 0)
         quantize_hidden(s - 1)
         quantize_cat(s + 1, 1)
-        weave_x(LAST, "scalar", P)
+        weave_x(LAST, "scalar", P // 2)
         second_layer(s - 1)
-        weave_x(LAST, "vector", 0, P)
+        weave_x(LAST, "vector", 0, P // 2)
         quantize_cat(LAST, 1)
-        weave_hidden(s, "vector", 0, HALF)
+        weave_hidden(s, "vector")
         quantize_cat(LAST, 0)
-        weave_hidden(s, "vector", HALF)
-        agg_to_bank(s - 1, w, 3 * w)
+        agg_to_bank(s - 1, 0, 2)
+        agg_to_bank(s - 1, 2, 3)
         first_layer_rows(s + 1)
-        product(s - 1, 0, 1)
-        store(s - 1, 0, 1)
         quantize_hidden(s)
         second_layer(s, 0, 2)
         first_layer_rows(LAST)
         second_layer(s, 2, 4)
         product(s - 1, 3, 4, "gpsimd")
-        for t in (1, 2):
-            product_from_bank(s - 1, t * w, (t + 1) * w, w)
+        for t in range(3):
+            product_from_bank(s - 1, t, t + 1)
             store(s - 1, t, t + 1)
         store(s - 1, 3, 4)
         weave_hidden(s + 1, "vector")

@@ -35,7 +35,8 @@ ROWS_FROM = LAST - 2
 VECTOR_PIXELS = 256
 VECTOR_PIXELS_LATE = 384
 HEAD_SPLIT = 96
-AGG_PAIRED = 64
+X_PAIRED = 48
+AGG_PAIRED = 48
 
 
 def tile_graphaugmentation_pb_t_w8_kernel(
@@ -196,26 +197,38 @@ def tile_graphaugmentation_pb_t_w8_kernel(
         def weave_x(h, engine, c0=0, c1=None):
             weave(engine, woven_tile(x_woven, two, "x_woven", h), x_wide[h], c0, WIDTHS[h] if c1 is None else c1)
 
-        def pair_in_bank(rows, c0, c1):
-            bank = scalar_banks.tile([P, 2, c1 - c0, 2], BF16, name="bank")
-            for u in range(2):
+        def pair_rows(bank, rows, pairs=(0, 1)):
+            for u in pairs:
                 nc.tensor.matmul(
                     out=bank[:, u],
                     lhsT=ident[:],
-                    rhs=rows[:, 2 * u : 2 * u + 2, c0:c1].rearrange("p e n -> p n e"),
+                    rhs=rows[:, 2 * u : 2 * u + 2, :].rearrange("p e n -> p n e"),
                     start=True,
                     stop=True,
                 )
-            return bank
+
+        def pair_in_bank(rows, c0, c1):
+            bank = scalar_banks.tile([P, 2, c1 - c0, 2], BF16, name="bank")
+            pair_rows(bank[:], rows[:, :, c0:c1])
+            return bank[:]
 
         def join_bank(bank, dst, c0, c1):
             nc.scalar.copy(
                 out=dst[:, ROWS * c0 : ROWS * c1].bitcast(F32).rearrange("p (n u) -> p n u", u=2),
-                in_=bank[:].rearrange("p u n e -> p u (n e)").bitcast(F32).rearrange("p u n -> p n u"),
+                in_=bank.rearrange("p u n e -> p u (n e)").bitcast(F32).rearrange("p u n -> p n u"),
             )
 
-        def pair_x(h, c0, c1):
-            x_bank[h, c0] = pair_in_bank(x_wide[h], c0, c1)
+        def weave_shares_by_matmul(h):
+            bank = scalar_banks.tile([P, 2, X_PAIRED + AGG_PAIRED, 2], BF16, name="bank")
+            pair_rows(bank[:, :, :X_PAIRED], x_wide[h][:, :, HALF : HALF + X_PAIRED])
+            pair_rows(bank[:, :, X_PAIRED:], agg_rows[h][:, :, :AGG_PAIRED])
+            join_bank(bank[:, :, :X_PAIRED], x_woven[h], HALF, HALF + X_PAIRED)
+            join_bank(bank[:, :, X_PAIRED:], agg_tile(h), 0, AGG_PAIRED)
+
+        def pair_x(h, c0, c1, pairs=(0, 1)):
+            if 0 in pairs:
+                x_bank[h, c0] = scalar_banks.tile([P, 2, c1 - c0, 2], BF16, name="bank")[:]
+            pair_rows(x_bank[h, c0], x_wide[h][:, :, c0:c1], pairs)
 
         def join_x_bank(h, c0, c1):
             join_bank(x_bank[h, c0], woven_tile(x_woven, two, "x_woven", h), c0, c1)
@@ -253,12 +266,10 @@ def tile_graphaugmentation_pb_t_w8_kernel(
                 stop=(g == 1),
             )
 
-        def first_layer(h, first_last=False):
-            count = WIDTHS[h] // P
-            for j in range(count):
-                sums[h, j] = vector_banks.tile([P, 2, HALF], F32, name="bank")
-            for j in list(range(1, count)) + [0] if first_last else range(count):
+        def first_layer(h, j0=0, j1=None):
+            for j in range(j0, WIDTHS[h] // P if j1 is None else j1):
                 c, u = divmod(j, 2)
+                sums[h, j] = vector_banks.tile([P, 2, HALF], F32, name="bank")
                 for e in range(2):
                     for g in range(2):
                         first_pass(sums[h, j][:, e, :], h, g, 2 * u + e, slice(HALF * c, HALF * (c + 1)))
@@ -309,10 +320,10 @@ def tile_graphaugmentation_pb_t_w8_kernel(
                 out=hidden_codes[h][:].bitcast(FP8X4), scales=hidden_scales[h][:], in_=hidden_woven[h][:]
             )
 
-        def second_layer(h, t0=0, t1=ROWS):
+        def second_layer(h, t0=0, t1=ROWS, order=None):
             if t0 == 0:
                 gate[h] = four.tile([P, ROWS, WIDTHS[h]], F32, name="gate")
-            for t in range(t0, t1):
+            for t in order or range(t0, t1):
                 m = slice(P * t, P * t + P)
                 acc = scalar_banks.tile([P, WIDTHS[h]], F32, name="bank")
                 nc.tensor.matmul_mx(
@@ -378,7 +389,6 @@ def tile_graphaugmentation_pb_t_w8_kernel(
         quantize_cat(2, 0)
         widen(3, "scalar", 2, 4)
         weave_agg_by_matmul(3, 0, HALF)
-        weave_x(3, "scalar", 0, HEAD_SPLIT)
         second_layer(0)
         relu(1)
         quantize_cat(2, 1)
@@ -386,7 +396,7 @@ def tile_graphaugmentation_pb_t_w8_kernel(
         quantize_hidden(1)
         first_layer(2)
         weave_x(3, "vector", HALF)
-        weave_x(3, "vector", HEAD_SPLIT, HALF)
+        weave_x(3, "vector", 0, HALF)
         widen(4, "scalar")
         second_layer(1)
         quantize_cat(3, 0, HALF)
@@ -404,7 +414,7 @@ def tile_graphaugmentation_pb_t_w8_kernel(
         store(0, 0, 4)
         product_from_bank(1, 0, 4)
         store(1, 0, 4)
-        first_layer(3, first_last=True)
+        first_layer(3, 0, 3)
         widen(5, "scalar")
         for s in range(3, ROWS_FROM):
             h = s - 1
@@ -416,25 +426,27 @@ def tile_graphaugmentation_pb_t_w8_kernel(
             quantize_hidden(h)
             quantize_cat(s + 1, 1)
             quantize_cat(s + 1, 0, 0, HALF)
-            second_layer(h)
+            second_layer(h, order=(2, 3, 0, 1))
+            first_layer(s, 3, 4)
             weave_agg(s + 2, "gpsimd", paired)
             if s + 3 == LAST:
                 weave_agg(LAST, "gpsimd")
             add_bias(s)
-            agg_to_bank(h, 0, 2)
             agg_to_bank(h, 2, 4, mine)
-            pair_x(s + 2, 0, half)
-            weave_x(s + 2, "scalar", half)
+            pair_x(s + 2, 0, half, (0,))
+            agg_to_bank(h, 0, 2)
+            pair_x(s + 2, 0, half, (1,))
+            weave_x(s + 2, "scalar", half + (X_PAIRED if paired else 0))
             join_x_bank(s + 2, 0, half)
             if paired:
-                weave_agg_by_matmul(s + 2, 0, paired)
-            product_from_bank(h, 0, 2)
-            store(h, 0, 2)
+                weave_shares_by_matmul(s + 2)
             product_from_bank(h, 2, 4, mine)
             product(h, 2, 4, "gpsimd", mine)
+            product_from_bank(h, 0, 2)
+            store(h, 0, 2)
             store(h, 2, ROWS)
             if s + 1 < ROWS_FROM:
-                first_layer(s + 1, first_last=True)
+                first_layer(s + 1, 0, 3)
             if s + 3 < LAST:
                 widen(s + 3, "scalar")
             if s + 4 == LAST:
@@ -445,9 +457,9 @@ def tile_graphaugmentation_pb_t_w8_kernel(
         quantize_cat(s + 1, 0)
         quantize_hidden(s - 1)
         quantize_cat(s + 1, 1)
-        weave_x(LAST, "scalar", P // 2)
+        weave_x(LAST, "scalar", P)
         second_layer(s - 1)
-        weave_x(LAST, "vector", 0, P // 2)
+        weave_x(LAST, "vector", 0, P)
         quantize_cat(LAST, 1)
         weave_hidden(s, "vector")
         quantize_cat(LAST, 0)

@@ -32,11 +32,11 @@ AGG_LOADS = [256, 256] + [512] * 3 + [PIX] * (IMAGES - 2)
 
 BY_GPSIMD = list(range(3, LAST))
 ROWS_FROM = LAST - 2
-VECTOR_PIXELS = 256
+VECTOR_PIXELS = 224
 VECTOR_PIXELS_LATE = 384
 HEAD_SPLIT = 96
-X_PAIRED = 48
-AGG_PAIRED = 48
+X_PAIRED = 32
+AGG_PAIRED = 80
 
 
 def tile_graphaugmentation_pb_t_w8_kernel(
@@ -389,6 +389,7 @@ def tile_graphaugmentation_pb_t_w8_kernel(
         quantize_cat(2, 0)
         widen(3, "scalar", 2, 4)
         weave_agg_by_matmul(3, 0, HALF)
+        weave_x(3, "scalar", 0, HEAD_SPLIT)
         second_layer(0)
         relu(1)
         quantize_cat(2, 1)
@@ -396,7 +397,7 @@ def tile_graphaugmentation_pb_t_w8_kernel(
         quantize_hidden(1)
         first_layer(2)
         weave_x(3, "vector", HALF)
-        weave_x(3, "vector", 0, HALF)
+        weave_x(3, "vector", HEAD_SPLIT, HALF)
         widen(4, "scalar")
         second_layer(1)
         quantize_cat(3, 0, HALF)
@@ -457,9 +458,9 @@ def tile_graphaugmentation_pb_t_w8_kernel(
         quantize_cat(s + 1, 0)
         quantize_hidden(s - 1)
         quantize_cat(s + 1, 1)
-        weave_x(LAST, "scalar", P)
+        weave_x(LAST, "scalar", P // 2)
         second_layer(s - 1)
-        weave_x(LAST, "vector", 0, P)
+        weave_x(LAST, "vector", 0, P // 2)
         quantize_cat(LAST, 1)
         weave_hidden(s, "vector")
         quantize_cat(LAST, 0)

@@ -16,6 +16,7 @@ ALU = mybir.AluOpType
 IMAGES, C, PIX = 6, 512, 1024
 P = 128
 ROWS = 4
+BANK = 512
 HALF = 256
 SPREAD = 16
 NEIGHBOURS = 4
@@ -32,11 +33,11 @@ AGG_LOADS = [256, 256] + [512] * 3 + [PIX] * (IMAGES - 2)
 
 BY_GPSIMD = list(range(3, LAST))
 ROWS_FROM = LAST - 2
-VECTOR_PIXELS = 224
+VECTOR_PIXELS = 256
 VECTOR_PIXELS_LATE = 384
 HEAD_SPLIT = 96
 X_PAIRED = 32
-AGG_PAIRED = 80
+AGG_PAIRED = 48
 
 
 def tile_graphaugmentation_pb_t_w8_kernel(
@@ -303,11 +304,17 @@ def tile_graphaugmentation_pb_t_w8_kernel(
         def first_layer_rows(h, t0=0, t1=ROWS):
             if t0 == 0:
                 hidden[h] = two.tile([P, ROWS, WIDTHS[h]], BF16, name="hidden")
-            for t in range(t0, t1):
-                acc = scalar_banks.tile([P, WIDTHS[h]], F32, name="bank")
-                for g in range(2):
-                    first_pass(acc[:], h, g, t, slice(0, WIDTHS[h]))
-                nc.scalar.activation(out=hidden[h][:, t, :], in_=acc[:], func=ACT.Relu, bias=b1[:, t : t + 1])
+            rows = BANK // WIDTHS[h]
+            for first in range(t0, t1, rows):
+                acc = scalar_banks.tile([P, rows, WIDTHS[h]], F32, name="bank")
+                for r in range(rows):
+                    for g in range(2):
+                        first_pass(acc[:, r, :], h, g, first + r, slice(0, WIDTHS[h]))
+                for r in range(rows):
+                    t = first + r
+                    nc.scalar.activation(
+                        out=hidden[h][:, t, :], in_=acc[:, r, :], func=ACT.Relu, bias=b1[:, t : t + 1]
+                    )
 
         def weave_hidden(h, engine, c0=0, c1=None):
             dst = woven_tile(hidden_woven, two, "hidden_woven", h)
@@ -323,19 +330,25 @@ def tile_graphaugmentation_pb_t_w8_kernel(
         def second_layer(h, t0=0, t1=ROWS, order=None):
             if t0 == 0:
                 gate[h] = four.tile([P, ROWS, WIDTHS[h]], F32, name="gate")
-            for t in order or range(t0, t1):
-                m = slice(P * t, P * t + P)
-                acc = scalar_banks.tile([P, WIDTHS[h]], F32, name="bank")
-                nc.tensor.matmul_mx(
-                    out=acc[:],
-                    lhsT=w2[:, m].bitcast(FP8X4),
-                    lhsT_scale=s2[:, m],
-                    rhs=hidden_codes[h][:].bitcast(FP8X4),
-                    rhs_scale=hidden_scales[h][:],
-                    start=True,
-                    stop=True,
-                )
-                nc.scalar.activation(out=gate[h][:, t, :], in_=acc[:], func=ACT.Sigmoid, bias=b2[:, t : t + 1])
+            order = list(order or range(t0, t1))
+            rows = BANK // WIDTHS[h]
+            for first in range(0, len(order), rows):
+                acc = scalar_banks.tile([P, rows, WIDTHS[h]], F32, name="bank")
+                for r, t in enumerate(order[first : first + rows]):
+                    m = slice(P * t, P * t + P)
+                    nc.tensor.matmul_mx(
+                        out=acc[:, r, :],
+                        lhsT=w2[:, m].bitcast(FP8X4),
+                        lhsT_scale=s2[:, m],
+                        rhs=hidden_codes[h][:].bitcast(FP8X4),
+                        rhs_scale=hidden_scales[h][:],
+                        start=True,
+                        stop=True,
+                    )
+                for r, t in enumerate(order[first : first + rows]):
+                    nc.scalar.activation(
+                        out=gate[h][:, t, :], in_=acc[:, r, :], func=ACT.Sigmoid, bias=b2[:, t : t + 1]
+                    )
 
         def agg_to_bank(h, t0, t1, c1=None):
             c1 = WIDTHS[h] if c1 is None else c1
@@ -415,7 +428,7 @@ def tile_graphaugmentation_pb_t_w8_kernel(
         store(0, 0, 4)
         product_from_bank(1, 0, 4)
         store(1, 0, 4)
-        first_layer(3, 0, 3)
+        first_layer(3)
         widen(5, "scalar")
         for s in range(3, ROWS_FROM):
             h = s - 1
@@ -428,7 +441,6 @@ def tile_graphaugmentation_pb_t_w8_kernel(
             quantize_cat(s + 1, 1)
             quantize_cat(s + 1, 0, 0, HALF)
             second_layer(h, order=(2, 3, 0, 1))
-            first_layer(s, 3, 4)
             weave_agg(s + 2, "gpsimd", paired)
             if s + 3 == LAST:
                 weave_agg(LAST, "gpsimd")
@@ -447,7 +459,7 @@ def tile_graphaugmentation_pb_t_w8_kernel(
             store(h, 0, 2)
             store(h, 2, ROWS)
             if s + 1 < ROWS_FROM:
-                first_layer(s + 1, 0, 3)
+                first_layer(s + 1)
             if s + 3 < LAST:
                 widen(s + 3, "scalar")
             if s + 4 == LAST:

@@ -37,7 +37,7 @@ VECTOR_PIXELS = 256
 VECTOR_PIXELS_LATE = 384
 HEAD_SPLIT = 96
 X_PAIRED = 32
-AGG_PAIRED = 48
+AGG_PAIRED = 64
 
 
 def tile_graphaugmentation_pb_t_w8_kernel(
@@ -221,8 +221,14 @@ def tile_graphaugmentation_pb_t_w8_kernel(
 
         def weave_shares_by_matmul(h):
             bank = scalar_banks.tile([P, 2, X_PAIRED + AGG_PAIRED, 2], BF16, name="bank")
-            pair_rows(bank[:, :, :X_PAIRED], x_wide[h][:, :, HALF : HALF + X_PAIRED])
-            pair_rows(bank[:, :, X_PAIRED:], agg_rows[h][:, :, :AGG_PAIRED])
+            shares = (
+                (bank[:, :, :X_PAIRED], x_wide[h][:, :, HALF : HALF + X_PAIRED]),
+                (bank[:, :, X_PAIRED:], agg_rows[h][:, :, :AGG_PAIRED]),
+            )
+            for dst, rows in shares:
+                nc.tensor.matmul(
+                    out=dst, lhsT=ident[:], rhs=rows.rearrange("p (u e) n -> p u n e", e=2), start=True, stop=True
+                )
             join_bank(bank[:, :, :X_PAIRED], x_woven[h], HALF, HALF + X_PAIRED)
             join_bank(bank[:, :, X_PAIRED:], agg_tile(h), 0, AGG_PAIRED)
 
@@ -355,7 +361,16 @@ def tile_graphaugmentation_pb_t_w8_kernel(
             bank = vector_banks.tile([P, t1 - t0, c1], BF16, name="bank")
             for t in range(t0, t1):
                 agg_bank[h, t] = bank[:, t - t0 :, :]
-                nc.tensor.matmul(out=bank[:, t - t0, :], lhsT=ident[:], rhs=agg_rows[h][:, t, :c1], start=True, stop=True)
+            rows = BANK // c1
+            for t in range(t0, t1, rows):
+                end = min(t + rows, t1)
+                nc.tensor.matmul(
+                    out=bank[:, t - t0 : end - t0, :],
+                    lhsT=ident[:],
+                    rhs=agg_rows[h][:, t:end, :c1],
+                    start=True,
+                    stop=True,
+                )
 
         def product_from_bank(h, t0, t1, c1=None):
             part = gate[h][:, t0:t1, :c1]
@@ -401,8 +416,8 @@ def tile_graphaugmentation_pb_t_w8_kernel(
         quantize_hidden(0)
         quantize_cat(2, 0)
         widen(3, "scalar", 2, 4)
-        weave_agg_by_matmul(3, 0, HALF)
         weave_x(3, "scalar", 0, HEAD_SPLIT)
+        weave_agg_by_matmul(3, 0, HALF)
         second_layer(0)
         relu(1)
         quantize_cat(2, 1)

@@ -174,8 +174,8 @@ def tile_graphaugmentation_pb_t_w8_kernel(
         def weave(engine, dst, rows, c0, c1):
             if engine == "gpsimd":
                 nc.gpsimd.tensor_scalar(
-                    out=dst[:, ROWS * c0 : ROWS * c1].rearrange("p (n t) -> p n t", t=ROWS),
-                    in0=rows[:, :, c0:c1].rearrange("p t n -> p n t"),
+                    out=dst[:, ROWS * c0 : ROWS * c1].rearrange("p (c i t) -> p c t i", i=NEIGHBOURS, t=ROWS),
+                    in0=rows[:, :, c0:c1].rearrange("p t (c i) -> p c t i", i=NEIGHBOURS),
                     scalar1=1.0,
                     scalar2=0.0,
                     op0=ALU.mult,

@@ -18,24 +18,20 @@ P = 128
 ROWS = 4
 BANK = 512
 HALF = 256
+FULL = 2 * HALF
 SPREAD = 16
 NEIGHBOURS = 4
 
 FLOPS = 2 * IMAGES * PIX * C * (2 * C + C)
 
-WIDTHS = [256, 256] + [512] * 10 + [256, 256]
+WIDTHS = [HALF, HALF] + [FULL] * 11
 COUNT = len(WIDTHS)
 LAST = COUNT - 1
 STARTS = [sum(WIDTHS[:h]) for h in range(COUNT)]
-
-X_LOADS = [512] * 4 + [PIX] * (IMAGES - 2)
-AGG_LOADS = [256, 256] + [512] * 3 + [PIX] * (IMAGES - 2)
-
-BY_GPSIMD = list(range(3, LAST))
-ROWS_FROM = LAST - 2
+X_LOADS = [PIX] * IMAGES
+AGG_LOADS = [512, 512] + [PIX] * (IMAGES - 1)
+HEAD_SPLIT = 128
 VECTOR_PIXELS = 256
-VECTOR_PIXELS_LATE = 384
-HEAD_SPLIT = 96
 X_PAIRED = 32
 AGG_PAIRED = 64
 
@@ -50,7 +46,6 @@ def tile_graphaugmentation_pb_t_w8_kernel(
 
     with ExitStack() as ctx:
         keep = ctx.enter_context(tc.tile_pool(name="keep", bufs=1))
-        one = ctx.enter_context(tc.tile_pool(name="one", bufs=1))
         two = ctx.enter_context(tc.tile_pool(name="two", bufs=2))
         three = ctx.enter_context(tc.tile_pool(name="three", bufs=3))
         four = ctx.enter_context(tc.tile_pool(name="four", bufs=4))
@@ -83,12 +78,12 @@ def tile_graphaugmentation_pb_t_w8_kernel(
         x_rows = [chunk_of(x_loaded, X_LOADS, h) for h in range(COUNT)]
         agg_rows = [chunk_of(agg_loaded, AGG_LOADS, h) for h in range(COUNT)]
 
-        def load(loaded, hbm, sizes, j):
+        def load(loaded, hbm, sizes, j, t0=0, t1=ROWS):
             b, c0 = divmod(sum(sizes[:j]), PIX)
-            nc.sync.dma_start(out=loaded[j][:], in_=hbm[b][:, :, c0 : c0 + sizes[j]])
+            nc.sync.dma_start(out=loaded[j][:, t0:t1, :], in_=hbm[b][:, t0:t1, c0 : c0 + sizes[j]])
 
-        def load_x(j):
-            load(x_loaded, x_hbm, X_LOADS, j)
+        def load_x(j, t0=0, t1=ROWS):
+            load(x_loaded, x_hbm, X_LOADS, j, t0, t1)
 
         def load_agg(j):
             load(agg_loaded, agg_hbm, AGG_LOADS, j)
@@ -96,29 +91,34 @@ def tile_graphaugmentation_pb_t_w8_kernel(
         def load_words(dst, words):
             nc.sync.dma_start(out=dst[:], in_=words.rearrange("p n t -> p (n t)").bitcast(I32))
 
+        def load_scales(dst, scales):
+            rows = 4 * scales.shape[0]
+            for q in range(4):
+                nc.sync.dma_start(
+                    out=dst[32 * q : 32 * q + rows, :].bitcast(I32), in_=scales[:, 4 * q : 4 * q + 4, :].bitcast(I32)
+                )
+
         nc.scalar.dma_start(out=xs[:], in_=x_scale.rearrange("o (p t) h w -> p (o t h w)", t=ROWS))
         nc.scalar.dma_start(out=b1[:], in_=g1b.rearrange("(p t) -> p t", t=ROWS))
         warm = keep.tile([P, 1], F32, name="warm")
         nc.vector.memset(warm[:], 0.0)
         nc.scalar.activation(out=warm[:], in_=warm[:], func=ACT.Sigmoid)
 
-        load_x(0)
+        def load_b2():
+            nc.sync.dma_start(out=b2[:], in_=g2b.rearrange("(p t) -> p t", t=ROWS))
+
+        load_x(0, 0, 2)
+        load_x(0, 2, 4)
         load_agg(0)
-        load_agg(1)
-        for q in range(4):
-            nc.sync.dma_start(
-                out=s1_raw[32 * q : 32 * q + 8, :].bitcast(I32), in_=g1w_scales[:, 4 * q : 4 * q + 4, :].bitcast(I32)
-            )
         load_words(w1_raw[0], g1w_words[0])
         load_words(w1_raw[1], g1w_words[1])
+        load_scales(s1_raw, g1w_scales)
         load_x(1)
-        for q in range(4):
-            nc.sync.dma_start(
-                out=s2_raw[32 * q : 32 * q + 4, :].bitcast(I32), in_=g2w_scales[0, 4 * q : 4 * q + 4, :].bitcast(I32)
-            )
+        load_agg(1)
         load_words(w2_raw, g2w_words[0])
+        load_scales(s2_raw, g2w_scales)
         load_agg(2)
-        nc.sync.dma_start(out=b2[:], in_=g2b.rearrange("(p t) -> p t", t=ROWS))
+        load_b2()
         for j in range(2, len(X_LOADS)):
             load_x(j)
             load_agg(j + 1)
@@ -141,123 +141,103 @@ def tile_graphaugmentation_pb_t_w8_kernel(
                 )
 
         x_wide, x_woven, agg_woven, cat_codes, cat_scales, sums, biased, hidden = ({} for stage in range(8))
-        hidden_woven, hidden_codes, hidden_scales, gate, x_bank, agg_bank = ({} for stage in range(6))
+        hidden_woven, hidden_codes, hidden_scales, gate, pair_bank, agg_bank, aside = ({} for stage in range(7))
+
+        def span(h, c0, c1):
+            return c0, WIDTHS[h] if c1 is None else c1
+
+        def tile_of(store, h, pool, shape, dtype, name):
+            if h not in store:
+                store[h] = pool.tile(shape, dtype, name=name, align_bytes=64)
+            return store[h]
 
         def widen(h, engine, t0=0, t1=ROWS):
-            if t0 == 0:
-                x_wide[h] = four.tile([P, ROWS, WIDTHS[h]], BF16, name="x_wide")
+            dst = tile_of(x_wide, h, four, [P, ROWS, WIDTHS[h]], BF16, "x_wide")
             for t in range(t0, t1):
                 codes = x_rows[h][:, t, :].bitcast(FP8)
                 if engine == "scalar":
-                    nc.scalar.activation(out=x_wide[h][:, t, :], in_=codes, func=ACT.Copy, scale=xs[:, t : t + 1])
+                    nc.scalar.activation(out=dst[:, t, :], in_=codes, func=ACT.Copy, scale=xs[:, t : t + 1])
                 else:
                     nc.vector.tensor_scalar(
-                        out=x_wide[h][:, t, :], in0=codes, scalar1=xs[:, t : t + 1], scalar2=None, op0=ALU.mult
+                        out=dst[:, t, :], in0=codes, scalar1=xs[:, t : t + 1], scalar2=None, op0=ALU.mult
                     )
 
         def widen_pairs(h):
-            x_wide[h] = four.tile([P, 2, 2 * WIDTHS[h]], BF16, name="x_wide")
+            dst = tile_of(x_wide, h, four, [P, 2, 2 * WIDTHS[h]], BF16, "x_wide")
             for t in range(ROWS):
                 nc.vector.tensor_scalar(
-                    out=x_wide[h][:, t // 2, t % 2 :: 2],
+                    out=dst[:, t // 2, t % 2 :: 2],
                     in0=x_rows[h][:, t, :].bitcast(FP8),
                     scalar1=xs[:, t : t + 1],
                     scalar2=None,
                     op0=ALU.mult,
                 )
 
-        def woven_tile(store, pool, name, h):
-            if h not in store:
-                store[h] = pool.tile([P, ROWS * WIDTHS[h]], BF16, name=name, align_bytes=64)
-            return store[h]
+        def x_tile(h):
+            return tile_of(x_woven, h, two, [P, ROWS * WIDTHS[h]], BF16, "x_woven")
+
+        def agg_tile(h):
+            return tile_of(agg_woven, h, three, [P, ROWS * FULL], BF16, "agg_woven")
+
+        def hidden_tile(h):
+            return tile_of(hidden_woven, h, two, [P, ROWS * WIDTHS[h]], BF16, "hidden_woven")
+
+        def share_tile(h):
+            shared = three.tile([P, 3 * ROWS * HALF], BF16, name="shared", align_bytes=64)
+            hidden_woven[h] = shared[:, ROWS * HALF :]
+            agg_woven[h + 3] = shared[:, : ROWS * FULL]
 
         def weave(engine, dst, rows, c0, c1):
+            woven = dst[:, ROWS * c0 : ROWS * c1].rearrange("p (c i t) -> p c t i", i=NEIGHBOURS, t=ROWS)
+            rows = rows[:, :, c0:c1].rearrange("p t (c i) -> p c t i", i=NEIGHBOURS)
             if engine == "gpsimd":
-                nc.gpsimd.tensor_scalar(
-                    out=dst[:, ROWS * c0 : ROWS * c1].rearrange("p (c i t) -> p c t i", i=NEIGHBOURS, t=ROWS),
-                    in0=rows[:, :, c0:c1].rearrange("p t (c i) -> p c t i", i=NEIGHBOURS),
-                    scalar1=1.0,
-                    scalar2=0.0,
-                    op0=ALU.mult,
-                    op1=ALU.add,
-                )
+                nc.gpsimd.tensor_scalar(out=woven, in0=rows, scalar1=1.0, scalar2=0.0, op0=ALU.mult, op1=ALU.add)
             else:
                 copy = nc.vector.tensor_copy if engine == "vector" else nc.scalar.copy
-                copy(
-                    out=dst[:, ROWS * c0 : ROWS * c1].rearrange("p (c i t) -> p c t i", i=NEIGHBOURS, t=ROWS),
-                    in_=rows[:, :, c0:c1].rearrange("p t (c i) -> p c t i", i=NEIGHBOURS),
-                )
+                copy(out=woven, in_=rows)
 
-        def join_x(h, copy):
-            dst = woven_tile(x_woven, two, "x_woven", h)
-            copy(
-                out=dst[:].bitcast(F32).rearrange("p (n u) -> p n u", u=2),
+        def weave_x(h, engine, c0=0, c1=None):
+            weave(engine, x_tile(h), x_wide[h], *span(h, c0, c1))
+
+        def weave_agg(h, engine, c0=0, c1=None):
+            weave(engine, agg_tile(h), agg_rows[h], *span(h, c0, c1))
+
+        def weave_hidden(h, engine, c0=0, c1=None):
+            weave(engine, hidden_tile(h), hidden[h], *span(h, c0, c1))
+
+        def join_x(h):
+            nc.vector.tensor_copy(
+                out=x_tile(h)[:].bitcast(F32).rearrange("p (n u) -> p n u", u=2),
                 in_=x_wide[h][:].bitcast(F32).rearrange("p u n -> p n u"),
             )
 
-        def weave_x(h, engine, c0=0, c1=None):
-            weave(engine, woven_tile(x_woven, two, "x_woven", h), x_wide[h], c0, WIDTHS[h] if c1 is None else c1)
-
-        def pair_rows(bank, rows, pairs=(0, 1)):
+        def pair(name, h, c0, c1, pairs=(0, 1)):
+            rows = {"x": x_wide, "agg": agg_rows, "hidden": hidden}[name][h]
+            if 0 in pairs:
+                pair_bank[name, h, c0] = scalar_banks.tile([P, 2, c1 - c0, 2], BF16, name="bank")[:]
             for u in pairs:
                 nc.tensor.matmul(
-                    out=bank[:, u],
+                    out=pair_bank[name, h, c0][:, u],
                     lhsT=ident[:],
-                    rhs=rows[:, 2 * u : 2 * u + 2, :].rearrange("p e n -> p n e"),
+                    rhs=rows[:, 2 * u : 2 * u + 2, c0:c1].rearrange("p e n -> p n e"),
                     start=True,
                     stop=True,
                 )
 
-        def pair_in_bank(rows, c0, c1):
-            bank = scalar_banks.tile([P, 2, c1 - c0, 2], BF16, name="bank")
-            pair_rows(bank[:], rows[:, :, c0:c1])
-            return bank[:]
-
-        def join_bank(bank, dst, c0, c1):
+        def join(name, h, c0, c1):
+            dst = {"x": x_tile, "agg": agg_tile, "hidden": hidden_tile}[name](h)
             nc.scalar.copy(
                 out=dst[:, ROWS * c0 : ROWS * c1].bitcast(F32).rearrange("p (n u) -> p n u", u=2),
-                in_=bank.rearrange("p u n e -> p u (n e)").bitcast(F32).rearrange("p u n -> p n u"),
+                in_=pair_bank[name, h, c0].rearrange("p u n e -> p u (n e)").bitcast(F32).rearrange("p u n -> p n u"),
             )
-
-        def weave_shares_by_matmul(h):
-            bank = scalar_banks.tile([P, 2, X_PAIRED + AGG_PAIRED, 2], BF16, name="bank")
-            shares = (
-                (bank[:, :, :X_PAIRED], x_wide[h][:, :, HALF : HALF + X_PAIRED]),
-                (bank[:, :, X_PAIRED:], agg_rows[h][:, :, :AGG_PAIRED]),
-            )
-            for dst, rows in shares:
-                nc.tensor.matmul(
-                    out=dst, lhsT=ident[:], rhs=rows.rearrange("p (u e) n -> p u n e", e=2), start=True, stop=True
-                )
-            join_bank(bank[:, :, :X_PAIRED], x_woven[h], HALF, HALF + X_PAIRED)
-            join_bank(bank[:, :, X_PAIRED:], agg_tile(h), 0, AGG_PAIRED)
-
-        def pair_x(h, c0, c1, pairs=(0, 1)):
-            if 0 in pairs:
-                x_bank[h, c0] = scalar_banks.tile([P, 2, c1 - c0, 2], BF16, name="bank")[:]
-            pair_rows(x_bank[h, c0], x_wide[h][:, :, c0:c1], pairs)
-
-        def join_x_bank(h, c0, c1):
-            join_bank(x_bank[h, c0], woven_tile(x_woven, two, "x_woven", h), c0, c1)
-
-        def agg_tile(h):
-            pool, name = (one, "agg_woven") if h in BY_GPSIMD else (two, "agg_woven_first")
-            return woven_tile(agg_woven, pool, name, h)
-
-        def weave_agg_by_matmul(h, c0, c1):
-            join_bank(pair_in_bank(agg_rows[h], c0, c1), agg_tile(h), c0, c1)
-
-        def weave_agg(h, engine, c0=0, c1=None):
-            weave(engine, agg_tile(h), agg_rows[h], c0, WIDTHS[h] if c1 is None else c1)
 
         def quantize_cat(h, g, c0=0, c1=None):
-            c1 = WIDTHS[h] if c1 is None else c1
-            if h not in cat_codes:
-                cat_codes[h] = two.tile([P, 2, WIDTHS[h]], U32, name="cat_codes", align_bytes=64)
-                cat_scales[h] = two.tile([P, 2, WIDTHS[h]], U8, name="cat_scales", align_bytes=64)
+            c0, c1 = span(h, c0, c1)
+            codes = tile_of(cat_codes, h, three, [P, 2, WIDTHS[h]], U32, "cat_codes")
+            scales = tile_of(cat_scales, h, three, [P, 2, WIDTHS[h]], U8, "cat_scales")
             nc.vector.quantize_mx(
-                out=cat_codes[h][:, g, c0:c1].bitcast(FP8X4),
-                scales=cat_scales[h][:, g, c0:c1],
+                out=codes[:, g, c0:c1].bitcast(FP8X4),
+                scales=scales[:, g, c0:c1],
                 in_=(x_woven, agg_woven)[g][h][:, ROWS * c0 : ROWS * c1],
             )
 
@@ -282,11 +262,10 @@ def tile_graphaugmentation_pb_t_w8_kernel(
                         first_pass(sums[h, j][:, e, :], h, g, 2 * u + e, slice(HALF * c, HALF * (c + 1)))
 
         def add_bias(h, j0=0, j1=None):
-            if j0 == 0:
-                biased[h] = two.tile([P, 2, 2 * WIDTHS[h]], BF16, name="biased")
+            dst = tile_of(biased, h, two, [P, 2, 2 * WIDTHS[h]], BF16, "biased")
             for j in range(j0, WIDTHS[h] // P if j1 is None else j1):
                 c, u = divmod(j, 2)
-                pixels = biased[h][:, u, 2 * HALF * c : 2 * HALF * (c + 1)]
+                pixels = dst[:, u, 2 * HALF * c : 2 * HALF * (c + 1)]
                 nc.vector.tensor_tensor(
                     out=pixels.rearrange("p (r n i e) -> p r n e i", n=SPREAD, i=2, e=2),
                     in0=b1_pairs[:, u, :]
@@ -297,232 +276,270 @@ def tile_graphaugmentation_pb_t_w8_kernel(
                     op=ALU.add,
                 )
 
-        def relu(h):
-            dst = woven_tile(hidden_woven, two, "hidden_woven", h)
+        def relu(h, c0=0, c1=None):
+            c0, c1 = span(h, c0, c1)
             nc.vector.tensor_scalar(
-                out=dst[:].rearrange("p (n u e) -> p n u e", u=2, e=2),
-                in0=biased[h][:].rearrange("p u (n e) -> p n u e", e=2),
+                out=hidden_tile(h)[:, ROWS * c0 : ROWS * c1].rearrange("p (n u e) -> p n u e", u=2, e=2),
+                in0=biased[h][:, :, 2 * c0 : 2 * c1].rearrange("p u (n e) -> p n u e", e=2),
                 scalar1=0.0,
                 scalar2=None,
                 op0=ALU.max,
             )
 
-        def first_layer_rows(h, t0=0, t1=ROWS):
-            if t0 == 0:
-                hidden[h] = two.tile([P, ROWS, WIDTHS[h]], BF16, name="hidden")
-            rows = BANK // WIDTHS[h]
+        def first_layer_rows(h, c0=0, c1=None, t0=0, t1=ROWS):
+            c0, c1 = span(h, c0, c1)
+            dst = tile_of(hidden, h, two, [P, ROWS, WIDTHS[h]], BF16, "hidden")
+            rows = BANK // (c1 - c0)
             for first in range(t0, t1, rows):
-                acc = scalar_banks.tile([P, rows, WIDTHS[h]], F32, name="bank")
+                acc = scalar_banks.tile([P, rows, c1 - c0], F32, name="bank")
                 for r in range(rows):
                     for g in range(2):
-                        first_pass(acc[:, r, :], h, g, first + r, slice(0, WIDTHS[h]))
+                        first_pass(acc[:, r, :], h, g, first + r, slice(c0, c1))
                 for r in range(rows):
                     t = first + r
-                    nc.scalar.activation(
-                        out=hidden[h][:, t, :], in_=acc[:, r, :], func=ACT.Relu, bias=b1[:, t : t + 1]
-                    )
+                    nc.scalar.activation(out=dst[:, t, c0:c1], in_=acc[:, r, :], func=ACT.Relu, bias=b1[:, t : t + 1])
 
-        def weave_hidden(h, engine, c0=0, c1=None):
-            dst = woven_tile(hidden_woven, two, "hidden_woven", h)
-            weave(engine, dst, hidden[h], c0, WIDTHS[h] if c1 is None else c1)
-
-        def quantize_hidden(h):
-            hidden_codes[h] = two.tile([P, WIDTHS[h]], U32, name="hidden_codes", align_bytes=64)
-            hidden_scales[h] = two.tile([P, WIDTHS[h]], U8, name="hidden_scales", align_bytes=64)
+        def quantize_hidden(h, c0=0, c1=None):
+            c0, c1 = span(h, c0, c1)
+            codes = tile_of(hidden_codes, h, two, [P, WIDTHS[h]], U32, "hidden_codes")
+            scales = tile_of(hidden_scales, h, two, [P, WIDTHS[h]], U8, "hidden_scales")
             nc.vector.quantize_mx(
-                out=hidden_codes[h][:].bitcast(FP8X4), scales=hidden_scales[h][:], in_=hidden_woven[h][:]
+                out=codes[:, c0:c1].bitcast(FP8X4), scales=scales[:, c0:c1], in_=hidden_woven[h][:, ROWS * c0 : ROWS * c1]
             )
 
-        def second_layer(h, t0=0, t1=ROWS, order=None):
-            if t0 == 0:
-                gate[h] = four.tile([P, ROWS, WIDTHS[h]], F32, name="gate")
-            order = list(order or range(t0, t1))
-            rows = BANK // WIDTHS[h]
+        def second_layer(h, order=(0, 1, 2, 3), c0=0, c1=None):
+            c0, c1 = span(h, c0, c1)
+            dst = tile_of(gate, h, four, [P, ROWS, WIDTHS[h]], F32, "gate")
+            rows = BANK // (c1 - c0)
             for first in range(0, len(order), rows):
-                acc = scalar_banks.tile([P, rows, WIDTHS[h]], F32, name="bank")
+                acc = scalar_banks.tile([P, rows, c1 - c0], F32, name="bank")
                 for r, t in enumerate(order[first : first + rows]):
                     m = slice(P * t, P * t + P)
                     nc.tensor.matmul_mx(
                         out=acc[:, r, :],
                         lhsT=w2[:, m].bitcast(FP8X4),
                         lhsT_scale=s2[:, m],
-                        rhs=hidden_codes[h][:].bitcast(FP8X4),
-                        rhs_scale=hidden_scales[h][:],
+                        rhs=hidden_codes[h][:, c0:c1].bitcast(FP8X4),
+                        rhs_scale=hidden_scales[h][:, c0:c1],
                         start=True,
                         stop=True,
                     )
                 for r, t in enumerate(order[first : first + rows]):
                     nc.scalar.activation(
-                        out=gate[h][:, t, :], in_=acc[:, r, :], func=ACT.Sigmoid, bias=b2[:, t : t + 1]
+                        out=dst[:, t, c0:c1], in_=acc[:, r, :], func=ACT.Sigmoid, bias=b2[:, t : t + 1]
                     )
 
-        def agg_to_bank(h, t0, t1, c1=None):
-            c1 = WIDTHS[h] if c1 is None else c1
-            bank = vector_banks.tile([P, t1 - t0, c1], BF16, name="bank")
+        def agg_to_bank(h, t0, t1, c0=0, c1=None):
+            c0, c1 = span(h, c0, c1)
+            bank = vector_banks.tile([P, t1 - t0, c1 - c0], BF16, name="bank")
             for t in range(t0, t1):
-                agg_bank[h, t] = bank[:, t - t0 :, :]
-            rows = BANK // c1
+                agg_bank[h, t, c0] = bank[:, t - t0 :, :]
+            rows = BANK // (c1 - c0)
             for t in range(t0, t1, rows):
                 end = min(t + rows, t1)
                 nc.tensor.matmul(
                     out=bank[:, t - t0 : end - t0, :],
                     lhsT=ident[:],
-                    rhs=agg_rows[h][:, t:end, :c1],
+                    rhs=agg_rows[h][:, t:end, c0:c1],
                     start=True,
                     stop=True,
                 )
 
-        def product_from_bank(h, t0, t1, c1=None):
-            part = gate[h][:, t0:t1, :c1]
-            nc.vector.tensor_tensor(out=part, in0=part, in1=agg_bank[h, t0][:, : t1 - t0, :], op=ALU.mult)
+        def product_from_bank(h, t0, t1, c0=0, c1=None):
+            c0, c1 = span(h, c0, c1)
+            part = gate[h][:, t0:t1, c0:c1]
+            nc.vector.tensor_tensor(out=part, in0=part, in1=agg_bank[h, t0, c0][:, : t1 - t0, :], op=ALU.mult)
 
-        def store(h, t0, t1):
-            b, c0 = divmod(STARTS[h], PIX)
-            nc.sync.dma_start(out=out_hbm[b][:, t0:t1, c0 : c0 + WIDTHS[h]], in_=gate[h][:, t0:t1, :])
-
-        def product(h, t0, t1, engine="vector", c0=0):
-            rows = gate[h][:, t0:t1, c0:]
+        def product(h, t0, t1, engine="vector", c0=0, c1=None):
+            c0, c1 = span(h, c0, c1)
+            part = gate[h][:, t0:t1, c0:c1]
             multiply = nc.vector.tensor_tensor if engine == "vector" else nc.gpsimd.tensor_tensor
-            multiply(out=rows, in0=rows, in1=agg_rows[h][:, t0:t1, c0:], op=ALU.mult)
+            multiply(out=part, in0=part, in1=agg_rows[h][:, t0:t1, c0:c1], op=ALU.mult)
+
+        def store(h, t0, t1, c0=0, c1=None, src=None):
+            c0, c1 = span(h, c0, c1)
+            b, first = divmod(STARTS[h], PIX)
+            src = gate[h][:, t0:t1, c0:c1] if src is None else src
+            nc.sync.dma_start(out=out_hbm[b][:, t0:t1, first + c0 : first + c1], in_=src)
+
+        def last_row_to_bank(h):
+            bank = vector_banks.tile([P, FULL + VECTOR_PIXELS], BF16, name="bank")
+            agg_bank[h, 2, 0] = bank[:, :FULL].unsqueeze(1)
+            agg_bank[h, 3, 0] = bank[:, FULL:]
+            for t, n in ((2, FULL), (3, VECTOR_PIXELS)):
+                nc.tensor.matmul(
+                    out=agg_bank[h, t, 0], lhsT=ident[:], rhs=agg_rows[h][:, t, :n], start=True, stop=True
+                )
+
+        def last_row_aside(h, spent):
+            aside[h] = spent[:, : 2 * FULL].bitcast(F32)
+            nc.gpsimd.tensor_tensor(
+                out=aside[h][:, VECTOR_PIXELS:],
+                in0=gate[h][:, 3, VECTOR_PIXELS:],
+                in1=agg_rows[h][:, 3, VECTOR_PIXELS:],
+                op=ALU.mult,
+            )
+            nc.vector.tensor_tensor(
+                out=aside[h][:, :VECTOR_PIXELS], in0=gate[h][:, 3, :VECTOR_PIXELS], in1=agg_bank[h, 3, 0], op=ALU.mult
+            )
+
+        def product_aside(h, t0, t1, spent):
+            rows = spent[:, : 2 * (t1 - t0) * FULL].bitcast(F32).rearrange("p (t n) -> p t n", n=FULL)
+            nc.gpsimd.tensor_tensor(out=rows, in0=gate[h][:, t0:t1, :], in1=agg_rows[h][:, t0:t1, :], op=ALU.mult)
+            return rows
+
+        def weave_shares_by_matmul(h):
+            bank = scalar_banks.tile([P, 2, X_PAIRED + AGG_PAIRED, 2], BF16, name="bank")
+            pair_bank["x", h, HALF] = bank[:, :, :X_PAIRED]
+            pair_bank["agg", h, 0] = bank[:, :, X_PAIRED:]
+            shares = (
+                (pair_bank["x", h, HALF], x_wide[h][:, :, HALF : HALF + X_PAIRED]),
+                (pair_bank["agg", h, 0], agg_rows[h][:, :, :AGG_PAIRED]),
+            )
+            for dst, rows in shares:
+                nc.tensor.matmul(
+                    out=dst, lhsT=ident[:], rhs=rows.rearrange("p (u e) n -> p u n e", e=2), start=True, stop=True
+                )
+            join("x", h, HALF, HALF + X_PAIRED)
+            join("agg", h, 0, AGG_PAIRED)
 
         widen(1, "scalar")
         widen_pairs(0)
-        weave_agg(0, "scalar")
-        join_x(0, nc.vector.tensor_copy)
-        weave_x(1, "vector")
-        weave_agg(1, "scalar")
-        spread_bias()
-        move_columns(s1, s1_raw)
-        quantize_cat(0, 0)
-        quantize_cat(0, 1)
-        move_columns(w1[0], w1_raw[0])
-        move_columns(w1[1], w1_raw[1])
-        first_layer(0)
-        quantize_cat(1, 0)
-        quantize_cat(1, 1)
-        first_layer(1)
         widen(2, "scalar", 0, 2)
-        move_columns(s2, s2_raw)
-        widen(2, "vector", 2, 4)
-        weave_x(2, "gpsimd", HEAD_SPLIT)
-        weave_x(2, "scalar", 0, HEAD_SPLIT)
+        join_x(0)
+        weave_x(1, "vector", 0, P)
+        weave_agg(0, "vector")
+        weave_agg(1, "scalar")
+        quantize_cat(0, 0)
+        move_columns(w1[0], w1_raw[0])
+        quantize_cat(0, 1)
+        move_columns(w1[1], w1_raw[1])
+        move_columns(s1, s1_raw)
+        first_layer(0)
+        widen(2, "scalar", 2, 4)
+        spread_bias()
+        weave_x(1, "vector", P)
+        quantize_cat(1, 1)
+        quantize_cat(1, 0)
+        first_layer(1)
+        shared = three.tile([P, 3 * ROWS * HALF], BF16, name="shared", align_bytes=64)
+        x_woven[2] = shared[:, ROWS * HALF :]
+        agg_woven[2] = shared[:, : ROWS * FULL]
+        weave_x(2, "vector", 0, HALF)
+        weave_x(2, "vector", HALF)
+        quantize_cat(2, 0, 0, HALF)
+        quantize_cat(2, 0, HALF)
+        widen(3, "scalar")
+        weave_agg(2, "gpsimd", HEAD_SPLIT)
+        weave_agg(2, "scalar", 0, HEAD_SPLIT)
         add_bias(0)
         add_bias(1)
-        weave_agg(2, "scalar", HALF)
-        widen(3, "scalar", 0, 2)
-        weave_agg_by_matmul(2, 0, HALF)
+        weave_x(3, "scalar")
+        pair("agg", 3, 0, HALF)
+        quantize_cat(2, 1)
+        first_layer(2, 0, 2)
         relu(0)
         move_columns(w2, w2_raw)
+        move_columns(s2, s2_raw)
         quantize_hidden(0)
-        quantize_cat(2, 0)
-        widen(3, "scalar", 2, 4)
-        weave_x(3, "scalar", 0, HEAD_SPLIT)
-        weave_agg_by_matmul(3, 0, HALF)
-        second_layer(0)
         relu(1)
-        quantize_cat(2, 1)
-        weave_agg(3, "vector", HALF)
+        widen(4, "scalar", 0, 1)
+        join("agg", 3, 0, HALF)
+        weave_agg(3, "scalar", HALF, HALF + P)
+        widen(4, "scalar", 1, 2)
+        second_layer(0)
+        first_layer(2, 2, 4)
+        weave_agg(3, "vector", HALF + P)
         quantize_hidden(1)
-        first_layer(2)
-        weave_x(3, "vector", HALF)
-        weave_x(3, "vector", HEAD_SPLIT, HALF)
-        widen(4, "scalar")
+        widen(4, "scalar", 2, 4)
         second_layer(1)
         quantize_cat(3, 0, HALF)
         quantize_cat(3, 1)
         quantize_cat(3, 0, 0, HALF)
+        agg_woven[4] = agg_woven[3]
         weave_agg(4, "gpsimd")
         add_bias(2)
-        agg_to_bank(0, 0, 2)
+        agg_to_bank(0, 0, 3)
         agg_to_bank(1, 0, 4)
-        pair_x(4, 0, HALF)
+        pair("x", 4, 0, HALF)
         weave_x(4, "scalar", HALF)
-        join_x_bank(4, 0, HALF)
-        product(0, 2, 4, "gpsimd")
-        product_from_bank(0, 0, 2)
+        join("x", 4, 0, HALF)
+        product(0, 3, 4, "gpsimd")
+        product_from_bank(0, 0, 3)
         store(0, 0, 4)
         product_from_bank(1, 0, 4)
         store(1, 0, 4)
         first_layer(3)
         widen(5, "scalar")
-        for s in range(3, ROWS_FROM):
+
+        for s in range(3, LAST - 1):
             h = s - 1
-            half = WIDTHS[s + 2] // 2
-            mine = VECTOR_PIXELS_LATE if s + 3 == LAST else VECTOR_PIXELS
-            paired = AGG_PAIRED if s + 3 < LAST else 0
             relu(h)
             quantize_cat(s + 1, 0, HALF)
             quantize_hidden(h)
             quantize_cat(s + 1, 1)
             quantize_cat(s + 1, 0, 0, HALF)
-            second_layer(h, order=(2, 3, 0, 1))
-            weave_agg(s + 2, "gpsimd", paired)
-            if s + 3 == LAST:
-                weave_agg(LAST, "gpsimd")
+            second_layer(h, (2, 3, 0, 1))
+            agg_woven[s + 2] = agg_woven[s + 1]
+            weave_agg(s + 2, "gpsimd", AGG_PAIRED)
             add_bias(s)
-            agg_to_bank(h, 2, 4, mine)
-            pair_x(s + 2, 0, half, (0,))
+            agg_to_bank(h, 2, 4, 0, VECTOR_PIXELS)
+            pair("x", s + 2, 0, HALF, (0,))
             agg_to_bank(h, 0, 2)
-            pair_x(s + 2, 0, half, (1,))
-            weave_x(s + 2, "scalar", half + (X_PAIRED if paired else 0))
-            join_x_bank(s + 2, 0, half)
-            if paired:
-                weave_shares_by_matmul(s + 2)
-            product_from_bank(h, 2, 4, mine)
-            product(h, 2, 4, "gpsimd", mine)
+            pair("x", s + 2, 0, HALF, (1,))
+            weave_x(s + 2, "scalar", HALF + X_PAIRED)
+            join("x", s + 2, 0, HALF)
+            weave_shares_by_matmul(s + 2)
+            product_from_bank(h, 2, 4, 0, VECTOR_PIXELS)
+            product(h, 2, 4, "gpsimd", VECTOR_PIXELS)
             product_from_bank(h, 0, 2)
             store(h, 0, 2)
             store(h, 2, ROWS)
-            if s + 1 < ROWS_FROM:
+            if s + 2 < LAST:
                 first_layer(s + 1)
-            if s + 3 < LAST:
                 widen(s + 3, "scalar")
-            if s + 4 == LAST:
-                widen(LAST, "scalar")
-        s = ROWS_FROM
+
+        s = LAST - 1
         first_layer_rows(s)
         relu(s - 1)
-        quantize_cat(s + 1, 0)
+        quantize_cat(LAST, 0, 0, HALF)
         quantize_hidden(s - 1)
-        quantize_cat(s + 1, 1)
-        weave_x(LAST, "scalar", P // 2)
-        second_layer(s - 1)
-        weave_x(LAST, "vector", 0, P // 2)
         quantize_cat(LAST, 1)
+        second_layer(s - 1)
+        quantize_cat(LAST, 0, HALF)
         weave_hidden(s, "vector")
-        quantize_cat(LAST, 0)
         agg_to_bank(s - 1, 0, 2)
         agg_to_bank(s - 1, 2, 3)
-        first_layer_rows(s + 1)
+        first_layer_rows(LAST, 0, HALF)
         quantize_hidden(s)
-        second_layer(s, 0, 2)
-        first_layer_rows(LAST)
-        second_layer(s, 2, 4)
+        second_layer(s, (0, 1))
+        first_layer_rows(LAST, HALF)
+        second_layer(s, (2, 3))
         product(s - 1, 3, 4, "gpsimd")
         for t in range(3):
             product_from_bank(s - 1, t, t + 1)
             store(s - 1, t, t + 1)
         store(s - 1, 3, 4)
-        weave_hidden(s + 1, "vector")
+        weave_hidden(LAST, "vector", 0, HALF)
         product(s, 0, 1)
         store(s, 0, 1)
-        quantize_hidden(s + 1)
-        second_layer(s + 1)
+        quantize_hidden(LAST, 0, HALF)
+        second_layer(LAST, c1=HALF)
         product(s, 1, 2)
         store(s, 1, 2)
-        weave_hidden(LAST, "vector")
+        weave_hidden(LAST, "vector", HALF)
         product(s, 2, 3)
         store(s, 2, 3)
-        quantize_hidden(LAST)
-        second_layer(LAST)
+        quantize_hidden(LAST, HALF)
+        second_layer(LAST, c0=HALF)
         product(s, 3, 4)
         store(s, 3, 4)
-        product(s + 1, 0, 2)
-        store(s + 1, 0, 2)
-        product(s + 1, 2, 4)
-        store(s + 1, 2, 4)
-        product(LAST, 0, 2)
-        store(LAST, 0, 2)
+        product(LAST, 0, 2, c1=HALF)
+        store(LAST, 0, 2, c1=HALF)
+        product(LAST, 2, 4, c1=HALF)
+        store(LAST, 2, 4, c1=HALF)
+        product(LAST, 0, 2, c0=HALF)
+        store(LAST, 0, 2, c0=HALF)
         for t in range(2, ROWS):
-            product(LAST, t, t + 1)
-            store(LAST, t, t + 1)
+            product(LAST, t, t + 1, c0=HALF)
+            store(LAST, t, t + 1, c0=HALF)

@@ -29,11 +29,13 @@ COUNT = len(WIDTHS)
 LAST = COUNT - 1
 STARTS = [sum(WIDTHS[:h]) for h in range(COUNT)]
 X_LOADS = [PIX] * IMAGES
-AGG_LOADS = [512, 512] + [PIX] * (IMAGES - 1)
+AGG_LOADS = [512] * 4 + [PIX] * (IMAGES - 2)
 HEAD_SPLIT = 128
 VECTOR_PIXELS = 256
 X_PAIRED = 32
 AGG_PAIRED = 64
+BOTH_FROM = 13
+TAIL_SPLIT = 128
 
 
 def tile_graphaugmentation_pb_t_w8_kernel(
@@ -115,13 +117,14 @@ def tile_graphaugmentation_pb_t_w8_kernel(
         load_scales(s1_raw, g1w_scales)
         load_x(1)
         load_agg(1)
+        load_agg(2)
         load_words(w2_raw, g2w_words[0])
         load_scales(s2_raw, g2w_scales)
-        load_agg(2)
+        load_agg(3)
         load_b2()
         for j in range(2, len(X_LOADS)):
             load_x(j)
-            load_agg(j + 1)
+            load_agg(j + 2)
 
         w1 = [keep.tile([P, C], I32, name=f"w1_{g}", align_bytes=64) for g in range(2)]
         w2 = keep.tile([P, C], I32, name="w2", align_bytes=64)
@@ -142,6 +145,11 @@ def tile_graphaugmentation_pb_t_w8_kernel(
 
         x_wide, x_woven, agg_woven, cat_codes, cat_scales, sums, biased, hidden = ({} for stage in range(8))
         hidden_woven, hidden_codes, hidden_scales, gate, pair_bank, agg_bank, aside = ({} for stage in range(7))
+
+        cat_woven = keep.tile([P, 2 * ROWS * FULL], BF16, name="cat_woven", align_bytes=64)
+        for h in range(BOTH_FROM, COUNT):
+            x_woven[h] = cat_woven[:, : ROWS * FULL]
+            agg_woven[h] = cat_woven[:, ROWS * FULL :]
 
         def span(h, c0, c1):
             return c0, WIDTHS[h] if c1 is None else c1
@@ -403,6 +411,15 @@ def tile_graphaugmentation_pb_t_w8_kernel(
             join("x", h, HALF, HALF + X_PAIRED)
             join("agg", h, 0, AGG_PAIRED)
 
+        def quantize_both(h):
+            codes = tile_of(cat_codes, h, three, [P, 2, FULL], U32, "cat_codes")
+            scales = tile_of(cat_scales, h, three, [P, 2, FULL], U8, "cat_scales")
+            nc.vector.quantize_mx(
+                out=codes[:].rearrange("p g n -> p (g n)").bitcast(FP8X4),
+                scales=scales[:].rearrange("p g n -> p (g n)"),
+                in_=cat_woven[:],
+            )
+
         widen(1, "scalar")
         widen_pairs(0)
         widen(2, "scalar", 0, 2)
@@ -500,34 +517,47 @@ def tile_graphaugmentation_pb_t_w8_kernel(
                 widen(s + 3, "scalar")
 
         s = LAST - 1
-        first_layer_rows(s)
+        first_layer_rows(s, 0, HALF)
+        first_layer_rows(s, HALF)
         relu(s - 1)
         quantize_cat(LAST, 0, 0, HALF)
         quantize_hidden(s - 1)
         quantize_cat(LAST, 1)
-        second_layer(s - 1)
-        quantize_cat(LAST, 0, HALF)
-        weave_hidden(s, "vector")
+        second_layer(s - 1, (2, 3))
+        first_layer(LAST, 0, 1)
+        second_layer(s - 1, (0, 1))
         agg_to_bank(s - 1, 0, 2)
-        agg_to_bank(s - 1, 2, 3)
-        first_layer_rows(LAST, 0, HALF)
-        quantize_hidden(s)
+        first_layer(LAST, 1, 2)
+        quantize_cat(LAST, 0, HALF)
+        share_tile(s)
+        weave_hidden(s, "vector", 0, HALF)
+        weave_hidden(s, "vector", HALF)
+        quantize_hidden(s, 0, HALF)
+        quantize_hidden(s, HALF)
         second_layer(s, (0, 1))
+        agg_to_bank(s, 0, 1)
         first_layer_rows(LAST, HALF)
-        second_layer(s, (2, 3))
+        second_layer(s, (2,))
+        weave_hidden(LAST, "scalar", HALF, HALF + TAIL_SPLIT)
+        second_layer(s, (3,))
+        rows = product_aside(s - 1, 2, 3, agg_woven[s + 3][:, 2 * FULL :])
         product(s - 1, 3, 4, "gpsimd")
-        for t in range(3):
-            product_from_bank(s - 1, t, t + 1)
-            store(s - 1, t, t + 1)
+        add_bias(LAST, 0, 1)
+        product_from_bank(s - 1, 0, 1)
+        store(s - 1, 0, 1)
+        store(s - 1, 2, 3, src=rows)
+        add_bias(LAST, 1, 2)
+        product_from_bank(s - 1, 1, 2)
+        store(s - 1, 1, 2)
+        product_from_bank(s, 0, 1)
         store(s - 1, 3, 4)
-        weave_hidden(LAST, "vector", 0, HALF)
-        product(s, 0, 1)
         store(s, 0, 1)
-        quantize_hidden(LAST, 0, HALF)
-        second_layer(LAST, c1=HALF)
+        relu(LAST, 0, HALF)
         product(s, 1, 2)
         store(s, 1, 2)
-        weave_hidden(LAST, "vector", HALF)
+        quantize_hidden(LAST, 0, HALF)
+        second_layer(LAST, c1=HALF)
+        weave_hidden(LAST, "vector", HALF + TAIL_SPLIT)
         product(s, 2, 3)
         store(s, 2, 3)
         quantize_hidden(LAST, HALF)

@@ -27,15 +27,21 @@ FLOPS = 2 * IMAGES * PIX * C * (2 * C + C)
 WIDTHS = [HALF, HALF] + [FULL] * 11
 COUNT = len(WIDTHS)
 LAST = COUNT - 1
+FIRST = 3
+PART = ROWS * FULL
 STARTS = [sum(WIDTHS[:h]) for h in range(COUNT)]
 X_LOADS = [PIX] * IMAGES
-AGG_LOADS = [512] * 4 + [PIX] * (IMAGES - 2)
+AGG_LOADS = [FULL, FULL] + [PIX] * (IMAGES - 1)
 HEAD_SPLIT = 128
-VECTOR_PIXELS = 256
-X_PAIRED = 32
-AGG_PAIRED = 64
-BOTH_FROM = 13
+HEAD_AGG = 192
+EARLY_PIXELS = 368
+VECTOR_PIXELS = 224
 TAIL_SPLIT = 128
+X_PAIRED = 32
+AGG_PAIRED = 48
+TURN_PIXELS = 256
+LATE_AGG = 64
+EARLY_AGG = 128
 
 
 def tile_graphaugmentation_pb_t_w8_kernel(
@@ -48,11 +54,21 @@ def tile_graphaugmentation_pb_t_w8_kernel(
 
     with ExitStack() as ctx:
         keep = ctx.enter_context(tc.tile_pool(name="keep", bufs=1))
+        one = ctx.enter_context(tc.tile_pool(name="one", bufs=1))
         two = ctx.enter_context(tc.tile_pool(name="two", bufs=2))
         three = ctx.enter_context(tc.tile_pool(name="three", bufs=3))
-        four = ctx.enter_context(tc.tile_pool(name="four", bufs=4))
-        vector_banks = ctx.enter_context(tc.psum_pool(name="vector_banks", bufs=4))
-        scalar_banks = ctx.enter_context(tc.psum_pool(name="scalar_banks", bufs=4))
+        banks = ctx.enter_context(tc.psum_pool(name="banks", bufs=1))
+        rings = {"vector": [0, 1, 2, 3], "scalar": [4, 5, 6], "held": [7]}
+
+        def next_bank(ring, shape, dtype):
+            k = rings[ring][0]
+            rings[ring] = rings[ring][1:] + [k]
+            return banks.tile(shape, dtype, name=f"bank{k}")
+
+        def hand_over(source, target):
+            rings[target] = rings[source][:1] + rings[target]
+            rings[source] = rings[source][1:]
+
         ctx.enter_context(tc.manual_schedule())
 
         xs = keep.tile([P, ROWS], F32, name="xs")
@@ -117,14 +133,13 @@ def tile_graphaugmentation_pb_t_w8_kernel(
         load_scales(s1_raw, g1w_scales)
         load_x(1)
         load_agg(1)
-        load_agg(2)
         load_words(w2_raw, g2w_words[0])
         load_scales(s2_raw, g2w_scales)
-        load_agg(3)
+        load_agg(2)
         load_b2()
         for j in range(2, len(X_LOADS)):
             load_x(j)
-            load_agg(j + 2)
+            load_agg(j + 1)
 
         w1 = [keep.tile([P, C], I32, name=f"w1_{g}", align_bytes=64) for g in range(2)]
         w2 = keep.tile([P, C], I32, name="w2", align_bytes=64)
@@ -146,10 +161,29 @@ def tile_graphaugmentation_pb_t_w8_kernel(
         x_wide, x_woven, agg_woven, cat_codes, cat_scales, sums, biased, hidden = ({} for stage in range(8))
         hidden_woven, hidden_codes, hidden_scales, gate, pair_bank, agg_bank, aside = ({} for stage in range(7))
 
-        cat_woven = keep.tile([P, 2 * ROWS * FULL], BF16, name="cat_woven", align_bytes=64)
-        for h in range(BOTH_FROM, COUNT):
-            x_woven[h] = cat_woven[:, : ROWS * FULL]
-            agg_woven[h] = cat_woven[:, ROWS * FULL :]
+        whole = {}
+
+        x_image = keep.tile([P, ROWS * PIX], BF16, name="x_image", align_bytes=64)
+        turns = keep.tile([P, 3 * PART], BF16, name="turns", align_bytes=64)
+        hidden_image = keep.tile([P, ROWS * PIX], BF16, name="hidden_image", align_bytes=64)
+        for h in range(FIRST, COUNT):
+            first = ROWS * (STARTS[h] % PIX)
+            x_woven[h] = x_image[:, first : first + PART]
+            agg_woven[h] = turns[:, first : first + PART]
+            hidden_woven[h] = hidden_image[:, first : first + PART]
+        hidden_woven[0] = turns[:, 3 * PART // 2 : 2 * PART]
+        hidden_woven[1] = turns[:, 2 * PART : 5 * PART // 2]
+        hidden_woven[2] = hidden_image[:, PART:]
+
+        def image_tile(store, h, pool, rows, scale, dtype, name):
+            if h not in store:
+                i = STARTS[h] // PIX
+                whole[name, i] = pool.tile([P, rows, scale * PIX], dtype, name=name, align_bytes=64)
+                for k in range(COUNT):
+                    if STARTS[k] // PIX == i and k not in store:
+                        first = STARTS[k] % PIX
+                        store[k] = whole[name, i][:, :, scale * first : scale * (first + WIDTHS[k])]
+            return store[h]
 
         def span(h, c0, c1):
             return c0, WIDTHS[h] if c1 is None else c1
@@ -160,7 +194,7 @@ def tile_graphaugmentation_pb_t_w8_kernel(
             return store[h]
 
         def widen(h, engine, t0=0, t1=ROWS):
-            dst = tile_of(x_wide, h, four, [P, ROWS, WIDTHS[h]], BF16, "x_wide")
+            dst = tile_of(x_wide, h, two, [P, ROWS, WIDTHS[h]], BF16, "x_wide")
             for t in range(t0, t1):
                 codes = x_rows[h][:, t, :].bitcast(FP8)
                 if engine == "scalar":
@@ -170,8 +204,18 @@ def tile_graphaugmentation_pb_t_w8_kernel(
                         out=dst[:, t, :], in0=codes, scalar1=xs[:, t : t + 1], scalar2=None, op0=ALU.mult
                     )
 
+        def widen_image(i, t0=0, t1=ROWS, c0=0, c1=PIX):
+            image_tile(x_wide, 2 * i + 1, two, ROWS, 1, BF16, "x_wide")
+            for t in range(t0, t1):
+                nc.scalar.activation(
+                    out=whole["x_wide", i][:, t, c0:c1],
+                    in_=x_loaded[i][:, t, c0:c1].bitcast(FP8),
+                    func=ACT.Copy,
+                    scale=xs[:, t : t + 1],
+                )
+
         def widen_pairs(h):
-            dst = tile_of(x_wide, h, four, [P, 2, 2 * WIDTHS[h]], BF16, "x_wide")
+            dst = tile_of(x_wide, h, one, [P, 2, 2 * WIDTHS[h]], BF16, "x_pairs")
             for t in range(ROWS):
                 nc.vector.tensor_scalar(
                     out=dst[:, t // 2, t % 2 :: 2],
@@ -185,15 +229,10 @@ def tile_graphaugmentation_pb_t_w8_kernel(
             return tile_of(x_woven, h, two, [P, ROWS * WIDTHS[h]], BF16, "x_woven")
 
         def agg_tile(h):
-            return tile_of(agg_woven, h, three, [P, ROWS * FULL], BF16, "agg_woven")
+            return tile_of(agg_woven, h, two, [P, ROWS * WIDTHS[h]], BF16, "agg_woven")
 
         def hidden_tile(h):
             return tile_of(hidden_woven, h, two, [P, ROWS * WIDTHS[h]], BF16, "hidden_woven")
-
-        def share_tile(h):
-            shared = three.tile([P, 3 * ROWS * HALF], BF16, name="shared", align_bytes=64)
-            hidden_woven[h] = shared[:, ROWS * HALF :]
-            agg_woven[h + 3] = shared[:, : ROWS * FULL]
 
         def weave(engine, dst, rows, c0, c1):
             woven = dst[:, ROWS * c0 : ROWS * c1].rearrange("p (c i t) -> p c t i", i=NEIGHBOURS, t=ROWS)
@@ -210,8 +249,13 @@ def tile_graphaugmentation_pb_t_w8_kernel(
         def weave_agg(h, engine, c0=0, c1=None):
             weave(engine, agg_tile(h), agg_rows[h], *span(h, c0, c1))
 
+        def weave_agg_image(i, engine, c0, c1):
+            weave(engine, turns, agg_loaded[i + 1], c0, c1)
+
         def weave_hidden(h, engine, c0=0, c1=None):
-            weave(engine, hidden_tile(h), hidden[h], *span(h, c0, c1))
+            c0, c1 = span(h, c0, c1)
+            first = c0 // HALF * HALF
+            weave(engine, hidden_tile(h)[:, ROWS * first :], hidden[h, c0 // HALF], c0 - first, c1 - first)
 
         def join_x(h):
             nc.vector.tensor_copy(
@@ -219,10 +263,10 @@ def tile_graphaugmentation_pb_t_w8_kernel(
                 in_=x_wide[h][:].bitcast(F32).rearrange("p u n -> p n u"),
             )
 
-        def pair(name, h, c0, c1, pairs=(0, 1)):
+        def pair(name, h, c0, c1, pairs=(0, 1), ring="scalar"):
             rows = {"x": x_wide, "agg": agg_rows, "hidden": hidden}[name][h]
             if 0 in pairs:
-                pair_bank[name, h, c0] = scalar_banks.tile([P, 2, c1 - c0, 2], BF16, name="bank")[:]
+                pair_bank[name, h, c0] = next_bank(ring, [P, 2, c1 - c0, 2], BF16)[:]
             for u in pairs:
                 nc.tensor.matmul(
                     out=pair_bank[name, h, c0][:, u],
@@ -241,13 +285,26 @@ def tile_graphaugmentation_pb_t_w8_kernel(
 
         def quantize_cat(h, g, c0=0, c1=None):
             c0, c1 = span(h, c0, c1)
-            codes = tile_of(cat_codes, h, three, [P, 2, WIDTHS[h]], U32, "cat_codes")
-            scales = tile_of(cat_scales, h, three, [P, 2, WIDTHS[h]], U8, "cat_scales")
+            codes = image_tile(cat_codes, h, two, 2, 1, U32, "cat_codes")
+            scales = image_tile(cat_scales, h, two, 2, 1, U8, "cat_scales")
             nc.vector.quantize_mx(
                 out=codes[:, g, c0:c1].bitcast(FP8X4),
                 scales=scales[:, g, c0:c1],
                 in_=(x_woven, agg_woven)[g][h][:, ROWS * c0 : ROWS * c1],
             )
+
+        def pair_shares(h, k):
+            bank = next_bank("scalar", [P, 2, X_PAIRED + AGG_PAIRED, 2], BF16)
+            pair_bank["x", h, FULL - X_PAIRED] = bank[:, :, :X_PAIRED]
+            pair_bank["agg", k, FULL - AGG_PAIRED] = bank[:, :, X_PAIRED:]
+            shares = (
+                (bank[:, :, :X_PAIRED], x_wide[h][:, :, FULL - X_PAIRED :]),
+                (bank[:, :, X_PAIRED:], agg_rows[k][:, :, FULL - AGG_PAIRED :]),
+            )
+            for dst, rows in shares:
+                nc.tensor.matmul(
+                    out=dst, lhsT=ident[:], rhs=rows.rearrange("p (u e) n -> p u n e", e=2), start=True, stop=True
+                )
 
         def first_pass(dst, h, g, t, n):
             m = slice(P * t, P * t + P)
@@ -264,13 +321,25 @@ def tile_graphaugmentation_pb_t_w8_kernel(
         def first_layer(h, j0=0, j1=None):
             for j in range(j0, WIDTHS[h] // P if j1 is None else j1):
                 c, u = divmod(j, 2)
-                sums[h, j] = vector_banks.tile([P, 2, HALF], F32, name="bank")
+                sums[h, j] = next_bank("vector", [P, 2, HALF], F32)
                 for e in range(2):
                     for g in range(2):
                         first_pass(sums[h, j][:, e, :], h, g, 2 * u + e, slice(HALF * c, HALF * (c + 1)))
 
+        def first_layer_early(h, j0, j1):
+            for j in range(j0, j1):
+                c, u = divmod(j, 2)
+                sums[h, j] = next_bank("vector", [P, 2, HALF], F32)
+                first_pass(sums[h, j][:, 0, :], h, 0, 2 * u, slice(HALF * c, HALF * (c + 1)))
+
+        def first_layer_rest(h):
+            for j in range(WIDTHS[h] // P):
+                c, u = divmod(j, 2)
+                for e, g in ((0, 1), (1, 0), (1, 1)):
+                    first_pass(sums[h, j][:, e, :], h, g, 2 * u + e, slice(HALF * c, HALF * (c + 1)))
+
         def add_bias(h, j0=0, j1=None):
-            dst = tile_of(biased, h, two, [P, 2, 2 * WIDTHS[h]], BF16, "biased")
+            dst = image_tile(biased, h, one, 2, 2, BF16, "biased")
             for j in range(j0, WIDTHS[h] // P if j1 is None else j1):
                 c, u = divmod(j, 2)
                 pixels = dst[:, u, 2 * HALF * c : 2 * HALF * (c + 1)]
@@ -294,41 +363,50 @@ def tile_graphaugmentation_pb_t_w8_kernel(
                 op0=ALU.max,
             )
 
+        def relu_image(i, dst):
+            nc.vector.tensor_scalar(
+                out=dst.rearrange("p (n u e) -> p n u e", u=2, e=2),
+                in0=whole["biased", i][:].rearrange("p u (n e) -> p n u e", e=2),
+                scalar1=0.0,
+                scalar2=None,
+                op0=ALU.max,
+            )
+
         def first_layer_rows(h, c0=0, c1=None, t0=0, t1=ROWS):
             c0, c1 = span(h, c0, c1)
-            dst = tile_of(hidden, h, two, [P, ROWS, WIDTHS[h]], BF16, "hidden")
+            dst = tile_of(hidden, (h, c0 // HALF), three, [P, ROWS, HALF], BF16, "hidden")
             rows = BANK // (c1 - c0)
             for first in range(t0, t1, rows):
-                acc = scalar_banks.tile([P, rows, c1 - c0], F32, name="bank")
+                acc = next_bank("scalar", [P, rows, c1 - c0], F32)
                 for r in range(rows):
                     for g in range(2):
                         first_pass(acc[:, r, :], h, g, first + r, slice(c0, c1))
                 for r in range(rows):
                     t = first + r
-                    nc.scalar.activation(out=dst[:, t, c0:c1], in_=acc[:, r, :], func=ACT.Relu, bias=b1[:, t : t + 1])
+                    nc.scalar.activation(out=dst[:, t, :], in_=acc[:, r, :], func=ACT.Relu, bias=b1[:, t : t + 1])
 
         def quantize_hidden(h, c0=0, c1=None):
             c0, c1 = span(h, c0, c1)
-            codes = tile_of(hidden_codes, h, two, [P, WIDTHS[h]], U32, "hidden_codes")
-            scales = tile_of(hidden_scales, h, two, [P, WIDTHS[h]], U8, "hidden_scales")
+            codes = image_tile(hidden_codes, h, two, 1, 1, U32, "hidden_codes")[:, 0, :]
+            scales = image_tile(hidden_scales, h, two, 1, 1, U8, "hidden_scales")[:, 0, :]
             nc.vector.quantize_mx(
                 out=codes[:, c0:c1].bitcast(FP8X4), scales=scales[:, c0:c1], in_=hidden_woven[h][:, ROWS * c0 : ROWS * c1]
             )
 
         def second_layer(h, order=(0, 1, 2, 3), c0=0, c1=None):
             c0, c1 = span(h, c0, c1)
-            dst = tile_of(gate, h, four, [P, ROWS, WIDTHS[h]], F32, "gate")
+            dst = image_tile(gate, h, two, ROWS, 1, F32, "gate")
             rows = BANK // (c1 - c0)
             for first in range(0, len(order), rows):
-                acc = scalar_banks.tile([P, rows, c1 - c0], F32, name="bank")
+                acc = next_bank("scalar", [P, rows, c1 - c0], F32)
                 for r, t in enumerate(order[first : first + rows]):
                     m = slice(P * t, P * t + P)
                     nc.tensor.matmul_mx(
                         out=acc[:, r, :],
                         lhsT=w2[:, m].bitcast(FP8X4),
                         lhsT_scale=s2[:, m],
-                        rhs=hidden_codes[h][:, c0:c1].bitcast(FP8X4),
-                        rhs_scale=hidden_scales[h][:, c0:c1],
+                        rhs=hidden_codes[h][:, 0, c0:c1].bitcast(FP8X4),
+                        rhs_scale=hidden_scales[h][:, 0, c0:c1],
                         start=True,
                         stop=True,
                     )
@@ -339,7 +417,7 @@ def tile_graphaugmentation_pb_t_w8_kernel(
 
         def agg_to_bank(h, t0, t1, c0=0, c1=None):
             c0, c1 = span(h, c0, c1)
-            bank = vector_banks.tile([P, t1 - t0, c1 - c0], BF16, name="bank")
+            bank = next_bank("vector", [P, t1 - t0, c1 - c0], BF16)
             for t in range(t0, t1):
                 agg_bank[h, t, c0] = bank[:, t - t0 :, :]
             rows = BANK // (c1 - c0)
@@ -370,58 +448,13 @@ def tile_graphaugmentation_pb_t_w8_kernel(
             src = gate[h][:, t0:t1, c0:c1] if src is None else src
             nc.sync.dma_start(out=out_hbm[b][:, t0:t1, first + c0 : first + c1], in_=src)
 
-        def last_row_to_bank(h):
-            bank = vector_banks.tile([P, FULL + VECTOR_PIXELS], BF16, name="bank")
-            agg_bank[h, 2, 0] = bank[:, :FULL].unsqueeze(1)
-            agg_bank[h, 3, 0] = bank[:, FULL:]
-            for t, n in ((2, FULL), (3, VECTOR_PIXELS)):
-                nc.tensor.matmul(
-                    out=agg_bank[h, t, 0], lhsT=ident[:], rhs=agg_rows[h][:, t, :n], start=True, stop=True
-                )
-
-        def last_row_aside(h, spent):
-            aside[h] = spent[:, : 2 * FULL].bitcast(F32)
-            nc.gpsimd.tensor_tensor(
-                out=aside[h][:, VECTOR_PIXELS:],
-                in0=gate[h][:, 3, VECTOR_PIXELS:],
-                in1=agg_rows[h][:, 3, VECTOR_PIXELS:],
-                op=ALU.mult,
-            )
-            nc.vector.tensor_tensor(
-                out=aside[h][:, :VECTOR_PIXELS], in0=gate[h][:, 3, :VECTOR_PIXELS], in1=agg_bank[h, 3, 0], op=ALU.mult
-            )
-
         def product_aside(h, t0, t1, spent):
             rows = spent[:, : 2 * (t1 - t0) * FULL].bitcast(F32).rearrange("p (t n) -> p t n", n=FULL)
             nc.gpsimd.tensor_tensor(out=rows, in0=gate[h][:, t0:t1, :], in1=agg_rows[h][:, t0:t1, :], op=ALU.mult)
             return rows
 
-        def weave_shares_by_matmul(h):
-            bank = scalar_banks.tile([P, 2, X_PAIRED + AGG_PAIRED, 2], BF16, name="bank")
-            pair_bank["x", h, HALF] = bank[:, :, :X_PAIRED]
-            pair_bank["agg", h, 0] = bank[:, :, X_PAIRED:]
-            shares = (
-                (pair_bank["x", h, HALF], x_wide[h][:, :, HALF : HALF + X_PAIRED]),
-                (pair_bank["agg", h, 0], agg_rows[h][:, :, :AGG_PAIRED]),
-            )
-            for dst, rows in shares:
-                nc.tensor.matmul(
-                    out=dst, lhsT=ident[:], rhs=rows.rearrange("p (u e) n -> p u n e", e=2), start=True, stop=True
-                )
-            join("x", h, HALF, HALF + X_PAIRED)
-            join("agg", h, 0, AGG_PAIRED)
-
-        def quantize_both(h):
-            codes = tile_of(cat_codes, h, three, [P, 2, FULL], U32, "cat_codes")
-            scales = tile_of(cat_scales, h, three, [P, 2, FULL], U8, "cat_scales")
-            nc.vector.quantize_mx(
-                out=codes[:].rearrange("p g n -> p (g n)").bitcast(FP8X4),
-                scales=scales[:].rearrange("p g n -> p (g n)"),
-                in_=cat_woven[:],
-            )
-
-        widen(1, "scalar")
         widen_pairs(0)
+        widen(1, "scalar")
         widen(2, "scalar", 0, 2)
         join_x(0)
         weave_x(1, "vector", 0, P)
@@ -439,82 +472,200 @@ def tile_graphaugmentation_pb_t_w8_kernel(
         quantize_cat(1, 1)
         quantize_cat(1, 0)
         first_layer(1)
-        shared = three.tile([P, 3 * ROWS * HALF], BF16, name="shared", align_bytes=64)
-        x_woven[2] = shared[:, ROWS * HALF :]
-        agg_woven[2] = shared[:, : ROWS * FULL]
+        shared = one.tile([P, 3 * PART // 2], BF16, name="shared", align_bytes=64)
+        x_woven[2] = shared[:, PART // 2 :]
+        agg_woven[2] = shared[:, :PART]
         weave_x(2, "vector", 0, HALF)
         weave_x(2, "vector", HALF)
         quantize_cat(2, 0, 0, HALF)
         quantize_cat(2, 0, HALF)
-        widen(3, "scalar")
+        widen_image(1, 0, 2)
         weave_agg(2, "gpsimd", HEAD_SPLIT)
         weave_agg(2, "scalar", 0, HEAD_SPLIT)
+        widen_image(1, 2, 4)
         add_bias(0)
         add_bias(1)
-        weave_x(3, "scalar")
-        pair("agg", 3, 0, HALF)
+        first_layer_early(2, 0, 2)
+        pair("x", 3, 0, HALF, (0,), "held")
+        first_layer_early(2, 2, 4)
+        weave_agg_image(1, "scalar", 0, HEAD_AGG)
+        weave_x(3, "scalar", HALF)
+        widen_image(2, 0, 1, 0, FULL)
         quantize_cat(2, 1)
-        first_layer(2, 0, 2)
-        relu(0)
+        first_layer_rest(2)
         move_columns(w2, w2_raw)
+        relu(0)
         move_columns(s2, s2_raw)
-        quantize_hidden(0)
         relu(1)
-        widen(4, "scalar", 0, 1)
-        join("agg", 3, 0, HALF)
-        weave_agg(3, "scalar", HALF, HALF + P)
-        widen(4, "scalar", 1, 2)
-        second_layer(0)
-        first_layer(2, 2, 4)
-        weave_agg(3, "vector", HALF + P)
+        quantize_hidden(0)
         quantize_hidden(1)
-        widen(4, "scalar", 2, 4)
-        second_layer(1)
-        quantize_cat(3, 0, HALF)
-        quantize_cat(3, 1)
-        quantize_cat(3, 0, 0, HALF)
-        agg_woven[4] = agg_woven[3]
-        weave_agg(4, "gpsimd")
+        weave_agg_image(1, "gpsimd", HEAD_AGG, PIX)
+        second_layer(0)
+        second_layer(1, (0, 1))
         add_bias(2)
-        agg_to_bank(0, 0, 3)
+        agg_to_bank(0, 0, 4)
+        second_layer(1, (2, 3))
         agg_to_bank(1, 0, 4)
+        pair("x", 3, 0, HALF, (1,))
+        widen_image(2, 0, 1, FULL)
+        join("x", 3, 0, HALF)
+        widen_image(2, 1, 2, 0, FULL)
         pair("x", 4, 0, HALF)
-        weave_x(4, "scalar", HALF)
-        join("x", 4, 0, HALF)
-        product(0, 3, 4, "gpsimd")
-        product_from_bank(0, 0, 3)
+        pair("x", 4, HALF, FULL)
+        product_from_bank(0, 0, 4)
         store(0, 0, 4)
         product_from_bank(1, 0, 4)
         store(1, 0, 4)
-        first_layer(3)
-        widen(5, "scalar")
 
-        for s in range(3, LAST - 1):
-            h = s - 1
-            relu(h)
-            quantize_cat(s + 1, 0, HALF)
-            quantize_hidden(h)
-            quantize_cat(s + 1, 1)
-            quantize_cat(s + 1, 0, 0, HALF)
-            second_layer(h, (2, 3, 0, 1))
-            agg_woven[s + 2] = agg_woven[s + 1]
-            weave_agg(s + 2, "gpsimd", AGG_PAIRED)
-            add_bias(s)
-            agg_to_bank(h, 2, 4, 0, VECTOR_PIXELS)
-            pair("x", s + 2, 0, HALF, (0,))
-            agg_to_bank(h, 0, 2)
-            pair("x", s + 2, 0, HALF, (1,))
-            weave_x(s + 2, "scalar", HALF + X_PAIRED)
-            join("x", s + 2, 0, HALF)
-            weave_shares_by_matmul(s + 2)
-            product_from_bank(h, 2, 4, 0, VECTOR_PIXELS)
-            product(h, 2, 4, "gpsimd", VECTOR_PIXELS)
-            product_from_bank(h, 0, 2)
-            store(h, 0, 2)
-            store(h, 2, ROWS)
-            if s + 2 < LAST:
-                first_layer(s + 1)
-                widen(s + 3, "scalar")
+        hand_over("held", "vector")
+        join("x", 4, 0, HALF)
+        widen_image(2, 1, 2, FULL)
+        join("x", 4, HALF, FULL)
+        widen_image(2, 2, 4)
+        quantize_cat(3, 1)
+        quantize_cat(3, 0)
+        first_layer(3)
+        relu(2, 0, HALF)
+        relu(2, HALF)
+        quantize_hidden(2, 0, HALF)
+        quantize_hidden(2, HALF)
+        second_layer(2, (0, 1, 2))
+        quantize_cat(4, 1)
+        quantize_cat(4, 0)
+        first_layer(4, 0, 1)
+        weave_agg_image(2, "gpsimd", EARLY_AGG, PIX - AGG_PAIRED)
+        add_bias(3, 0, 1)
+        first_layer(4, 1, 2)
+        second_layer(2, (3,))
+        for j in range(2, ROWS):
+            add_bias(3, j - 1, j)
+            first_layer(4, j, j + 1)
+        add_bias(3, 3, 4)
+        add_bias(4)
+        agg_to_bank(2, 0, 2, 0, EARLY_PIXELS)
+        agg_to_bank(2, 2, 4, 0, EARLY_PIXELS)
+        product(2, 0, 4, "gpsimd", EARLY_PIXELS)
+        product_from_bank(2, 0, 2, 0, EARLY_PIXELS)
+        product_from_bank(2, 2, 4, 0, EARLY_PIXELS)
+        store(2, 0, 4)
+        pair_shares(5, 6)
+        weave_agg_image(2, "scalar", 0, EARLY_AGG)
+        weave_x(5, "scalar", 0, FULL - X_PAIRED)
+        join("x", 5, FULL - X_PAIRED, FULL)
+        pair("x", 6, 0, HALF)
+        pair("x", 6, HALF, FULL)
+
+        for i in range(2, IMAGES - 2):
+            a, b = 2 * i + 1, 2 * i + 2
+            join("x", b, 0, HALF)
+            join("agg", b, FULL - AGG_PAIRED, FULL)
+            widen_image(i + 1, 0, 1, 0, FULL)
+            join("x", b, HALF, FULL)
+            widen_image(i + 1, 0, 1, FULL)
+            widen_image(i + 1, 1, 3)
+            quantize_cat(a, 1)
+            quantize_cat(a, 0)
+            first_layer(a)
+            relu_image(i - 1, hidden_image[:])
+            quantize_cat(b, 0)
+            quantize_hidden(a - 2)
+            second_layer(a - 2, (0, 1, 2))
+            quantize_cat(b, 1)
+            first_layer(b, 0, 1)
+            quantize_hidden(b - 2)
+            weave_agg_image(i + 1, "gpsimd", 0, PIX - AGG_PAIRED)
+            add_bias(a, 0, 1)
+            first_layer(b, 1, 2)
+            widen_image(i + 1, 3, 4)
+            second_layer(a - 2, (3,))
+            add_bias(a, 1, 2)
+            first_layer(b, 2, 3)
+            add_bias(a, 2, 3)
+            second_layer(b - 2, (0,))
+            first_layer(b, 3, 4)
+            add_bias(a, 3, 4)
+            add_bias(b)
+            second_layer(b - 2, (1,))
+            agg_to_bank(a - 2, 0, 4, 0, VECTOR_PIXELS)
+            weave_x(a + 2, "scalar", 0, P)
+            second_layer(b - 2, (2,))
+            agg_to_bank(b - 2, 0, 2)
+            second_layer(b - 2, (3,))
+            agg_to_bank(b - 2, 2, 4)
+            product(a - 2, 0, 4, "gpsimd", VECTOR_PIXELS)
+            product_from_bank(a - 2, 0, 4, 0, VECTOR_PIXELS)
+            product_from_bank(b - 2, 0, 2)
+            store(b - 2, 0, 2)
+            store(a - 2, 0, 4)
+            product_from_bank(b - 2, 2, 4)
+            store(b - 2, 2, 4)
+            pair_shares(a + 2, b + 2)
+            weave_x(a + 2, "scalar", P, FULL - X_PAIRED)
+            join("x", a + 2, FULL - X_PAIRED, FULL)
+            pair("x", b + 2, 0, HALF)
+            pair("x", b + 2, HALF, FULL)
+        a, b = LAST - 3, LAST - 2
+        agg_woven[a + 2] = agg_woven[b]
+        hidden_woven[a + 2] = turns[:, 2 * PART :]
+        hidden_woven[LAST] = hidden_woven[a]
+        join("x", b, 0, HALF)
+        join("agg", b, FULL - AGG_PAIRED, FULL)
+        widen(a + 2, "scalar", 0, 1)
+        join("x", b, HALF, FULL)
+        widen(a + 2, "scalar", 1, 4)
+        widen(LAST, "scalar", 0, 1)
+        quantize_cat(a, 1)
+        quantize_cat(a, 0)
+        first_layer(a)
+        relu_image(IMAGES - 3, hidden_image[:])
+        quantize_cat(b, 0)
+        quantize_hidden(a - 2)
+        second_layer(a - 2, (0, 1, 2))
+        quantize_cat(b, 1)
+        quantize_hidden(b - 2)
+        hand_over("vector", "scalar")
+        weave_agg(a + 2, "gpsimd")
+        second_layer(a - 2, (3,))
+        add_bias(a)
+        second_layer(b - 2, (0,))
+        agg_to_bank(a - 2, 0, 4, 0, TURN_PIXELS)
+        second_layer(b - 2, (1,))
+        agg_to_bank(b - 2, 0, 2)
+        second_layer(b - 2, (2, 3))
+        agg_to_bank(b - 2, 2, 4)
+        pair("x", a + 2, 0, HALF)
+        weave_x(a + 2, "scalar", HALF)
+        join("x", a + 2, 0, HALF)
+        product(a - 2, 0, 4, "gpsimd", TURN_PIXELS)
+        product_from_bank(a - 2, 0, 4, 0, TURN_PIXELS)
+        product_from_bank(b - 2, 0, 2)
+        store(b - 2, 0, 2)
+        store(a - 2, 0, 4)
+        product_from_bank(b - 2, 2, 4)
+        store(b - 2, 2, 4)
+        first_layer(b)
+        widen(LAST, "scalar", 1, 4)
+        relu(a)
+        quantize_cat(a + 2, 0, HALF)
+        quantize_hidden(a)
+        quantize_cat(a + 2, 1)
+        quantize_cat(a + 2, 0, 0, HALF)
+        second_layer(a, (2, 3, 0, 1))
+        weave_agg(LAST, "gpsimd", 0, FULL - LATE_AGG)
+        add_bias(b)
+        agg_to_bank(a, 2, 4, 0, HALF)
+        pair("x", LAST, 0, HALF, (0,))
+        agg_to_bank(a, 0, 2)
+        pair("x", LAST, 0, HALF, (1,))
+        weave_x(LAST, "scalar", HALF)
+        join("x", LAST, 0, HALF)
+        pair("agg", LAST, FULL - LATE_AGG, FULL)
+        join("agg", LAST, FULL - LATE_AGG, FULL)
+        product_from_bank(a, 2, 4, 0, HALF)
+        product(a, 2, 4, "gpsimd", HALF)
+        product_from_bank(a, 0, 2)
+        store(a, 0, 2)
+        store(a, 2, ROWS)
 
         s = LAST - 1
         first_layer_rows(s, 0, HALF)
@@ -529,7 +680,6 @@ def tile_graphaugmentation_pb_t_w8_kernel(
         agg_to_bank(s - 1, 0, 2)
         first_layer(LAST, 1, 2)
         quantize_cat(LAST, 0, HALF)
-        share_tile(s)
         weave_hidden(s, "vector", 0, HALF)
         weave_hidden(s, "vector", HALF)
         quantize_hidden(s, 0, HALF)
@@ -540,7 +690,7 @@ def tile_graphaugmentation_pb_t_w8_kernel(
         second_layer(s, (2,))
         weave_hidden(LAST, "scalar", HALF, HALF + TAIL_SPLIT)
         second_layer(s, (3,))
-        rows = product_aside(s - 1, 2, 3, agg_woven[s + 3][:, 2 * FULL :])
+        rows = product_aside(s - 1, 2, 3, hidden_woven[s])
         product(s - 1, 3, 4, "gpsimd")
         add_bias(LAST, 0, 1)
         product_from_bank(s - 1, 0, 1)

@@ -33,15 +33,16 @@ STARTS = [sum(WIDTHS[:h]) for h in range(COUNT)]
 X_LOADS = [PIX] * IMAGES
 AGG_LOADS = [FULL, FULL] + [PIX] * (IMAGES - 1)
 HEAD_SPLIT = 128
-HEAD_AGG = 192
+HEAD_AGG = 200
 EARLY_PIXELS = 368
 VECTOR_PIXELS = 224
 TAIL_SPLIT = 128
-X_PAIRED = 32
-AGG_PAIRED = 48
+X_PAIRED = 48
+AGG_PAIRED = 56
 TURN_PIXELS = 256
 LATE_AGG = 64
 EARLY_AGG = 128
+TURN_AGG = 128
 
 
 def tile_graphaugmentation_pb_t_w8_kernel(
@@ -214,9 +215,9 @@ def tile_graphaugmentation_pb_t_w8_kernel(
                     scale=xs[:, t : t + 1],
                 )
 
-        def widen_pairs(h):
+        def widen_pairs(h, t0, t1):
             dst = tile_of(x_wide, h, one, [P, 2, 2 * WIDTHS[h]], BF16, "x_pairs")
-            for t in range(ROWS):
+            for t in range(t0, t1):
                 nc.vector.tensor_scalar(
                     out=dst[:, t // 2, t % 2 :: 2],
                     in0=x_rows[h][:, t, :].bitcast(FP8),
@@ -306,7 +307,7 @@ def tile_graphaugmentation_pb_t_w8_kernel(
                     out=dst, lhsT=ident[:], rhs=rows.rearrange("p (u e) n -> p u n e", e=2), start=True, stop=True
                 )
 
-        def first_pass(dst, h, g, t, n):
+        def first_pass(dst, h, g, t, n, opens=0):
             m = slice(P * t, P * t + P)
             nc.tensor.matmul_mx(
                 out=dst,
@@ -314,8 +315,8 @@ def tile_graphaugmentation_pb_t_w8_kernel(
                 lhsT_scale=s1[4 * g :, m],
                 rhs=cat_codes[h][:, g, n].bitcast(FP8X4),
                 rhs_scale=cat_scales[h][:, g, n],
-                start=(g == 0),
-                stop=(g == 1),
+                start=(g == opens),
+                stop=(g != opens),
             )
 
         def first_layer(h, j0=0, j1=None):
@@ -326,17 +327,17 @@ def tile_graphaugmentation_pb_t_w8_kernel(
                     for g in range(2):
                         first_pass(sums[h, j][:, e, :], h, g, 2 * u + e, slice(HALF * c, HALF * (c + 1)))
 
-        def first_layer_early(h, j0, j1):
+        def first_layer_early(h, g, j0=0, j1=ROWS):
             for j in range(j0, j1):
                 c, u = divmod(j, 2)
                 sums[h, j] = next_bank("vector", [P, 2, HALF], F32)
-                first_pass(sums[h, j][:, 0, :], h, 0, 2 * u, slice(HALF * c, HALF * (c + 1)))
+                first_pass(sums[h, j][:, 0, :], h, g, 2 * u, slice(HALF * c, HALF * (c + 1)), g)
 
-        def first_layer_rest(h):
-            for j in range(WIDTHS[h] // P):
+        def first_layer_rest(h, opens):
+            for j in range(ROWS):
                 c, u = divmod(j, 2)
-                for e, g in ((0, 1), (1, 0), (1, 1)):
-                    first_pass(sums[h, j][:, e, :], h, g, 2 * u + e, slice(HALF * c, HALF * (c + 1)))
+                for e, g in ((0, 1 - opens), (1, opens), (1, 1 - opens)):
+                    first_pass(sums[h, j][:, e, :], h, g, 2 * u + e, slice(HALF * c, HALF * (c + 1)), opens)
 
         def add_bias(h, j0=0, j1=None):
             dst = image_tile(biased, h, one, 2, 2, BF16, "biased")
@@ -453,11 +454,14 @@ def tile_graphaugmentation_pb_t_w8_kernel(
             nc.gpsimd.tensor_tensor(out=rows, in0=gate[h][:, t0:t1, :], in1=agg_rows[h][:, t0:t1, :], op=ALU.mult)
             return rows
 
-        widen_pairs(0)
         widen(1, "scalar")
-        widen(2, "scalar", 0, 2)
+        widen_pairs(0, 0, 2)
+        widen(2, "vector", 0, 1)
+        widen_pairs(0, 2, 4)
+        widen(2, "vector", 1, 2)
+        widen(2, "scalar", 2, 4)
         join_x(0)
-        weave_x(1, "vector", 0, P)
+        weave_x(1, "scalar")
         weave_agg(0, "vector")
         weave_agg(1, "scalar")
         quantize_cat(0, 0)
@@ -466,16 +470,14 @@ def tile_graphaugmentation_pb_t_w8_kernel(
         move_columns(w1[1], w1_raw[1])
         move_columns(s1, s1_raw)
         first_layer(0)
-        widen(2, "scalar", 2, 4)
         spread_bias()
-        weave_x(1, "vector", P)
-        quantize_cat(1, 1)
         quantize_cat(1, 0)
-        first_layer(1)
         shared = one.tile([P, 3 * PART // 2], BF16, name="shared", align_bytes=64)
         x_woven[2] = shared[:, PART // 2 :]
         agg_woven[2] = shared[:, :PART]
         weave_x(2, "vector", 0, HALF)
+        quantize_cat(1, 1)
+        first_layer(1)
         weave_x(2, "vector", HALF)
         quantize_cat(2, 0, 0, HALF)
         quantize_cat(2, 0, HALF)
@@ -485,14 +487,13 @@ def tile_graphaugmentation_pb_t_w8_kernel(
         widen_image(1, 2, 4)
         add_bias(0)
         add_bias(1)
-        first_layer_early(2, 0, 2)
+        first_layer_early(2, 0, 0, 2)
         pair("x", 3, 0, HALF, (0,), "held")
-        first_layer_early(2, 2, 4)
+        first_layer_early(2, 0, 2, 4)
         weave_agg_image(1, "scalar", 0, HEAD_AGG)
         weave_x(3, "scalar", HALF)
-        widen_image(2, 0, 1, 0, FULL)
         quantize_cat(2, 1)
-        first_layer_rest(2)
+        first_layer_rest(2, 0)
         move_columns(w2, w2_raw)
         relu(0)
         move_columns(s2, s2_raw)
@@ -507,9 +508,9 @@ def tile_graphaugmentation_pb_t_w8_kernel(
         second_layer(1, (2, 3))
         agg_to_bank(1, 0, 4)
         pair("x", 3, 0, HALF, (1,))
-        widen_image(2, 0, 1, FULL)
+        widen_image(2, 0, 1, 0, FULL)
         join("x", 3, 0, HALF)
-        widen_image(2, 1, 2, 0, FULL)
+        widen_image(2, 0, 1, FULL)
         pair("x", 4, 0, HALF)
         pair("x", 4, HALF, FULL)
         product_from_bank(0, 0, 4)
@@ -519,27 +520,32 @@ def tile_graphaugmentation_pb_t_w8_kernel(
 
         hand_over("held", "vector")
         join("x", 4, 0, HALF)
-        widen_image(2, 1, 2, FULL)
+        widen_image(2, 1, 2, 0, FULL)
         join("x", 4, HALF, FULL)
+        widen_image(2, 1, 2, FULL)
         widen_image(2, 2, 4)
         quantize_cat(3, 1)
+        first_layer_early(3, 1)
         quantize_cat(3, 0)
-        first_layer(3)
+        first_layer_rest(3, 1)
         relu(2, 0, HALF)
         relu(2, HALF)
         quantize_hidden(2, 0, HALF)
         quantize_hidden(2, HALF)
+        weave_agg_image(2, "scalar", 0, EARLY_AGG // 2)
         second_layer(2, (0, 1, 2))
+        weave_agg_image(2, "scalar", EARLY_AGG // 2, EARLY_AGG)
         quantize_cat(4, 1)
         quantize_cat(4, 0)
         first_layer(4, 0, 1)
         weave_agg_image(2, "gpsimd", EARLY_AGG, PIX - AGG_PAIRED)
         add_bias(3, 0, 1)
         first_layer(4, 1, 2)
+        add_bias(3, 1, 2)
+        first_layer(4, 2, 3)
         second_layer(2, (3,))
-        for j in range(2, ROWS):
-            add_bias(3, j - 1, j)
-            first_layer(4, j, j + 1)
+        add_bias(3, 2, 3)
+        first_layer(4, 3, 4)
         add_bias(3, 3, 4)
         add_bias(4)
         agg_to_bank(2, 0, 2, 0, EARLY_PIXELS)
@@ -549,7 +555,6 @@ def tile_graphaugmentation_pb_t_w8_kernel(
         product_from_bank(2, 2, 4, 0, EARLY_PIXELS)
         store(2, 0, 4)
         pair_shares(5, 6)
-        weave_agg_image(2, "scalar", 0, EARLY_AGG)
         weave_x(5, "scalar", 0, FULL - X_PAIRED)
         join("x", 5, FULL - X_PAIRED, FULL)
         pair("x", 6, 0, HALF)
@@ -564,8 +569,9 @@ def tile_graphaugmentation_pb_t_w8_kernel(
             widen_image(i + 1, 0, 1, FULL)
             widen_image(i + 1, 1, 3)
             quantize_cat(a, 1)
+            first_layer_early(a, 1)
             quantize_cat(a, 0)
-            first_layer(a)
+            first_layer_rest(a, 1)
             relu_image(i - 1, hidden_image[:])
             quantize_cat(b, 0)
             quantize_hidden(a - 2)
@@ -615,8 +621,9 @@ def tile_graphaugmentation_pb_t_w8_kernel(
         widen(a + 2, "scalar", 1, 4)
         widen(LAST, "scalar", 0, 1)
         quantize_cat(a, 1)
+        first_layer_early(a, 1)
         quantize_cat(a, 0)
-        first_layer(a)
+        first_layer_rest(a, 1)
         relu_image(IMAGES - 3, hidden_image[:])
         quantize_cat(b, 0)
         quantize_hidden(a - 2)

@@ -31,18 +31,21 @@ FIRST = 3
 PART = ROWS * FULL
 STARTS = [sum(WIDTHS[:h]) for h in range(COUNT)]
 X_LOADS = [PIX] * IMAGES
-AGG_LOADS = [FULL, FULL] + [PIX] * (IMAGES - 1)
-HEAD_SPLIT = 128
-HEAD_AGG = 200
-EARLY_PIXELS = 368
+AGG_LOADS = [HALF, HALF, FULL] + [PIX] * (IMAGES - 1)
+HEAD_SPLIT = 160
+HEAD_AGG = 240
+EARLY_PIXELS = 360
 VECTOR_PIXELS = 224
-TAIL_SPLIT = 128
-X_PAIRED = 48
+TAIL_SPLIT = 80
+X_PAIRED = 64
 AGG_PAIRED = 56
 TURN_PIXELS = 256
 LATE_AGG = 64
-EARLY_AGG = 128
+EARLY_AGG = 144
 TURN_AGG = 128
+LATE_PIXELS = 256
+LATE_X = 224
+LOOP_AGG = 64
 
 
 def tile_graphaugmentation_pb_t_w8_kernel(
@@ -81,6 +84,8 @@ def tile_graphaugmentation_pb_t_w8_kernel(
 
         s1_raw = keep.tile([P, C], U8, name="s1_raw", align_bytes=64)
         s2_raw = keep.tile([P, C], U8, name="s2_raw", align_bytes=64)
+        warm = keep.tile([P, 1], F32, name="warm")
+        nc.vector.memset(warm[:], 0.0)
         nc.vector.memset(s1_raw[:].bitcast(I32), 0)
         nc.vector.memset(s2_raw[:].bitcast(I32), 0)
 
@@ -119,28 +124,27 @@ def tile_graphaugmentation_pb_t_w8_kernel(
 
         nc.scalar.dma_start(out=xs[:], in_=x_scale.rearrange("o (p t) h w -> p (o t h w)", t=ROWS))
         nc.scalar.dma_start(out=b1[:], in_=g1b.rearrange("(p t) -> p t", t=ROWS))
-        warm = keep.tile([P, 1], F32, name="warm")
-        nc.vector.memset(warm[:], 0.0)
         nc.scalar.activation(out=warm[:], in_=warm[:], func=ACT.Sigmoid)
 
         def load_b2():
             nc.sync.dma_start(out=b2[:], in_=g2b.rearrange("(p t) -> p t", t=ROWS))
 
-        load_x(0, 0, 2)
-        load_x(0, 2, 4)
+        for t in range(ROWS):
+            load_x(0, t, t + 1)
         load_agg(0)
         load_words(w1_raw[0], g1w_words[0])
         load_words(w1_raw[1], g1w_words[1])
         load_scales(s1_raw, g1w_scales)
         load_x(1)
         load_agg(1)
+        load_agg(2)
         load_words(w2_raw, g2w_words[0])
         load_scales(s2_raw, g2w_scales)
-        load_agg(2)
+        load_agg(3)
         load_b2()
         for j in range(2, len(X_LOADS)):
             load_x(j)
-            load_agg(j + 1)
+            load_agg(j + 2)
 
         w1 = [keep.tile([P, C], I32, name=f"w1_{g}", align_bytes=64) for g in range(2)]
         w2 = keep.tile([P, C], I32, name="w2", align_bytes=64)
@@ -251,7 +255,7 @@ def tile_graphaugmentation_pb_t_w8_kernel(
             weave(engine, agg_tile(h), agg_rows[h], *span(h, c0, c1))
 
         def weave_agg_image(i, engine, c0, c1):
-            weave(engine, turns, agg_loaded[i + 1], c0, c1)
+            weave(engine, turns, agg_loaded[i + 2], c0, c1)
 
         def weave_hidden(h, engine, c0=0, c1=None):
             c0, c1 = span(h, c0, c1)
@@ -455,15 +459,16 @@ def tile_graphaugmentation_pb_t_w8_kernel(
             return rows
 
         widen(1, "scalar")
-        widen_pairs(0, 0, 2)
+        widen_pairs(0, 0, 1)
         widen(2, "vector", 0, 1)
-        widen_pairs(0, 2, 4)
+        widen_pairs(0, 1, 2)
         widen(2, "vector", 1, 2)
-        widen(2, "scalar", 2, 4)
+        widen_pairs(0, 2, 4)
+        widen(2, "vector", 2, 3)
+        widen(2, "scalar", 3, 4)
         join_x(0)
         weave_x(1, "scalar")
         weave_agg(0, "vector")
-        weave_agg(1, "scalar")
         quantize_cat(0, 0)
         move_columns(w1[0], w1_raw[0])
         quantize_cat(0, 1)
@@ -471,16 +476,17 @@ def tile_graphaugmentation_pb_t_w8_kernel(
         move_columns(s1, s1_raw)
         first_layer(0)
         spread_bias()
-        quantize_cat(1, 0)
         shared = one.tile([P, 3 * PART // 2], BF16, name="shared", align_bytes=64)
         x_woven[2] = shared[:, PART // 2 :]
         agg_woven[2] = shared[:, :PART]
-        weave_x(2, "vector", 0, HALF)
+        weave_x(2, "scalar", 0, 256)
+        quantize_cat(1, 0)
+        weave_x(2, "vector", 256)
+        weave_agg(1, "vector")
+        quantize_cat(2, 0, HALF)
+        quantize_cat(2, 0, 0, HALF)
         quantize_cat(1, 1)
         first_layer(1)
-        weave_x(2, "vector", HALF)
-        quantize_cat(2, 0, 0, HALF)
-        quantize_cat(2, 0, HALF)
         widen_image(1, 0, 2)
         weave_agg(2, "gpsimd", HEAD_SPLIT)
         weave_agg(2, "scalar", 0, HEAD_SPLIT)
@@ -490,8 +496,8 @@ def tile_graphaugmentation_pb_t_w8_kernel(
         first_layer_early(2, 0, 0, 2)
         pair("x", 3, 0, HALF, (0,), "held")
         first_layer_early(2, 0, 2, 4)
-        weave_agg_image(1, "scalar", 0, HEAD_AGG)
         weave_x(3, "scalar", HALF)
+        weave_agg_image(1, "scalar", 0, HEAD_AGG)
         quantize_cat(2, 1)
         first_layer_rest(2, 0)
         move_columns(w2, w2_raw)
@@ -652,6 +658,7 @@ def tile_graphaugmentation_pb_t_w8_kernel(
         store(b - 2, 2, 4)
         first_layer(b)
         widen(LAST, "scalar", 1, 4)
+        weave_x(LAST, "scalar", FULL - 64)
         relu(a)
         quantize_cat(a + 2, 0, HALF)
         quantize_hidden(a)
@@ -660,16 +667,16 @@ def tile_graphaugmentation_pb_t_w8_kernel(
         second_layer(a, (2, 3, 0, 1))
         weave_agg(LAST, "gpsimd", 0, FULL - LATE_AGG)
         add_bias(b)
-        agg_to_bank(a, 2, 4, 0, HALF)
-        pair("x", LAST, 0, HALF, (0,))
+        agg_to_bank(a, 2, 4, 0, LATE_PIXELS)
+        pair("x", LAST, 0, LATE_X, (0,))
         agg_to_bank(a, 0, 2)
-        pair("x", LAST, 0, HALF, (1,))
-        weave_x(LAST, "scalar", HALF)
-        join("x", LAST, 0, HALF)
+        pair("x", LAST, 0, LATE_X, (1,))
+        weave_x(LAST, "scalar", LATE_X, FULL - 64)
+        join("x", LAST, 0, LATE_X)
         pair("agg", LAST, FULL - LATE_AGG, FULL)
         join("agg", LAST, FULL - LATE_AGG, FULL)
-        product_from_bank(a, 2, 4, 0, HALF)
-        product(a, 2, 4, "gpsimd", HALF)
+        product_from_bank(a, 2, 4, 0, LATE_PIXELS)
+        product(a, 2, 4, "gpsimd", LATE_PIXELS)
         product_from_bank(a, 0, 2)
         store(a, 0, 2)
         store(a, 2, ROWS)

@@ -135,9 +135,10 @@ def tile_graphaugmentation_pb_t_w8_kernel(
         load_words(w1_raw[0], g1w_words[0])
         load_words(w1_raw[1], g1w_words[1])
         load_scales(s1_raw, g1w_scales)
-        load_x(1)
+        load_x(1, 0, 2)
         load_agg(1)
         load_agg(2)
+        load_x(1, 2, 4)
         load_words(w2_raw, g2w_words[0])
         load_scales(s2_raw, g2w_scales)
         load_agg(3)
@@ -154,6 +155,12 @@ def tile_graphaugmentation_pb_t_w8_kernel(
         def move_columns(dst, src):
             nc.vector.tensor_copy(
                 out=dst[:].rearrange("p (t m) -> p m t", t=ROWS), in_=src[:].rearrange("p (m t) -> p m t", t=ROWS)
+            )
+
+        def move_columns_on_scalar(dst, src):
+            nc.scalar.copy(
+                out=dst[:].bitcast(U32).rearrange("p (t m) -> p t m", t=ROWS),
+                in_=src[:].bitcast(U32).rearrange("p (m t) -> p t m", t=ROWS),
             )
 
         def spread_bias():
@@ -541,8 +548,8 @@ def tile_graphaugmentation_pb_t_w8_kernel(
         weave_agg_image(2, "scalar", 0, EARLY_AGG // 2)
         second_layer(2, (0, 1, 2))
         weave_agg_image(2, "scalar", EARLY_AGG // 2, EARLY_AGG)
-        quantize_cat(4, 1)
         quantize_cat(4, 0)
+        quantize_cat(4, 1)
         first_layer(4, 0, 1)
         weave_agg_image(2, "gpsimd", EARLY_AGG, PIX - AGG_PAIRED)
         add_bias(3, 0, 1)

from contextlib import ExitStack

import concourse.mybir as mybir
from concourse.masks import make_identity

F32 = mybir.dt.float32
BF16 = mybir.dt.bfloat16
I32 = mybir.dt.int32
U32 = mybir.dt.uint32
U8 = mybir.dt.uint8
FP8 = mybir.dt.float8_e4m3fn
FP8X4 = mybir.dt.float8_e4m3fn_x4
ACT = mybir.ActivationFunctionType
ALU = mybir.AluOpType

IMAGES, C, PIX = 6, 512, 1024
P = 128
ROWS = 4
BANK = 512
HALF = 256
FULL = 2 * HALF
SPREAD = 16
NEIGHBOURS = 4

FLOPS = 2 * IMAGES * PIX * C * (2 * C + C)

WIDTHS = [HALF, HALF] + [FULL] * 11
COUNT = len(WIDTHS)
LAST = COUNT - 1
FIRST = 3
PART = ROWS * FULL
STARTS = [sum(WIDTHS[:h]) for h in range(COUNT)]
X_LOADS = [PIX] * IMAGES
AGG_LOADS = [HALF, HALF, FULL] + [PIX] * (IMAGES - 1)
HEAD_SPLIT = 160
HEAD_AGG = 240
EARLY_PIXELS = 360
VECTOR_PIXELS = 224
TAIL_SPLIT = 80
X_PAIRED = 64
AGG_PAIRED = 56
TURN_PIXELS = 256
LATE_AGG = 64
EARLY_AGG = 144
TURN_AGG = 128
LATE_PIXELS = 256
LATE_X = 224
LOOP_AGG = 64


def tile_graphaugmentation_pb_t_w8_kernel(
    tc, x_bytes, x_scale, agg, g1w_words, g1w_scales, g1b, g2w_words, g2w_scales, g2b, out
):
    nc = tc.nc
    x_hbm = x_bytes.rearrange("b (p t) h w -> b p t (h w)", t=ROWS)
    agg_hbm = agg.rearrange("b (p t) h w -> b p t (h w)", t=ROWS)
    out_hbm = out.rearrange("b (p t) h w -> b p t (h w)", t=ROWS)

    with ExitStack() as ctx:
        keep = ctx.enter_context(tc.tile_pool(name="keep", bufs=1))
        one = ctx.enter_context(tc.tile_pool(name="one", bufs=1))
        two = ctx.enter_context(tc.tile_pool(name="two", bufs=2))
        three = ctx.enter_context(tc.tile_pool(name="three", bufs=3))
        banks = ctx.enter_context(tc.psum_pool(name="banks", bufs=1))
        rings = {"vector": [0, 1, 2, 3], "scalar": [4, 5, 6], "held": [7]}

        def next_bank(ring, shape, dtype):
            k = rings[ring][0]
            rings[ring] = rings[ring][1:] + [k]
            return banks.tile(shape, dtype, name=f"bank{k}")

        def hand_over(source, target):
            rings[target] = rings[source][:1] + rings[target]
            rings[source] = rings[source][1:]

        ctx.enter_context(tc.manual_schedule())

        xs = keep.tile([P, ROWS], F32, name="xs")
        b1 = keep.tile([P, ROWS], BF16, name="b1")
        b2 = keep.tile([P, ROWS], BF16, name="b2")
        b1_pairs = keep.tile([P, 2, 4 * SPREAD], BF16, name="b1_pairs")
        ident = keep.tile([P, P], BF16, name="ident")
        make_identity(nc, ident[:])

        s1_raw = keep.tile([P, C], U8, name="s1_raw", align_bytes=64)
        s2_raw = keep.tile([P, C], U8, name="s2_raw", align_bytes=64)
        warm = keep.tile([P, 1], F32, name="warm")
        nc.vector.memset(warm[:], 0.0)
        nc.vector.memset(s1_raw[:].bitcast(I32), 0)
        nc.vector.memset(s2_raw[:].bitcast(I32), 0)

        x_loaded = [keep.tile([P, ROWS, n], U8, name=f"x_loaded{j}") for j, n in enumerate(X_LOADS)]
        agg_loaded = [keep.tile([P, ROWS, n], BF16, name=f"agg_loaded{j}") for j, n in enumerate(AGG_LOADS)]
        w1_raw = [keep.tile([P, C], I32, name=f"w1_raw{g}", align_bytes=64) for g in range(2)]
        w2_raw = keep.tile([P, C], I32, name="w2_raw", align_bytes=64)

        def chunk_of(loaded, sizes, h):
            j = max(j for j in range(len(sizes)) if sum(sizes[:j]) <= STARTS[h])
            c0 = STARTS[h] - sum(sizes[:j])
            return loaded[j][:, :, c0 : c0 + WIDTHS[h]]

        x_rows = [chunk_of(x_loaded, X_LOADS, h) for h in range(COUNT)]
        agg_rows = [chunk_of(agg_loaded, AGG_LOADS, h) for h in range(COUNT)]

        def load(loaded, hbm, sizes, j, t0=0, t1=ROWS):
            b, c0 = divmod(sum(sizes[:j]), PIX)
            nc.sync.dma_start(out=loaded[j][:, t0:t1, :], in_=hbm[b][:, t0:t1, c0 : c0 + sizes[j]])

        def load_x(j, t0=0, t1=ROWS):
            load(x_loaded, x_hbm, X_LOADS, j, t0, t1)

        def load_agg(j):
            load(agg_loaded, agg_hbm, AGG_LOADS, j)

        def load_words(dst, words):
            nc.sync.dma_start(out=dst[:], in_=words.rearrange("p n t -> p (n t)").bitcast(I32))

        def load_scales(dst, scales):
            rows = 4 * scales.shape[0]
            for q in range(4):
                nc.sync.dma_start(
                    out=dst[32 * q : 32 * q + rows, :].bitcast(I32), in_=scales[:, 4 * q : 4 * q + 4, :].bitcast(I32)
                )

        nc.scalar.dma_start(out=xs[:], in_=x_scale.rearrange("o (p t) h w -> p (o t h w)", t=ROWS))
        nc.scalar.dma_start(out=b1[:], in_=g1b.rearrange("(p t) -> p t", t=ROWS))
        nc.scalar.activation(out=warm[:], in_=warm[:], func=ACT.Sigmoid)

        def load_b2():
            nc.sync.dma_start(out=b2[:], in_=g2b.rearrange("(p t) -> p t", t=ROWS))

        for t in range(ROWS):
            load_x(0, t, t + 1)
        load_agg(0)
        load_words(w1_raw[0], g1w_words[0])
        load_words(w1_raw[1], g1w_words[1])
        load_scales(s1_raw, g1w_scales)
        load_x(1, 0, 2)
        load_agg(1)
        load_agg(2)
        load_x(1, 2, 4)
        load_words(w2_raw, g2w_words[0])
        load_scales(s2_raw, g2w_scales)
        load_agg(3)
        load_b2()
        for j in range(2, len(X_LOADS)):
            load_x(j)
            load_agg(j + 2)

        w1 = [keep.tile([P, C], I32, name=f"w1_{g}", align_bytes=64) for g in range(2)]
        w2 = keep.tile([P, C], I32, name="w2", align_bytes=64)
        s1 = keep.tile([P, C], U8, name="s1", align_bytes=64)
        s2 = keep.tile([P, C], U8, name="s2", align_bytes=64)

        def move_columns(dst, src):
            nc.vector.tensor_copy(
                out=dst[:].rearrange("p (t m) -> p m t", t=ROWS), in_=src[:].rearrange("p (m t) -> p m t", t=ROWS)
            )

        def move_columns_on_scalar(dst, src):
            nc.scalar.copy(
                out=dst[:].bitcast(U32).rearrange("p (t m) -> p t m", t=ROWS),
                in_=src[:].bitcast(U32).rearrange("p (m t) -> p t m", t=ROWS),
            )

        def spread_bias():
            for u in range(2):
                nc.scalar.copy(
                    out=b1_pairs[:, u, :].rearrange("p (n e i) -> p n e i", e=2, i=2),
                    in_=b1[:, 2 * u : 2 * u + 2].unsqueeze(1).unsqueeze(3).to_broadcast([P, SPREAD, 2, 2]),
                )

        x_wide, x_woven, agg_woven, cat_codes, cat_scales, sums, biased, hidden = ({} for stage in range(8))
        hidden_woven, hidden_codes, hidden_scales, gate, pair_bank, agg_bank, aside = ({} for stage in range(7))

        whole = {}

        x_image = keep.tile([P, ROWS * PIX], BF16, name="x_image", align_bytes=64)
        turns = keep.tile([P, 3 * PART], BF16, name="turns", align_bytes=64)
        hidden_image = keep.tile([P, ROWS * PIX], BF16, name="hidden_image", align_bytes=64)
        for h in range(FIRST, COUNT):
            first = ROWS * (STARTS[h] % PIX)
            x_woven[h] = x_image[:, first : first + PART]
            agg_woven[h] = turns[:, first : first + PART]
            hidden_woven[h] = hidden_image[:, first : first + PART]
        hidden_woven[0] = turns[:, 3 * PART // 2 : 2 * PART]
        hidden_woven[1] = turns[:, 2 * PART : 5 * PART // 2]
        hidden_woven[2] = hidden_image[:, PART:]

        def image_tile(store, h, pool, rows, scale, dtype, name):
            if h not in store:
                i = STARTS[h] // PIX
                whole[name, i] = pool.tile([P, rows, scale * PIX], dtype, name=name, align_bytes=64)
                for k in range(COUNT):
                    if STARTS[k] // PIX == i and k not in store:
                        first = STARTS[k] % PIX
                        store[k] = whole[name, i][:, :, scale * first : scale * (first + WIDTHS[k])]
            return store[h]

        def span(h, c0, c1):
            return c0, WIDTHS[h] if c1 is None else c1

        def tile_of(store, h, pool, shape, dtype, name):
            if h not in store:
                store[h] = pool.tile(shape, dtype, name=name, align_bytes=64)
            return store[h]

        def widen(h, engine, t0=0, t1=ROWS):
            dst = tile_of(x_wide, h, two, [P, ROWS, WIDTHS[h]], BF16, "x_wide")
            for t in range(t0, t1):
                codes = x_rows[h][:, t, :].bitcast(FP8)
                if engine == "scalar":
                    nc.scalar.activation(out=dst[:, t, :], in_=codes, func=ACT.Copy, scale=xs[:, t : t + 1])
                else:
                    nc.vector.tensor_scalar(
                        out=dst[:, t, :], in0=codes, scalar1=xs[:, t : t + 1], scalar2=None, op0=ALU.mult
                    )

        def widen_image(i, t0=0, t1=ROWS, c0=0, c1=PIX):
            image_tile(x_wide, 2 * i + 1, two, ROWS, 1, BF16, "x_wide")
            for t in range(t0, t1):
                nc.scalar.activation(
                    out=whole["x_wide", i][:, t, c0:c1],
                    in_=x_loaded[i][:, t, c0:c1].bitcast(FP8),
                    func=ACT.Copy,
                    scale=xs[:, t : t + 1],
                )

        def widen_pairs(h, t0, t1):
            dst = tile_of(x_wide, h, one, [P, 2, 2 * WIDTHS[h]], BF16, "x_pairs")
            for t in range(t0, t1):
                nc.vector.tensor_scalar(
                    out=dst[:, t // 2, t % 2 :: 2],
                    in0=x_rows[h][:, t, :].bitcast(FP8),
                    scalar1=xs[:, t : t + 1],
                    scalar2=None,
                    op0=ALU.mult,
                )

        def x_tile(h):
            return tile_of(x_woven, h, two, [P, ROWS * WIDTHS[h]], BF16, "x_woven")

        def agg_tile(h):
            return tile_of(agg_woven, h, two, [P, ROWS * WIDTHS[h]], BF16, "agg_woven")

        def hidden_tile(h):
            return tile_of(hidden_woven, h, two, [P, ROWS * WIDTHS[h]], BF16, "hidden_woven")

        def weave(engine, dst, rows, c0, c1):
            woven = dst[:, ROWS * c0 : ROWS * c1].rearrange("p (c i t) -> p c t i", i=NEIGHBOURS, t=ROWS)
            rows = rows[:, :, c0:c1].rearrange("p t (c i) -> p c t i", i=NEIGHBOURS)
            if engine == "gpsimd":
                nc.gpsimd.tensor_scalar(out=woven, in0=rows, scalar1=1.0, scalar2=0.0, op0=ALU.mult, op1=ALU.add)
            else:
                copy = nc.vector.tensor_copy if engine == "vector" else nc.scalar.copy
                copy(out=woven, in_=rows)

        def weave_x(h, engine, c0=0, c1=None):
            weave(engine, x_tile(h), x_wide[h], *span(h, c0, c1))

        def weave_agg(h, engine, c0=0, c1=None):
            weave(engine, agg_tile(h), agg_rows[h], *span(h, c0, c1))

        def weave_agg_image(i, engine, c0, c1):
            weave(engine, turns, agg_loaded[i + 2], c0, c1)

        def weave_hidden(h, engine, c0=0, c1=None):
            c0, c1 = span(h, c0, c1)
            first = c0 // HALF * HALF
            weave(engine, hidden_tile(h)[:, ROWS * first :], hidden[h, c0 // HALF], c0 - first, c1 - first)

        def join_x(h):
            nc.vector.tensor_copy(
                out=x_tile(h)[:].bitcast(F32).rearrange("p (n u) -> p n u", u=2),
                in_=x_wide[h][:].bitcast(F32).rearrange("p u n -> p n u"),
            )

        def pair(name, h, c0, c1, pairs=(0, 1), ring="scalar"):
            rows = {"x": x_wide, "agg": agg_rows, "hidden": hidden}[name][h]
            if 0 in pairs:
                pair_bank[name, h, c0] = next_bank(ring, [P, 2, c1 - c0, 2], BF16)[:]
            for u in pairs:
                nc.tensor.matmul(
                    out=pair_bank[name, h, c0][:, u],
                    lhsT=ident[:],
                    rhs=rows[:, 2 * u : 2 * u + 2, c0:c1].rearrange("p e n -> p n e"),
                    start=True,
                    stop=True,
                )

        def join(name, h, c0, c1):
            dst = {"x": x_tile, "agg": agg_tile, "hidden": hidden_tile}[name](h)
            nc.scalar.copy(
                out=dst[:, ROWS * c0 : ROWS * c1].bitcast(F32).rearrange("p (n u) -> p n u", u=2),
                in_=pair_bank[name, h, c0].rearrange("p u n e -> p u (n e)").bitcast(F32).rearrange("p u n -> p n u"),
            )

        def quantize_cat(h, g, c0=0, c1=None):
            c0, c1 = span(h, c0, c1)
            codes = image_tile(cat_codes, h, two, 2, 1, U32, "cat_codes")
            scales = image_tile(cat_scales, h, two, 2, 1, U8, "cat_scales")
            nc.vector.quantize_mx(
                out=codes[:, g, c0:c1].bitcast(FP8X4),
                scales=scales[:, g, c0:c1],
                in_=(x_woven, agg_woven)[g][h][:, ROWS * c0 : ROWS * c1],
            )

        def pair_shares(h, k):
            bank = next_bank("scalar", [P, 2, X_PAIRED + AGG_PAIRED, 2], BF16)
            pair_bank["x", h, FULL - X_PAIRED] = bank[:, :, :X_PAIRED]
            pair_bank["agg", k, FULL - AGG_PAIRED] = bank[:, :, X_PAIRED:]
            shares = (
                (bank[:, :, :X_PAIRED], x_wide[h][:, :, FULL - X_PAIRED :]),
                (bank[:, :, X_PAIRED:], agg_rows[k][:, :, FULL - AGG_PAIRED :]),
            )
            for dst, rows in shares:
                nc.tensor.matmul(
                    out=dst, lhsT=ident[:], rhs=rows.rearrange("p (u e) n -> p u n e", e=2), start=True, stop=True
                )

        def first_pass(dst, h, g, t, n, opens=0):
            m = slice(P * t, P * t + P)
            nc.tensor.matmul_mx(
                out=dst,
                lhsT=w1[g][:, m].bitcast(FP8X4),
                lhsT_scale=s1[4 * g :, m],
                rhs=cat_codes[h][:, g, n].bitcast(FP8X4),
                rhs_scale=cat_scales[h][:, g, n],
                start=(g == opens),
                stop=(g != opens),
            )

        def first_layer(h, j0=0, j1=None):
            for j in range(j0, WIDTHS[h] // P if j1 is None else j1):
                c, u = divmod(j, 2)
                sums[h, j] = next_bank("vector", [P, 2, HALF], F32)
                for e in range(2):
                    for g in range(2):
                        first_pass(sums[h, j][:, e, :], h, g, 2 * u + e, slice(HALF * c, HALF * (c + 1)))

        def first_layer_early(h, g, j0=0, j1=ROWS):
            for j in range(j0, j1):
                c, u = divmod(j, 2)
                sums[h, j] = next_bank("vector", [P, 2, HALF], F32)
                first_pass(sums[h, j][:, 0, :], h, g, 2 * u, slice(HALF * c, HALF * (c + 1)), g)

        def first_layer_rest(h, opens):
            for j in range(ROWS):
                c, u = divmod(j, 2)
                for e, g in ((0, 1 - opens), (1, opens), (1, 1 - opens)):
                    first_pass(sums[h, j][:, e, :], h, g, 2 * u + e, slice(HALF * c, HALF * (c + 1)), opens)

        def add_bias(h, j0=0, j1=None):
            dst = image_tile(biased, h, one, 2, 2, BF16, "biased")
            for j in range(j0, WIDTHS[h] // P if j1 is None else j1):
                c, u = divmod(j, 2)
                pixels = dst[:, u, 2 * HALF * c : 2 * HALF * (c + 1)]
                nc.vector.tensor_tensor(
                    out=pixels.rearrange("p (r n i e) -> p r n e i", n=SPREAD, i=2, e=2),
                    in0=b1_pairs[:, u, :]
                    .rearrange("p (n e i) -> p n e i", e=2, i=2)
                    .unsqueeze(1)
                    .to_broadcast([P, HALF // (2 * SPREAD), SPREAD, 2, 2]),
                    in1=sums[h, j][:].rearrange("p e (r n i) -> p r n e i", n=SPREAD, i=2),
                    op=ALU.add,
                )

        def relu(h, c0=0, c1=None):
            c0, c1 = span(h, c0, c1)
            nc.vector.tensor_scalar(
                out=hidden_tile(h)[:, ROWS * c0 : ROWS * c1].rearrange("p (n u e) -> p n u e", u=2, e=2),
                in0=biased[h][:, :, 2 * c0 : 2 * c1].rearrange("p u (n e) -> p n u e", e=2),
                scalar1=0.0,
                scalar2=None,
                op0=ALU.max,
            )

        def relu_image(i, dst):
            nc.vector.tensor_scalar(
                out=dst.rearrange("p (n u e) -> p n u e", u=2, e=2),
                in0=whole["biased", i][:].rearrange("p u (n e) -> p n u e", e=2),
                scalar1=0.0,
                scalar2=None,
                op0=ALU.max,
            )

        def first_layer_rows(h, c0=0, c1=None, t0=0, t1=ROWS):
            c0, c1 = span(h, c0, c1)
            dst = tile_of(hidden, (h, c0 // HALF), three, [P, ROWS, HALF], BF16, "hidden")
            rows = BANK // (c1 - c0)
            for first in range(t0, t1, rows):
                acc = next_bank("scalar", [P, rows, c1 - c0], F32)
                for r in range(rows):
                    for g in range(2):
                        first_pass(acc[:, r, :], h, g, first + r, slice(c0, c1))
                for r in range(rows):
                    t = first + r
                    nc.scalar.activation(out=dst[:, t, :], in_=acc[:, r, :], func=ACT.Relu, bias=b1[:, t : t + 1])

        def quantize_hidden(h, c0=0, c1=None):
            c0, c1 = span(h, c0, c1)
            codes = image_tile(hidden_codes, h, two, 1, 1, U32, "hidden_codes")[:, 0, :]
            scales = image_tile(hidden_scales, h, two, 1, 1, U8, "hidden_scales")[:, 0, :]
            nc.vector.quantize_mx(
                out=codes[:, c0:c1].bitcast(FP8X4), scales=scales[:, c0:c1], in_=hidden_woven[h][:, ROWS * c0 : ROWS * c1]
            )

        def second_layer(h, order=(0, 1, 2, 3), c0=0, c1=None):
            c0, c1 = span(h, c0, c1)
            dst = image_tile(gate, h, two, ROWS, 1, F32, "gate")
            rows = BANK // (c1 - c0)
            for first in range(0, len(order), rows):
                acc = next_bank("scalar", [P, rows, c1 - c0], F32)
                for r, t in enumerate(order[first : first + rows]):
                    m = slice(P * t, P * t + P)
                    nc.tensor.matmul_mx(
                        out=acc[:, r, :],
                        lhsT=w2[:, m].bitcast(FP8X4),
                        lhsT_scale=s2[:, m],
                        rhs=hidden_codes[h][:, 0, c0:c1].bitcast(FP8X4),
                        rhs_scale=hidden_scales[h][:, 0, c0:c1],
                        start=True,
                        stop=True,
                    )
                for r, t in enumerate(order[first : first + rows]):
                    nc.scalar.activation(
                        out=dst[:, t, c0:c1], in_=acc[:, r, :], func=ACT.Sigmoid, bias=b2[:, t : t + 1]
                    )

        def agg_to_bank(h, t0, t1, c0=0, c1=None):
            c0, c1 = span(h, c0, c1)
            bank = next_bank("vector", [P, t1 - t0, c1 - c0], BF16)
            for t in range(t0, t1):
                agg_bank[h, t, c0] = bank[:, t - t0 :, :]
            rows = BANK // (c1 - c0)
            for t in range(t0, t1, rows):
                end = min(t + rows, t1)
                nc.tensor.matmul(
                    out=bank[:, t - t0 : end - t0, :],
                    lhsT=ident[:],
                    rhs=agg_rows[h][:, t:end, c0:c1],
                    start=True,
                    stop=True,
                )

        def product_from_bank(h, t0, t1, c0=0, c1=None):
            c0, c1 = span(h, c0, c1)
            part = gate[h][:, t0:t1, c0:c1]
            nc.vector.tensor_tensor(out=part, in0=part, in1=agg_bank[h, t0, c0][:, : t1 - t0, :], op=ALU.mult)

        def product(h, t0, t1, engine="vector", c0=0, c1=None):
            c0, c1 = span(h, c0, c1)
            part = gate[h][:, t0:t1, c0:c1]
            multiply = nc.vector.tensor_tensor if engine == "vector" else nc.gpsimd.tensor_tensor
            multiply(out=part, in0=part, in1=agg_rows[h][:, t0:t1, c0:c1], op=ALU.mult)

        def store(h, t0, t1, c0=0, c1=None, src=None):
            c0, c1 = span(h, c0, c1)
            b, first = divmod(STARTS[h], PIX)
            src = gate[h][:, t0:t1, c0:c1] if src is None else src
            nc.sync.dma_start(out=out_hbm[b][:, t0:t1, first + c0 : first + c1], in_=src)

        def product_aside(h, t0, t1, spent):
            rows = spent[:, : 2 * (t1 - t0) * FULL].bitcast(F32).rearrange("p (t n) -> p t n", n=FULL)
            nc.gpsimd.tensor_tensor(out=rows, in0=gate[h][:, t0:t1, :], in1=agg_rows[h][:, t0:t1, :], op=ALU.mult)
            return rows

        widen(1, "scalar")
        widen_pairs(0, 0, 1)
        widen(2, "vector", 0, 1)
        widen_pairs(0, 1, 2)
        widen(2, "vector", 1, 2)
        widen_pairs(0, 2, 4)
        widen(2, "vector", 2, 3)
        widen(2, "scalar", 3, 4)
        join_x(0)
        weave_x(1, "scalar")
        weave_agg(0, "vector")
        quantize_cat(0, 0)
        move_columns(w1[0], w1_raw[0])
        quantize_cat(0, 1)
        move_columns(w1[1], w1_raw[1])
        move_columns(s1, s1_raw)
        first_layer(0)
        spread_bias()
        shared = one.tile([P, 3 * PART // 2], BF16, name="shared", align_bytes=64)
        x_woven[2] = shared[:, PART // 2 :]
        agg_woven[2] = shared[:, :PART]
        weave_x(2, "scalar", 0, 256)
        quantize_cat(1, 0)
        weave_x(2, "vector", 256)
        weave_agg(1, "vector")
        quantize_cat(2, 0, HALF)
        quantize_cat(2, 0, 0, HALF)
        quantize_cat(1, 1)
        first_layer(1)
        widen_image(1, 0, 2)
        weave_agg(2, "gpsimd", HEAD_SPLIT)
        weave_agg(2, "scalar", 0, HEAD_SPLIT)
        widen_image(1, 2, 4)
        add_bias(0)
        add_bias(1)
        first_layer_early(2, 0, 0, 2)
        pair("x", 3, 0, HALF, (0,), "held")
        first_layer_early(2, 0, 2, 4)
        weave_x(3, "scalar", HALF)
        weave_agg_image(1, "scalar", 0, HEAD_AGG)
        quantize_cat(2, 1)
        first_layer_rest(2, 0)
        move_columns(w2, w2_raw)
        relu(0)
        move_columns(s2, s2_raw)
        relu(1)
        quantize_hidden(0)
        quantize_hidden(1)
        weave_agg_image(1, "gpsimd", HEAD_AGG, PIX)
        second_layer(0)
        second_layer(1, (0, 1))
        add_bias(2)
        agg_to_bank(0, 0, 4)
        second_layer(1, (2, 3))
        agg_to_bank(1, 0, 4)
        pair("x", 3, 0, HALF, (1,))
        widen_image(2, 0, 1, 0, FULL)
        join("x", 3, 0, HALF)
        widen_image(2, 0, 1, FULL)
        pair("x", 4, 0, HALF)
        pair("x", 4, HALF, FULL)
        product_from_bank(0, 0, 4)
        store(0, 0, 4)
        product_from_bank(1, 0, 4)
        store(1, 0, 4)

        hand_over("held", "vector")
        join("x", 4, 0, HALF)
        widen_image(2, 1, 2, 0, FULL)
        join("x", 4, HALF, FULL)
        widen_image(2, 1, 2, FULL)
        widen_image(2, 2, 4)
        quantize_cat(3, 1)
        first_layer_early(3, 1)
        quantize_cat(3, 0)
        first_layer_rest(3, 1)
        relu(2, 0, HALF)
        relu(2, HALF)
        quantize_hidden(2, 0, HALF)
        quantize_hidden(2, HALF)
        weave_agg_image(2, "scalar", 0, EARLY_AGG // 2)
        second_layer(2, (0, 1, 2))
        weave_agg_image(2, "scalar", EARLY_AGG // 2, EARLY_AGG)
        quantize_cat(4, 0)
        quantize_cat(4, 1)
        first_layer(4, 0, 1)
        weave_agg_image(2, "gpsimd", EARLY_AGG, PIX - AGG_PAIRED)
        add_bias(3, 0, 1)
        first_layer(4, 1, 2)
        add_bias(3, 1, 2)
        first_layer(4, 2, 3)
        second_layer(2, (3,))
        add_bias(3, 2, 3)
        first_layer(4, 3, 4)
        add_bias(3, 3, 4)
        add_bias(4)
        agg_to_bank(2, 0, 2, 0, EARLY_PIXELS)
        agg_to_bank(2, 2, 4, 0, EARLY_PIXELS)
        product(2, 0, 4, "gpsimd", EARLY_PIXELS)
        product_from_bank(2, 0, 2, 0, EARLY_PIXELS)
        product_from_bank(2, 2, 4, 0, EARLY_PIXELS)
        store(2, 0, 4)
        pair_shares(5, 6)
        weave_x(5, "scalar", 0, FULL - X_PAIRED)
        join("x", 5, FULL - X_PAIRED, FULL)
        pair("x", 6, 0, HALF)
        pair("x", 6, HALF, FULL)

        for i in range(2, IMAGES - 2):
            a, b = 2 * i + 1, 2 * i + 2
            join("x", b, 0, HALF)
            join("agg", b, FULL - AGG_PAIRED, FULL)
            widen_image(i + 1, 0, 1, 0, FULL)
            join("x", b, HALF, FULL)
            widen_image(i + 1, 0, 1, FULL)
            widen_image(i + 1, 1, 3)
            quantize_cat(a, 1)
            first_layer_early(a, 1)
            quantize_cat(a, 0)
            first_layer_rest(a, 1)
            relu_image(i - 1, hidden_image[:])
            quantize_cat(b, 0)
            quantize_hidden(a - 2)
            second_layer(a - 2, (0, 1, 2))
            quantize_cat(b, 1)
            first_layer(b, 0, 1)
            quantize_hidden(b - 2)
            weave_agg_image(i + 1, "gpsimd", 0, PIX - AGG_PAIRED)
            add_bias(a, 0, 1)
            first_layer(b, 1, 2)
            widen_image(i + 1, 3, 4)
            second_layer(a - 2, (3,))
            add_bias(a, 1, 2)
            first_layer(b, 2, 3)
            add_bias(a, 2, 3)
            second_layer(b - 2, (0,))
            first_layer(b, 3, 4)
            add_bias(a, 3, 4)
            add_bias(b)
            second_layer(b - 2, (1,))
            agg_to_bank(a - 2, 0, 4, 0, VECTOR_PIXELS)
            weave_x(a + 2, "scalar", 0, P)
            second_layer(b - 2, (2,))
            agg_to_bank(b - 2, 0, 2)
            second_layer(b - 2, (3,))
            agg_to_bank(b - 2, 2, 4)
            product(a - 2, 0, 4, "gpsimd", VECTOR_PIXELS)
            product_from_bank(a - 2, 0, 4, 0, VECTOR_PIXELS)
            product_from_bank(b - 2, 0, 2)
            store(b - 2, 0, 2)
            store(a - 2, 0, 4)
            product_from_bank(b - 2, 2, 4)
            store(b - 2, 2, 4)
            pair_shares(a + 2, b + 2)
            weave_x(a + 2, "scalar", P, FULL - X_PAIRED)
            join("x", a + 2, FULL - X_PAIRED, FULL)
            pair("x", b + 2, 0, HALF)
            pair("x", b + 2, HALF, FULL)
        a, b = LAST - 3, LAST - 2
        agg_woven[a + 2] = agg_woven[b]
        hidden_woven[a + 2] = turns[:, 2 * PART :]
        hidden_woven[LAST] = hidden_woven[a]
        join("x", b, 0, HALF)
        join("agg", b, FULL - AGG_PAIRED, FULL)
        widen(a + 2, "scalar", 0, 1)
        join("x", b, HALF, FULL)
        widen(a + 2, "scalar", 1, 4)
        widen(LAST, "scalar", 0, 1)
        quantize_cat(a, 1)
        first_layer_early(a, 1)
        quantize_cat(a, 0)
        first_layer_rest(a, 1)
        relu_image(IMAGES - 3, hidden_image[:])
        quantize_cat(b, 0)
        quantize_hidden(a - 2)
        second_layer(a - 2, (0, 1, 2))
        quantize_cat(b, 1)
        quantize_hidden(b - 2)
        hand_over("vector", "scalar")
        weave_agg(a + 2, "gpsimd")
        second_layer(a - 2, (3,))
        add_bias(a)
        second_layer(b - 2, (0,))
        agg_to_bank(a - 2, 0, 4, 0, TURN_PIXELS)
        second_layer(b - 2, (1,))
        agg_to_bank(b - 2, 0, 2)
        second_layer(b - 2, (2, 3))
        agg_to_bank(b - 2, 2, 4)
        pair("x", a + 2, 0, HALF)
        weave_x(a + 2, "scalar", HALF)
        join("x", a + 2, 0, HALF)
        product(a - 2, 0, 4, "gpsimd", TURN_PIXELS)
        product_from_bank(a - 2, 0, 4, 0, TURN_PIXELS)
        product_from_bank(b - 2, 0, 2)
        store(b - 2, 0, 2)
        store(a - 2, 0, 4)
        product_from_bank(b - 2, 2, 4)
        store(b - 2, 2, 4)
        first_layer(b)
        widen(LAST, "scalar", 1, 4)
        weave_x(LAST, "scalar", FULL - 64)
        relu(a)
        quantize_cat(a + 2, 0, HALF)
        quantize_hidden(a)
        quantize_cat(a + 2, 1)
        quantize_cat(a + 2, 0, 0, HALF)
        second_layer(a, (2, 3, 0, 1))
        weave_agg(LAST, "gpsimd", 0, FULL - LATE_AGG)
        add_bias(b)
        agg_to_bank(a, 2, 4, 0, LATE_PIXELS)
        pair("x", LAST, 0, LATE_X, (0,))
        agg_to_bank(a, 0, 2)
        pair("x", LAST, 0, LATE_X, (1,))
        weave_x(LAST, "scalar", LATE_X, FULL - 64)
        join("x", LAST, 0, LATE_X)
        pair("agg", LAST, FULL - LATE_AGG, FULL)
        join("agg", LAST, FULL - LATE_AGG, FULL)
        product_from_bank(a, 2, 4, 0, LATE_PIXELS)
        product(a, 2, 4, "gpsimd", LATE_PIXELS)
        product_from_bank(a, 0, 2)
        store(a, 0, 2)
        store(a, 2, ROWS)

        s = LAST - 1
        first_layer_rows(s, 0, HALF)
        first_layer_rows(s, HALF)
        relu(s - 1)
        quantize_cat(LAST, 0, 0, HALF)
        quantize_hidden(s - 1)
        quantize_cat(LAST, 1)
        second_layer(s - 1, (2, 3))
        first_layer(LAST, 0, 1)
        second_layer(s - 1, (0, 1))
        agg_to_bank(s - 1, 0, 2)
        first_layer(LAST, 1, 2)
        quantize_cat(LAST, 0, HALF)
        weave_hidden(s, "vector", 0, HALF)
        weave_hidden(s, "vector", HALF)
        quantize_hidden(s, 0, HALF)
        quantize_hidden(s, HALF)
        second_layer(s, (0, 1))
        agg_to_bank(s, 0, 1)
        first_layer_rows(LAST, HALF)
        second_layer(s, (2,))
        weave_hidden(LAST, "scalar", HALF, HALF + TAIL_SPLIT)
        second_layer(s, (3,))
        rows = product_aside(s - 1, 2, 3, hidden_woven[s])
        product(s - 1, 3, 4, "gpsimd")
        add_bias(LAST, 0, 1)
        product_from_bank(s - 1, 0, 1)
        store(s - 1, 0, 1)
        store(s - 1, 2, 3, src=rows)
        add_bias(LAST, 1, 2)
        product_from_bank(s - 1, 1, 2)
        store(s - 1, 1, 2)
        product_from_bank(s, 0, 1)
        store(s - 1, 3, 4)
        store(s, 0, 1)
        relu(LAST, 0, HALF)
        product(s, 1, 2)
        store(s, 1, 2)
        quantize_hidden(LAST, 0, HALF)
        second_layer(LAST, c1=HALF)
        weave_hidden(LAST, "vector", HALF + TAIL_SPLIT)
        product(s, 2, 3)
        store(s, 2, 3)
        quantize_hidden(LAST, HALF)
        second_layer(LAST, c0=HALF)
        product(s, 3, 4)
        store(s, 3, 4)
        product(LAST, 0, 2, c1=HALF)
        store(LAST, 0, 2, c1=HALF)
        product(LAST, 2, 4, c1=HALF)
        store(LAST, 2, 4, c1=HALF)
        product(LAST, 0, 2, c0=HALF)
        store(LAST, 0, 2, c0=HALF)
        for t in range(2, ROWS):
            product(LAST, t, t + 1, c0=HALF)
            store(LAST, t, t + 1, c0=HALF)
